import numpy as np
import ml_dtypes


def mxq(x, axis, fmt="e4m3"):
    dtype, down = {"e4m3": (ml_dtypes.float8_e4m3fn, 7), "e5m2": (ml_dtypes.float8_e5m2, 14)}[fmt]
    v = np.moveaxis(np.asarray(x, np.float32).astype(ml_dtypes.bfloat16).astype(np.float64), axis, -1)
    blocks = v.reshape(v.shape[:-1] + (-1, 32))
    amax = np.abs(blocks).max(-1, keepdims=True)
    byte = np.maximum(np.where(amax > 0, np.frexp(amax)[1] - 1 + 127, 0) - down, 1)
    scale = np.exp2(byte - 127.0)
    codes = (blocks / scale).astype(np.float32).astype(dtype).astype(np.float64)
    return np.moveaxis((codes * scale).reshape(v.shape), -1, axis)


WIDE = False


def mx_kscale(k):
    if not WIDE:
        return np.ones(k)
    levels = np.array([10, -10, 5, -5, 0])
    if k % 512:
        return np.exp2(np.random.permutation(np.resize(levels, k // 32))).repeat(32)
    a = np.empty((k // 512, 16))
    for p in range(k // 512):
        a[p, :8] = np.random.permutation(np.resize(levels, 8))
        for g in range(8):
            far = levels[np.abs(levels - a[p, g]) >= 10]
            a[p, g + 8] = far[np.random.randint(len(far))]
    return np.exp2(a.ravel()).repeat(32)


BF16 = ml_dtypes.bfloat16


def bf(x):
    return np.asarray(x, np.float32).astype(BF16)


def f64(x):
    return np.asarray(x).astype(np.float64)


T, H, QR, NH, DN, DR, KVR = 4096, 1024, 512, 2, 128, 64, 64
EPS = 1e-6


def rmsnorm(x, gamma):
    var = np.mean(np.square(x), axis=-1, keepdims=True)
    return x * (1.0 / np.sqrt(var + EPS)) * gamma


def apply_rope(x, cos, sin):
    x1, x2 = np.split(x, 2, axis=-1)
    rot = np.concatenate([-x2, x1], axis=-1)
    return x * cos + rot * sin


def draw0():
    s, t = mx_kscale(H), mx_kscale(QR)
    return {"token_x": bf(np.random.standard_normal((T, H)) * s),
            "wq_a": bf(np.random.standard_normal((H, QR)) / np.sqrt(H) / s[:, None]),
            "wq_b": bf(np.random.standard_normal((QR, NH * (DN + DR))) / np.sqrt(QR) / t[:, None]),
            "wkv": bf(np.random.standard_normal((H, KVR + DR)) / np.sqrt(H) / s[:, None]),
            "rope_cos": bf(np.random.uniform(-1.0, 1.0, (T, DR))),
            "rope_sin": bf(np.random.uniform(-1.0, 1.0, (T, DR))),
            "gamma_cq": bf((1.0 + 0.1 * np.random.standard_normal(QR)) * t),
            "gamma_ckv": bf(1.0 + 0.1 * np.random.standard_normal(KVR))}


def core(token_x, wq_a, wq_b, wkv, rope_cos, rope_sin, gamma_cq, gamma_ckv):
    cos, sin = f64(rope_cos), f64(rope_sin)
    xq = mxq(f64(token_x), 1, "e4m3")
    cq = rmsnorm(xq @ mxq(f64(wq_a), 0, "e4m3"), f64(gamma_cq))
    q = (mxq(cq, 1, "e4m3") @ mxq(f64(wq_b), 0, "e4m3")).reshape(T, NH, DN + DR)
    q_nope, q_rope = q[..., :DN], q[..., DN:]
    q_rope = apply_rope(q_rope, cos[:, None, :], sin[:, None, :])
    query = np.concatenate([q_nope, q_rope], axis=-1)
    kv = xq @ mxq(f64(wkv), 0, "e4m3")
    ckv = rmsnorm(kv[:, :KVR], f64(gamma_ckv))
    k_rope = apply_rope(kv[:, KVR:], cos, sin)
    return np.concatenate([query.reshape(T, -1), ckv, k_rope], axis=-1)


def e4m3fn_bytes(y):
    return np.clip(np.asarray(y, np.float64), -448.0, 448.0).astype(np.float32).astype(ml_dtypes.float8_e4m3fn).view(np.uint8)


def e4m3fn_values(b):
    return np.asarray(b, np.uint8).view(ml_dtypes.float8_e4m3fn).astype(np.float64)


def setup_inputs():
    d = draw0()
    x0 = np.asarray(d['token_x']).astype(np.float64)
    s = (np.max(np.abs(x0), axis=(0,), keepdims=True) / 448.0).astype(np.float32)
    out = {}
    for k, v in d.items():
        if k == 'token_x':
            out['token_x_bytes'] = e4m3fn_bytes(x0 / s.astype(np.float64))
            out['token_x_scale'] = s
        else:
            out[k] = v
    return out


def reference(token_x_bytes, token_x_scale, wq_a, wq_b, wkv, rope_cos, rope_sin, gamma_cq, gamma_ckv):
    return core(e4m3fn_values(token_x_bytes) * token_x_scale.astype(np.float64), wq_a, wq_b, wkv, rope_cos, rope_sin, gamma_cq, gamma_ckv)

@@ -1,0 +1,492 @@
+from contextlib import ExitStack
+
+import concourse.mybir as mybir
+from concourse.masks import make_identity
+
+T, H, QR = 4096, 1024, 512
+NH, DN, DR, KVR = 2, 128, 64, 64
+HALF = DR // 2
+EPS = 1e-6
+OUT_W = NH * (DN + DR) + KVR + DR
+
+FLOPS = 2 * T * (H * (QR + KVR + DR) + QR * NH * (DN + DR))
+
+P = 128
+N_TILES = T // P
+PAIRS = N_TILES // 2
+
+F32 = mybir.dt.float32
+BF16 = mybir.dt.bfloat16
+U32 = mybir.dt.uint32
+U8 = mybir.dt.uint8
+FP8 = mybir.dt.float8_e4m3fn
+FP8X4 = mybir.dt.float8_e4m3fn_x4
+MULT = mybir.AluOpType.mult
+ADD = mybir.AluOpType.add
+ACT = mybir.ActivationFunctionType
+
+STEP = """
+    rope a0 a1 quant_x square_kv square0 mult square1 turn1 add quant_c turn0 kv_rope rms empty1 gain
+    norm0 nope gate ckv norm1 empty0 turn_c0 copy store turn_c1 empty_c
+"""
+FIRST = """
+    mult:0 wa_scalar:1 turn0:0 wa_scalar:0 turn1:0 mult:1 wa_vector:2 wa_vector:3 gamma:0 empty0:0
+    turn0:1 empty1:0 quant_x:0 turn1:1 wb_copy:0 wa_quant:0 wb_copy:2 wb_copy:3 wa_quant:1 a0:0 empty1:1
+    square0:0 a1:0 mult:2 mult:3 square1:0 rms_a:0 norm0:0 dummies:4 turn1:2 empty0:1 wb_copy:1 turn0:2
+    turn_c0:0 empty1:2 table:1 empty0:2 norm1:0 quant_x:1 mult:4 turn_c1:0 wb_quant:0 a0:1 a1:1
+    empty_c:0 square0:1 turn1:3 quant_c:0 kv_rope:0 square1:1 rms_a:1 quant_x:2 table:0 turn0:3 nope:0
+    square_kv:0 norm1:1 norm0:1 empty0:3 mult:5 empty1:3 a1:2 turn_c0:1 square1:2 turn_c1:1 quant_x:3
+    gate:5 rope:0 a0:2 empty_c:1 turn0:4 square0:2 rms_a:2 turn1:4 quant_c:1 copy:0 gain:0 empty1:4
+    empty0:4 kv_rope:1 norm0:2 nope:1 norm1:2 turn_c0:2 copy:1 turn_c1:2 empty_c:2
+"""
+LAST = """
+    a0:-3 square0:-3 gain:-5 quant_x:-2 quant_c:-4 a1:-3 turn1:-1 nope:-4 turn0:-1 kv_rope:-4 square1:-3
+    rope:-5 rms_a:-3 norm0:-3 empty1:-1 norm1:-3 a0:-2 turn_c0:-3 copy:-4 empty0:-1 add:-6 turn_c1:-3
+    a1:-2 quant_x:-1 add:-5 a0:-1 square_kv:-5 rms_kv:-6 rope:-4 rms_kv:-5 square0:-2 empty_c:-3 gain:-4
+    square1:-2 quant_c:-3 a1:-1 rms_a:-2 kv_rope:-3 square0:-1 add:-4 nope:-3 norm0:-2 turn_c0:-2
+    norm1:-2 square1:-1 ckv:-5 gain:-3 rms_a:-1 square_kv:-3 store:-5 norm0:-1 turn_c1:-2 empty_c:-2
+    norm1:-1 turn_c0:-1 quant_c:-2 rope:-3 add_vector:-3 rms_kv:-3 square_kv:-4 copy:-3 turn_c1:-1
+    rms_kv:-4 kv_rope:-2 ckv:-6 store:-6 empty_c:-1 ckv:-4 quant_c:-1 nope:-2 kv_rope:-1 rope:-2 gain:-2
+    ckv:-3 add_vector:-2 nope:-1 copy:-2 square_kv:-2 rms_kv:-2 ckv:-2 rope:-1 store:-4 store:-3 copy:-1
+    gain:-1 store:-2 add_vector:-1 square_kv:-1 rms_kv:-1 ckv:-1 store:-1
+"""
+FIRST_STEP = 5
+NORM_LAG = 2
+KV_LAG = 5
+
+
+def tile_mla_model_t_kernel(
+    tc, x_bytes, x_scale, wq_a, wq_b, wkv, rope_cos, rope_sin, gamma_cq, gamma_ckv, out
+):
+    nc = tc.nc
+    x_hbm = x_bytes.rearrange("(p i) k -> p i k", i=N_TILES)
+    cos_hbm = rope_cos.rearrange("(p i) d -> p i d", i=N_TILES)
+    sin_hbm = rope_sin.rearrange("(p i) d -> p i d", i=N_TILES)
+    out_hbm = out.rearrange("(p i) c -> p i c", i=N_TILES)
+
+    with ExitStack() as ctx:
+        keep = ctx.enter_context(tc.tile_pool(name="keep", bufs=1))
+        work = ctx.enter_context(tc.tile_pool(name="work", bufs=2))
+        ps_x = ctx.enter_context(tc.psum_pool(name="ps_x", bufs=2))
+        ps_a = ctx.enter_context(tc.psum_pool(name="ps_a", bufs=2))
+        ps_c = ctx.enter_context(tc.psum_pool(name="ps_c", bufs=1))
+        ps_q = ctx.enter_context(tc.psum_pool(name="ps_q", bufs=1))
+        ctx.enter_context(tc.manual_schedule())
+
+        x_raw = keep.tile([P, N_TILES * H], U8, name="x_raw")
+        scale_raw = keep.tile([P, 2, 4], F32, name="scale_raw")
+        scale = keep.tile([P, 2, H], F32, name="scale")
+        wa_raw = keep.tile([P, 2, 4, QR], BF16, name="wa_raw")
+        wkv_raw = keep.tile([P, 2, 4, KVR + DR], BF16, name="wkv_raw")
+        wb_raw = keep.tile([P, 4, NH * (DN + DR)], BF16, name="wb_raw")
+        gq_raw = keep.tile([P, QR], BF16, name="gq_raw")
+        gq = keep.tile([P, QR], BF16, name="gq")
+        gkv = keep.tile([P, KVR], BF16, name="gkv")
+        cos = keep.tile([P, N_TILES, DR], BF16, name="cos")
+        sin = keep.tile([P, N_TILES, DR], BF16, name="sin")
+        factors = keep.tile([P, N_TILES, 2, 2, HALF], BF16, name="factors")
+        ident = keep.tile([P, P], F32, name="ident")
+        eps = keep.tile([P, 1], F32, name="eps")
+        zero = keep.tile([P, 512], BF16, name="zero")
+        warm = keep.tile([P, 1], F32, name="warm")
+
+        wa_g = keep.tile([P, 2 * QR * 4], BF16, name="wa_g", align_bytes=64)
+        wa_c = keep.tile([P, 2, QR], U32, name="wa_c", align_bytes=64)
+        wa_s = keep.tile([P, 2, QR], U8, name="wa_s", align_bytes=64)
+        wkv_g = keep.tile([P, 4 * 128 * 4], BF16, name="wkv_g", align_bytes=64)
+        wkv_c = keep.tile([P, 2, 2, 128], U32, name="wkv_c", align_bytes=64)
+        wkv_s = keep.tile([P, 2, 2, 128], U8, name="wkv_s", align_bytes=64)
+        wb_g = keep.tile([P, 384 * 4], BF16, name="wb_g", align_bytes=64)
+        wb_c = keep.tile([P, 384], U32, name="wb_c", align_bytes=64)
+        wb_s = keep.tile([P, 384], U8, name="wb_s", align_bytes=64)
+
+        def load_x(i0, i1):
+            nc.sync.dma_start(
+                out=x_raw[:, i0 * H : i1 * H], in_=x_hbm[:, i0:i1, :].rearrange("p i k -> p (i k)")
+            )
+
+        wa_hbm = wq_a.rearrange("(g p j) c -> g p j c", p=P, j=4)
+        wkv_hbm = wkv.rearrange("(g p j) c -> g p j c", p=P, j=4)
+        nc.sync.dma_start(out=scale_raw[:], in_=x_scale.rearrange("o (h n c) -> n (o h) c", h=2, c=4))
+        load_x(0, 2)
+        load_x(2, 4)
+        nc.sync.dma_start(out=wa_raw[:, 0], in_=wa_hbm[0])
+        nc.sync.dma_start(out=wa_raw[:, 1], in_=wa_hbm[1])
+        nc.sync.dma_start(out=wb_raw[:], in_=wq_b.rearrange("(p j) c -> p j c", j=4))
+        nc.sync.dma_start(out=wkv_raw[:, 0], in_=wkv_hbm[0])
+        nc.sync.dma_start(out=wkv_raw[:, 1], in_=wkv_hbm[1])
+        nc.sync.dma_start(out=gq_raw[:], in_=gamma_cq.partition_broadcast(P))
+        nc.sync.dma_start(out=sin[:], in_=sin_hbm)
+        nc.sync.dma_start(out=cos[:], in_=cos_hbm)
+        load_x(4, 8)
+        nc.sync.dma_start(out=gkv[:], in_=gamma_ckv.partition_broadcast(P))
+        for i0 in range(8, N_TILES, 4):
+            load_x(i0, i0 + 4)
+
+        make_identity(nc, ident[:])
+        nc.gpsimd.memset(zero[:], 0.0)
+        nc.vector.memset(eps[:], EPS)
+        nc.vector.memset(warm[:], 1.0)
+        nc.scalar.activation(warm[:], warm[:], ACT.Abs_reciprocal_sqrt)
+
+        def dummies(count):
+            bank = ps_q.tile([P, OUT_W], F32, name="pr", bufs=2)
+            for i in range(count):
+                nc.tensor.matmul(bank[:], lhsT=zero[:, 0:P], rhs=zero[:], start=True, stop=True)
+
+        dummies(4)
+        for h in range(2):
+            bank = ps_x.tile([P, 4, P], F32, name="xt")
+            for c in range(4):
+                nc.tensor.transpose(bank[:, c, :], scale_raw[:, h, c : c + 1].to_broadcast([P, P]), ident[:])
+            for copy, j in ((nc.vector.tensor_copy, 0), (nc.scalar.copy, 1)):
+                copy(
+                    out=scale[:, j, 512 * h : 512 * (h + 1)].rearrange("p (n c) -> p n c", c=4),
+                    in_=bank[:].rearrange("p c n -> p n c"),
+                )
+
+        state = {}
+
+
+        def wa_copy(engine, part):
+            g, u = divmod(part, 2)
+            engine(
+                out=wa_g[:].rearrange("p (g u m e j) -> p g u m e j", g=2, u=2, e=2, j=4)[:, g, u],
+                in_=wa_raw[:, g].rearrange("p j (m u e) -> p u m e j", u=2, e=2)[:, u],
+            )
+
+        def wa_quant(g):
+            nc.vector.quantize_mx(
+                out=wa_c[:, g, :].bitcast(FP8X4), scales=wa_s[:, g, :], in_=wa_g[:, g * 2048 : (g + 1) * 2048]
+            )
+
+        def gamma_copy(part):
+            nc.scalar.copy(
+                out=gq[:].rearrange("p (u m e) -> p u m e", u=2, e=2),
+                in_=gq_raw[:].rearrange("p (m u e) -> p u m e", u=2, e=2),
+            )
+
+        def wb_copy(part):
+            wb_dst = wb_g[:].rearrange("p (c j) -> p c j", j=4)
+            wb_src = wb_raw[:].rearrange("p j (h c) -> p h c j", h=NH)
+            kv_dst = wkv_g[:].rearrange("p (v g c j) -> p v g c j", v=2, g=2, j=4)
+            kv_src = wkv_raw[:].rearrange("p g j c -> p g c j")
+            if part == 0:
+                nc.scalar.copy(
+                    out=wb_dst[:, 0:256].rearrange("p (h c) j -> p h c j", h=NH), in_=wb_src[:, :, 0:DN]
+                )
+            elif part == 1:
+                nc.scalar.copy(
+                    out=wb_dst[:, 256:384].rearrange("p (h c) j -> p h c j", h=NH), in_=wb_src[:, :, DN:]
+                )
+            elif part == 2:
+                nc.scalar.copy(out=kv_dst[:, 0], in_=kv_src)
+            else:
+                nc.scalar.copy(out=kv_dst[:, 1, :, 0:64], in_=kv_src[:, :, 64:128])
+                nc.scalar.copy(out=kv_dst[:, 1, :, 64:128], in_=kv_src[:, :, 0:64])
+
+        def wb_quant(part):
+            nc.vector.quantize_mx(
+                out=wkv_c[:].rearrange("p v g c -> p (v g c)").bitcast(FP8X4),
+                scales=wkv_s[:].rearrange("p v g c -> p (v g c)"),
+                in_=wkv_g[:],
+            )
+            nc.vector.quantize_mx(out=wb_c[:, 0:256].bitcast(FP8X4), scales=wb_s[:, 0:256], in_=wb_g[:, 0:1024])
+            nc.vector.quantize_mx(out=wb_c[:, 256:384].bitcast(FP8X4), scales=wb_s[:, 256:384], in_=wb_g[:, 1024:1536])
+
+        def rope_table(part):
+            if part == 0:
+                nc.scalar.copy(out=factors[:, :, 0, 1, :], in_=sin[:, :, HALF:])
+                nc.scalar.activation(factors[:, :, 1, 0, :], sin[:, :, 0:HALF], ACT.Copy, scale=-1.0)
+            else:
+                nc.scalar.copy(out=factors[:, :, 0, 0, :], in_=cos[:, :, 0:HALF])
+                nc.scalar.copy(out=factors[:, :, 1, 1, :], in_=cos[:, :, HALF:])
+
+
+        def mult_x(n):
+            xs = work.tile([P, 2 * H], BF16, name="xs", bufs=5)
+            state["xs", n] = xs
+            if n == 0:
+                pieces = ((0, 0, 512), (0, 512, H), (1, 0, H))
+                for j, k0, k1 in pieces:
+                    nc.vector.tensor_tensor(
+                        out=xs[:, j * H + k0 : j * H + k1],
+                        in0=x_raw[:, j * H + k0 : j * H + k1].bitcast(FP8),
+                        in1=scale[:, 0, k0:k1],
+                        op=MULT,
+                    )
+            else:
+                nc.vector.tensor_tensor(
+                    out=xs[:],
+                    in0=x_raw[:, 2 * n * H : 2 * (n + 1) * H].bitcast(FP8),
+                    in1=scale[:].rearrange("p j k -> p (j k)"),
+                    op=MULT,
+                )
+
+        def gate(n):
+            if n < PAIRS:
+                seen = work.tile([P, 1], BF16, name="seen")
+                nc.gpsimd.tensor_copy(out=seen[:], in_=state["xs", n][:, 0:1])
+
+        def turn_x(n, j):
+            xt = ps_x.tile([P, 4, P], F32, name="xt")
+            words = state["xs", n][:, j * H : (j + 1) * H].bitcast(F32)
+            for g in range(2):
+                for u in range(2):
+                    nc.tensor.transpose(xt[:, 2 * g + u, :], words[:, 256 * g + u : 256 * (g + 1) : 2], ident[:])
+            state["xt", n, j] = xt
+
+        def empty_x(n, j):
+            if ("xg", n) not in state:
+                state["xg", n] = work.tile([P, 2 * H], BF16, name="xg", bufs=4, align_bytes=64)
+            view = state["xg", n][:].bitcast(F32).rearrange("p (j g n u) -> p j g n u", j=2, g=2, u=2)
+            nc.scalar.copy(out=view[:, j], in_=state["xt", n, j][:].rearrange("p (g u) n -> p g n u", g=2))
+
+        def quant_x(n):
+            xc = work.tile([P, 512], U32, name="xc", bufs=7, align_bytes=64)
+            xsc = work.tile([P, 512], U8, name="xsc", bufs=7, align_bytes=64)
+            nc.vector.quantize_mx(out=xc[:].bitcast(FP8X4), scales=xsc[:], in_=state["xg", n][:])
+            state["xc", n] = (xc, xsc)
+
+
+        def mm_a(n, j):
+            xc, xsc = state["xc", n]
+            if n == PAIRS - 1:
+                bank = ps_x.tile([P, 4, P], F32, name="xt")
+                pa = bank[:].rearrange("p a b -> p (a b)")
+            else:
+                bank = ps_a.tile([P, QR], F32, name="pa")
+                pa = bank[:]
+            for g in range(2):
+                cols = slice((2 * j + g) * P, (2 * j + g + 1) * P)
+                nc.tensor.matmul_mx(
+                    out=pa,
+                    lhsT=xc[:, cols].bitcast(FP8X4),
+                    lhsT_scale=xsc[:, cols],
+                    rhs=wa_c[:, g, :].bitcast(FP8X4),
+                    rhs_scale=wa_s[:, g, :],
+                    start=(g == 0),
+                    stop=(g == 1),
+                )
+            state["pa", n, j] = pa
+
+        def stat(kind, s):
+            if (kind, s) not in state:
+                state[kind, s] = work.tile([P, 4], F32, name=kind, bufs=6)
+            return state[kind, s]
+
+        def square_a(n, j):
+            squares = work.tile([P, QR], BF16, name="squares_a")
+            mean = stat("mean", n + NORM_LAG)
+            nc.scalar.activation(
+                squares[:], state["pa", n, j], ACT.Square, scale=QR**-0.5, accum_out=mean[:, j : j + 1]
+            )
+
+        def inverse_rms(s, c0, c1):
+            nc.scalar.activation(
+                stat("rinv", s)[:, c0:c1], stat("mean", s)[:, c0:c1], ACT.Abs_reciprocal_sqrt, bias=eps[:]
+            )
+
+        def norm_a(n, j):
+            cq = work.tile([P, QR], BF16, name="cq", bufs=4)
+            nc.vector.scalar_tensor_tensor(
+                out=cq[:],
+                in0=state["pa", n, j],
+                scalar=stat("rinv", n + NORM_LAG)[:, j : j + 1],
+                in1=gq[:],
+                op0=MULT,
+                op1=MULT,
+            )
+            state["cq", n, j] = cq
+
+        def turn_c(n, j):
+            if j == 0:
+                state["ct", n] = ps_c.tile([P, 2, 2, P], F32, name="ct")
+            words = state["cq", n, j][:].bitcast(F32)
+            for u in range(2):
+                nc.tensor.transpose(state["ct", n][:, j, u, :], words[:, u * P : (u + 1) * P], ident[:])
+
+        def empty_c(n):
+            cg = work.tile([P, 1024], BF16, name="cg", bufs=4, align_bytes=64)
+            nc.scalar.copy(
+                out=cg[:].bitcast(F32).rearrange("p (j n u) -> p j n u", j=2, u=2),
+                in_=state["ct", n][:].rearrange("p j u n -> p j n u"),
+            )
+            state["cg", n] = cg
+
+        def quant_c(n):
+            cc = work.tile([P, 256], U32, name="cc", bufs=4, align_bytes=64)
+            cs = work.tile([P, 256], U8, name="cs", bufs=4, align_bytes=64)
+            nc.vector.quantize_mx(out=cc[:].bitcast(FP8X4), scales=cs[:], in_=state["cg", n][:])
+            state["cc", n] = (cc, cs)
+
+
+        def mm_kv_rope(n):
+            cc, cs = state["cc", n]
+            xc, xsc = state["xc", n]
+            pr = ps_q.tile([P, OUT_W], F32, name="pr", bufs=2)
+            for j in range(2):
+                cols = slice(j * P, (j + 1) * P)
+                for g in range(2):
+                    xcols = slice((2 * j + g) * P, (2 * j + g + 1) * P)
+                    nc.tensor.matmul_mx(
+                        out=pr[:, 384 * j : 384 * j + 128],
+                        lhsT=xc[:, xcols].bitcast(FP8X4),
+                        lhsT_scale=xsc[:, xcols],
+                        rhs=wkv_c[:, j, g, :].bitcast(FP8X4),
+                        rhs_scale=wkv_s[:, j, g, :],
+                        start=(g == 0),
+                        stop=(g == 1),
+                    )
+                nc.tensor.matmul_mx(
+                    out=pr[:, 128 + 128 * j : 256 + 128 * j],
+                    lhsT=cc[:, cols].bitcast(FP8X4),
+                    lhsT_scale=cs[:, cols],
+                    rhs=wb_c[:, 256:384].bitcast(FP8X4),
+                    rhs_scale=wb_s[:, 256:384],
+                    start=True,
+                    stop=True,
+                )
+            state["pr", n] = pr
+
+        def mm_nope(n):
+            cc, cs = state["cc", n]
+            pn = ps_q.tile([P, 2, 256], F32, name="pn", bufs=1)
+            for j in range(2):
+                cols = slice(j * P, (j + 1) * P)
+                nc.tensor.matmul_mx(
+                    out=pn[:, j, :],
+                    lhsT=cc[:, cols].bitcast(FP8X4),
+                    lhsT_scale=cs[:, cols],
+                    rhs=wb_c[:, 0:256].bitcast(FP8X4),
+                    rhs_scale=wb_s[:, 0:256],
+                    start=True,
+                    stop=True,
+                )
+            state["pn", n] = pn
+
+
+        def out_tile(n):
+            if ("ot", n) not in state:
+                state["ot", n] = work.tile([P, 1152], F32, name="ot", bufs=6)
+            return state["ot", n]
+
+        def copy_nope(n):
+            nc.scalar.copy(
+                out=out_tile(n)[:, 128:896].rearrange("p (h c) -> p h c", c=DN + DR)[:, :, 0:DN],
+                in_=state["pn", n][:].rearrange("p j (h c) -> p (j h) c", h=NH),
+            )
+
+        def square_kv(n):
+            mean = stat("mean", n + KV_LAG)
+            for j in range(2):
+                squares = work.tile([P, KVR], BF16, name="squares_kv")
+                nc.scalar.activation(
+                    squares[:],
+                    state["pr", n][:, 448 * j : 448 * j + KVR],
+                    ACT.Square,
+                    scale=KVR**-0.5,
+                    accum_out=mean[:, 2 + j : 3 + j],
+                )
+
+        def gain_kv(n):
+            gained = work.tile([P, 2, KVR], F32, name="gained", bufs=5)
+            nc.vector.tensor_tensor(
+                out=gained[:],
+                in0=state["pr", n][:].rearrange("p (b c) -> p b c", c=KVR)[:, 0:8:7, :],
+                in1=gkv[:].unsqueeze(1).to_broadcast([P, 2, KVR]),
+                op=MULT,
+            )
+            state["gained", n] = gained
+
+        def scale_ckv(n):
+            for j in range(2):
+                nc.scalar.activation(
+                    out_tile(n)[:, 960 * j : 960 * j + KVR],
+                    state["gained", n][:, j, :],
+                    ACT.Copy,
+                    scale=stat("rinv", n + KV_LAG)[:, 2 + j : 3 + j],
+                )
+
+        def rope_products(n):
+            products = work.tile([P, 6, 2, 2, HALF], F32, name="products", bufs=4)
+            nc.vector.tensor_tensor(
+                out=products[:].rearrange("p (j s) h w d -> p j s h w d", j=2),
+                in0=state["pr", n][:, 64:448]
+                .rearrange("p (j s h d) -> p j s h d", j=2, s=3, h=2)
+                .unsqueeze(4)
+                .to_broadcast([P, 2, 3, 2, 2, HALF]),
+                in1=factors[:, 2 * n : 2 * n + 2].unsqueeze(2).to_broadcast([P, 2, 3, 2, 2, HALF]),
+                op=MULT,
+            )
+            state["products", n] = products
+
+        def rope_add(n, engine):
+            products = state["products", n][:].rearrange("p s h w d -> p s h (w d)")
+            engine.tensor_tensor(
+                out=out_tile(n)[:].rearrange("p (s c) -> p s c", c=DN + DR)[:, :, 64:128],
+                in0=products[:, :, 0, :],
+                in1=products[:, :, 1, :],
+                op=ADD,
+            )
+
+        def store(n):
+            ot = out_tile(n)
+            nc.sync.dma_start(
+                out=out_hbm[:, 2 * n : 2 * n + 2, 0:384], in_=ot[:, 128:896].rearrange("p (j c) -> p j c", j=2)
+            )
+            nc.sync.dma_start(
+                out=out_hbm[:, 2 * n : 2 * n + 2, 384:512],
+                in_=ot[:].rearrange("p (b c) -> p b c", c=192)[:, 0:6:5, 0:128],
+            )
+
+        OPS = dict(
+            mult=(-1, mult_x),
+            gate=(-1, gate),
+            turn0=(0, lambda n: turn_x(n, 0)),
+            turn1=(0, lambda n: turn_x(n, 1)),
+            empty0=(0, lambda n: empty_x(n, 0)),
+            empty1=(0, lambda n: empty_x(n, 1)),
+            quant_x=(1, quant_x),
+            a0=(NORM_LAG, lambda n: mm_a(n, 0)),
+            a1=(NORM_LAG, lambda n: mm_a(n, 1)),
+            square0=(NORM_LAG, lambda n: square_a(n, 0)),
+            square1=(NORM_LAG, lambda n: square_a(n, 1)),
+            norm0=(NORM_LAG, lambda n: norm_a(n, 0)),
+            norm1=(NORM_LAG, lambda n: norm_a(n, 1)),
+            turn_c0=(NORM_LAG, lambda n: turn_c(n, 0)),
+            turn_c1=(NORM_LAG, lambda n: turn_c(n, 1)),
+            empty_c=(NORM_LAG, empty_c),
+            quant_c=(3, quant_c),
+            kv_rope=(3, mm_kv_rope),
+            nope=(3, mm_nope),
+            copy=(3, copy_nope),
+            rope=(4, rope_products),
+            gain=(4, gain_kv),
+            square_kv=(4, square_kv),
+            add=(5, lambda n: rope_add(n, nc.gpsimd)),
+            add_vector=(5, lambda n: rope_add(n, nc.vector)),
+            ckv=(KV_LAG, scale_ckv),
+            store=(5, store),
+            rms=(0, lambda s: inverse_rms(s, 0, 4)),
+            rms_a=(0, lambda n: inverse_rms(n + NORM_LAG, 0, 2)),
+            rms_kv=(0, lambda n: inverse_rms(n + KV_LAG, 2, 4)),
+            wa_scalar=(0, lambda part: wa_copy(nc.scalar.copy, part)),
+            wa_vector=(0, lambda part: wa_copy(nc.vector.tensor_copy, part)),
+            wa_quant=(0, wa_quant),
+            gamma=(0, gamma_copy),
+            wb_copy=(0, wb_copy),
+            wb_quant=(0, wb_quant),
+            table=(0, rope_table),
+            dummies=(0, dummies),
+        )
+        for word in FIRST.split():
+            stage, number = word.split(":")
+            OPS[stage][1](int(number))
+        for s in range(FIRST_STEP, PAIRS - 1):
+            for stage in STEP.split():
+                lag, run = OPS[stage]
+                run(s - lag)
+        for word in LAST.split():
+            stage, number = word.split(":")
+            OPS[stage][1](PAIRS + int(number))

@@ -14,6 +14,7 @@ FLOPS = 2 * T * (H * (QR + KVR + DR) + QR * NH * (DN + DR))
 P = 128
 N_TILES = T // P
 PAIRS = N_TILES // 2
+ROPED_ON_VECTOR = 2
 
 F32 = mybir.dt.float32
 BF16 = mybir.dt.bfloat16
@@ -24,35 +25,6 @@ FP8X4 = mybir.dt.float8_e4m3fn_x4
 MULT = mybir.AluOpType.mult
 ADD = mybir.AluOpType.add
 ACT = mybir.ActivationFunctionType
-
-STEP = """
-    rope a0 a1 quant_x square_kv square0 mult square1 turn1 add quant_c turn0 kv_rope rms empty1 gain
-    norm0 nope gate ckv norm1 empty0 turn_c0 copy store turn_c1 empty_c
-"""
-FIRST = """
-    mult:0 wa_scalar:1 turn0:0 wa_scalar:0 turn1:0 mult:1 wa_vector:2 wa_vector:3 gamma:0 empty0:0
-    turn0:1 empty1:0 quant_x:0 turn1:1 wb_copy:0 wa_quant:0 wb_copy:2 wb_copy:3 wa_quant:1 a0:0 empty1:1
-    square0:0 a1:0 mult:2 mult:3 square1:0 rms_a:0 norm0:0 dummies:4 turn1:2 empty0:1 wb_copy:1 turn0:2
-    turn_c0:0 empty1:2 table:1 empty0:2 norm1:0 quant_x:1 mult:4 turn_c1:0 wb_quant:0 a0:1 a1:1
-    empty_c:0 square0:1 turn1:3 quant_c:0 kv_rope:0 square1:1 rms_a:1 quant_x:2 table:0 turn0:3 nope:0
-    square_kv:0 norm1:1 norm0:1 empty0:3 mult:5 empty1:3 a1:2 turn_c0:1 square1:2 turn_c1:1 quant_x:3
-    gate:5 rope:0 a0:2 empty_c:1 turn0:4 square0:2 rms_a:2 turn1:4 quant_c:1 copy:0 gain:0 empty1:4
-    empty0:4 kv_rope:1 norm0:2 nope:1 norm1:2 turn_c0:2 copy:1 turn_c1:2 empty_c:2
-"""
-LAST = """
-    a0:-3 square0:-3 gain:-5 quant_x:-2 quant_c:-4 a1:-3 turn1:-1 nope:-4 turn0:-1 kv_rope:-4 square1:-3
-    rope:-5 rms_a:-3 norm0:-3 empty1:-1 norm1:-3 a0:-2 turn_c0:-3 copy:-4 empty0:-1 add:-6 turn_c1:-3
-    a1:-2 quant_x:-1 add:-5 a0:-1 square_kv:-5 rms_kv:-6 rope:-4 rms_kv:-5 square0:-2 empty_c:-3 gain:-4
-    square1:-2 quant_c:-3 a1:-1 rms_a:-2 kv_rope:-3 square0:-1 add:-4 nope:-3 norm0:-2 turn_c0:-2
-    norm1:-2 square1:-1 ckv:-5 gain:-3 rms_a:-1 square_kv:-3 store:-5 norm0:-1 turn_c1:-2 empty_c:-2
-    norm1:-1 turn_c0:-1 quant_c:-2 rope:-3 add_vector:-3 rms_kv:-3 square_kv:-4 copy:-3 turn_c1:-1
-    rms_kv:-4 kv_rope:-2 ckv:-6 store:-6 empty_c:-1 ckv:-4 quant_c:-1 nope:-2 kv_rope:-1 rope:-2 gain:-2
-    ckv:-3 add_vector:-2 nope:-1 copy:-2 square_kv:-2 rms_kv:-2 ckv:-2 rope:-1 store:-4 store:-3 copy:-1
-    gain:-1 store:-2 add_vector:-1 square_kv:-1 rms_kv:-1 ckv:-1 store:-1
-"""
-FIRST_STEP = 5
-NORM_LAG = 2
-KV_LAG = 5
 
 
 def tile_mla_model_t_kernel(
@@ -70,13 +42,13 @@ def tile_mla_model_t_kernel(
         ps_x = ctx.enter_context(tc.psum_pool(name="ps_x", bufs=2))
         ps_a = ctx.enter_context(tc.psum_pool(name="ps_a", bufs=2))
         ps_c = ctx.enter_context(tc.psum_pool(name="ps_c", bufs=1))
-        ps_q = ctx.enter_context(tc.psum_pool(name="ps_q", bufs=1))
+        ps_n = ctx.enter_context(tc.psum_pool(name="ps_n", bufs=1))
+        ps_r = ctx.enter_context(tc.psum_pool(name="ps_r", bufs=2))
         ctx.enter_context(tc.manual_schedule())
 
         x_raw = keep.tile([P, N_TILES * H], U8, name="x_raw")
-        scale_raw = keep.tile([P, 2, 4], F32, name="scale_raw")
-        scale = keep.tile([P, 2, H], F32, name="scale")
-        wa_raw = keep.tile([P, 2, 4, QR], BF16, name="wa_raw")
+        scale = keep.tile([P, 2, 4], F32, name="scale")
+        wa_raw = [keep.tile([P, 4, QR // 2], BF16, name="wa_raw%d" % part) for part in range(4)]
         wkv_raw = keep.tile([P, 2, 4, KVR + DR], BF16, name="wkv_raw")
         wb_raw = keep.tile([P, 4, NH * (DN + DR)], BF16, name="wb_raw")
         gq_raw = keep.tile([P, QR], BF16, name="gq_raw")
@@ -86,9 +58,8 @@ def tile_mla_model_t_kernel(
         sin = keep.tile([P, N_TILES, DR], BF16, name="sin")
         factors = keep.tile([P, N_TILES, 2, 2, HALF], BF16, name="factors")
         ident = keep.tile([P, P], F32, name="ident")
+        one = keep.tile([P, 1], F32, name="one")
         eps = keep.tile([P, 1], F32, name="eps")
-        zero = keep.tile([P, 512], BF16, name="zero")
-        warm = keep.tile([P, 1], F32, name="warm")
 
         wa_g = keep.tile([P, 2 * QR * 4], BF16, name="wa_g", align_bytes=64)
         wa_c = keep.tile([P, 2, QR], U32, name="wa_c", align_bytes=64)
@@ -105,54 +76,43 @@ def tile_mla_model_t_kernel(
                 out=x_raw[:, i0 * H : i1 * H], in_=x_hbm[:, i0:i1, :].rearrange("p i k -> p (i k)")
             )
 
-        wa_hbm = wq_a.rearrange("(g p j) c -> g p j c", p=P, j=4)
-        wkv_hbm = wkv.rearrange("(g p j) c -> g p j c", p=P, j=4)
-        nc.sync.dma_start(out=scale_raw[:], in_=x_scale.rearrange("o (h n c) -> n (o h) c", h=2, c=4))
-        load_x(0, 2)
+        def load_wa(part):
+            g, half = divmod(part, 2)
+            rows = wq_a.rearrange("(g p j) c -> g p j c", p=P, j=4)[g]
+            nc.sync.dma_start(out=wa_raw[part][:], in_=rows[:, :, 256 * half : 256 * (half + 1)])
+
+        load_wa(0)
+        load_x(0, 1)
+        nc.sync.dma_start(out=scale[:], in_=x_scale.rearrange("o (g p t) -> p (o g) t", g=2, t=4))
+        load_wa(1)
+        load_x(1, 2)
+        load_wa(2)
+        load_wa(3)
         load_x(2, 4)
-        nc.sync.dma_start(out=wa_raw[:, 0], in_=wa_hbm[0])
-        nc.sync.dma_start(out=wa_raw[:, 1], in_=wa_hbm[1])
-        nc.sync.dma_start(out=wb_raw[:], in_=wq_b.rearrange("(p j) c -> p j c", j=4))
-        nc.sync.dma_start(out=wkv_raw[:, 0], in_=wkv_hbm[0])
-        nc.sync.dma_start(out=wkv_raw[:, 1], in_=wkv_hbm[1])
+        nc.sync.dma_start(out=wkv_raw[:], in_=wkv.rearrange("(g p j) c -> p g j c", p=P, j=4))
+        load_x(4, 6)
         nc.sync.dma_start(out=gq_raw[:], in_=gamma_cq.partition_broadcast(P))
+        nc.sync.dma_start(out=wb_raw[:], in_=wq_b.rearrange("(p j) c -> p j c", j=4))
+        load_x(6, 8)
         nc.sync.dma_start(out=sin[:], in_=sin_hbm)
         nc.sync.dma_start(out=cos[:], in_=cos_hbm)
-        load_x(4, 8)
         nc.sync.dma_start(out=gkv[:], in_=gamma_ckv.partition_broadcast(P))
         for i0 in range(8, N_TILES, 4):
             load_x(i0, i0 + 4)
 
         make_identity(nc, ident[:])
-        nc.gpsimd.memset(zero[:], 0.0)
-        nc.vector.memset(eps[:], EPS)
-        nc.vector.memset(warm[:], 1.0)
-        nc.scalar.activation(warm[:], warm[:], ACT.Abs_reciprocal_sqrt)
-
-        def dummies(count):
-            bank = ps_q.tile([P, OUT_W], F32, name="pr", bufs=2)
-            for i in range(count):
-                nc.tensor.matmul(bank[:], lhsT=zero[:, 0:P], rhs=zero[:], start=True, stop=True)
-
-        dummies(4)
-        for h in range(2):
-            bank = ps_x.tile([P, 4, P], F32, name="xt")
-            for c in range(4):
-                nc.tensor.transpose(bank[:, c, :], scale_raw[:, h, c : c + 1].to_broadcast([P, P]), ident[:])
-            for copy, j in ((nc.vector.tensor_copy, 0), (nc.scalar.copy, 1)):
-                copy(
-                    out=scale[:, j, 512 * h : 512 * (h + 1)].rearrange("p (n c) -> p n c", c=4),
-                    in_=bank[:].rearrange("p c n -> p n c"),
-                )
+        nc.vector.memset(one[:], 1.0)
+        nc.scalar.activation(eps[:], one[:], ACT.Abs_reciprocal_sqrt, scale=EPS**-2)
 
         state = {}
 
 
-        def wa_copy(engine, part):
-            g, u = divmod(part, 2)
-            engine(
-                out=wa_g[:].rearrange("p (g u m e j) -> p g u m e j", g=2, u=2, e=2, j=4)[:, g, u],
-                in_=wa_raw[:, g].rearrange("p j (m u e) -> p u m e j", u=2, e=2)[:, u],
+        def wa_copy(part):
+            g, half = divmod(part, 2)
+            grouped = wa_g[:].rearrange("p (g u m e j) -> p g u m e j", g=2, u=2, e=2, j=4)
+            nc.vector.tensor_copy(
+                out=grouped[:, g, :, 64 * half : 64 * (half + 1)],
+                in_=wa_raw[part][:].rearrange("p j (m u e) -> p u m e j", u=2, e=2),
             )
 
         def wa_quant(g):
@@ -160,42 +120,37 @@ def tile_mla_model_t_kernel(
                 out=wa_c[:, g, :].bitcast(FP8X4), scales=wa_s[:, g, :], in_=wa_g[:, g * 2048 : (g + 1) * 2048]
             )
 
-        def gamma_copy(part):
+        def gamma_copy():
             nc.scalar.copy(
                 out=gq[:].rearrange("p (u m e) -> p u m e", u=2, e=2),
                 in_=gq_raw[:].rearrange("p (m u e) -> p u m e", u=2, e=2),
             )
 
-        def wb_copy(part):
-            wb_dst = wb_g[:].rearrange("p (c j) -> p c j", j=4)
-            wb_src = wb_raw[:].rearrange("p j (h c) -> p h c j", h=NH)
+        def wkv_copy():
             kv_dst = wkv_g[:].rearrange("p (v g c j) -> p v g c j", v=2, g=2, j=4)
             kv_src = wkv_raw[:].rearrange("p g j c -> p g c j")
-            if part == 0:
-                nc.scalar.copy(
-                    out=wb_dst[:, 0:256].rearrange("p (h c) j -> p h c j", h=NH), in_=wb_src[:, :, 0:DN]
-                )
-            elif part == 1:
-                nc.scalar.copy(
-                    out=wb_dst[:, 256:384].rearrange("p (h c) j -> p h c j", h=NH), in_=wb_src[:, :, DN:]
-                )
-            elif part == 2:
-                nc.scalar.copy(out=kv_dst[:, 0], in_=kv_src)
-            else:
-                nc.scalar.copy(out=kv_dst[:, 1, :, 0:64], in_=kv_src[:, :, 64:128])
-                nc.scalar.copy(out=kv_dst[:, 1, :, 64:128], in_=kv_src[:, :, 0:64])
+            nc.scalar.copy(out=kv_dst[:, 0], in_=kv_src)
+            nc.scalar.copy(out=kv_dst[:, 1, :, 0:64], in_=kv_src[:, :, 64:128])
+            nc.scalar.copy(out=kv_dst[:, 1, :, 64:128], in_=kv_src[:, :, 0:64])
 
-        def wb_quant(part):
+        def wb_copy():
+            wb_dst = wb_g[:].rearrange("p (c j) -> p c j", j=4)
+            wb_src = wb_raw[:].rearrange("p j (h c) -> p h c j", h=NH)
+            nc.scalar.copy(out=wb_dst[:, 0:256].rearrange("p (h c) j -> p h c j", h=NH), in_=wb_src[:, :, 0:DN])
+            nc.scalar.copy(out=wb_dst[:, 256:384].rearrange("p (h c) j -> p h c j", h=NH), in_=wb_src[:, :, DN:])
+
+        def wkv_quant():
             nc.vector.quantize_mx(
                 out=wkv_c[:].rearrange("p v g c -> p (v g c)").bitcast(FP8X4),
                 scales=wkv_s[:].rearrange("p v g c -> p (v g c)"),
                 in_=wkv_g[:],
             )
-            nc.vector.quantize_mx(out=wb_c[:, 0:256].bitcast(FP8X4), scales=wb_s[:, 0:256], in_=wb_g[:, 0:1024])
-            nc.vector.quantize_mx(out=wb_c[:, 256:384].bitcast(FP8X4), scales=wb_s[:, 256:384], in_=wb_g[:, 1024:1536])
 
-        def rope_table(part):
-            if part == 0:
+        def wb_quant():
+            nc.vector.quantize_mx(out=wb_c[:].bitcast(FP8X4), scales=wb_s[:], in_=wb_g[:])
+
+        def rope_table(source):
+            if source is sin:
                 nc.scalar.copy(out=factors[:, :, 0, 1, :], in_=sin[:, :, HALF:])
                 nc.scalar.activation(factors[:, :, 1, 0, :], sin[:, :, 0:HALF], ACT.Copy, scale=-1.0)
             else:
@@ -203,64 +158,47 @@ def tile_mla_model_t_kernel(
                 nc.scalar.copy(out=factors[:, :, 1, 1, :], in_=cos[:, :, HALF:])
 
 
-        def mult_x(n):
-            xs = work.tile([P, 2 * H], BF16, name="xs", bufs=5)
-            state["xs", n] = xs
-            if n == 0:
-                pieces = ((0, 0, 512), (0, 512, H), (1, 0, H))
-                for j, k0, k1 in pieces:
-                    nc.vector.tensor_tensor(
-                        out=xs[:, j * H + k0 : j * H + k1],
-                        in0=x_raw[:, j * H + k0 : j * H + k1].bitcast(FP8),
-                        in1=scale[:, 0, k0:k1],
-                        op=MULT,
-                    )
-            else:
-                nc.vector.tensor_tensor(
-                    out=xs[:],
-                    in0=x_raw[:, 2 * n * H : 2 * (n + 1) * H].bitcast(FP8),
-                    in1=scale[:].rearrange("p j k -> p (j k)"),
-                    op=MULT,
-                )
-
-        def gate(n):
-            if n < PAIRS:
-                seen = work.tile([P, 1], BF16, name="seen")
-                nc.gpsimd.tensor_copy(out=seen[:], in_=state["xs", n][:, 0:1])
+        def widen(n, j):
+            i = 2 * n + j
+            xw = work.tile([P, H], BF16, name="xw", bufs=6)
+            nc.scalar.copy(out=xw[:], in_=x_raw[:, i * H : (i + 1) * H].bitcast(FP8))
+            state["xw", n, j] = xw
 
         def turn_x(n, j):
-            xt = ps_x.tile([P, 4, P], F32, name="xt")
-            words = state["xs", n][:, j * H : (j + 1) * H].bitcast(F32)
+            xt = ps_x.tile([P, 2, 2, P], F32, name="xt")
+            words = state["xw", n, j][:].bitcast(F32)
             for g in range(2):
                 for u in range(2):
-                    nc.tensor.transpose(xt[:, 2 * g + u, :], words[:, 256 * g + u : 256 * (g + 1) : 2], ident[:])
+                    nc.tensor.transpose(xt[:, u, g, :], words[:, 256 * g + u : 256 * (g + 1) : 2], ident[:])
             state["xt", n, j] = xt
 
-        def empty_x(n, j):
-            if ("xg", n) not in state:
-                state["xg", n] = work.tile([P, 2 * H], BF16, name="xg", bufs=4, align_bytes=64)
-            view = state["xg", n][:].bitcast(F32).rearrange("p (j g n u) -> p j g n u", j=2, g=2, u=2)
-            nc.scalar.copy(out=view[:, j], in_=state["xt", n, j][:].rearrange("p (g u) n -> p g n u", g=2))
+        def scale_x(n, j):
+            if j == 0:
+                state["xg", n] = work.tile([P, 2 * H], BF16, name="xg", bufs=2, align_bytes=64)
+            nc.vector.tensor_tensor(
+                out=state["xg", n][:, j * H : (j + 1) * H].rearrange("p (g n u e) -> p g n u e", g=2, u=2, e=2),
+                in0=state["xt", n, j][:]
+                .rearrange("p u g n -> p (u g n)")
+                .bitcast(BF16)
+                .rearrange("p (u g n e) -> p g n u e", u=2, g=2, e=2),
+                in1=scale[:].rearrange("p g (u e) -> p g u e", u=2).unsqueeze(2).to_broadcast([P, 2, P, 2, 2]),
+                op=MULT,
+            )
 
         def quant_x(n):
-            xc = work.tile([P, 512], U32, name="xc", bufs=7, align_bytes=64)
-            xsc = work.tile([P, 512], U8, name="xsc", bufs=7, align_bytes=64)
+            xc = work.tile([P, 512], U32, name="xc", bufs=4, align_bytes=64)
+            xsc = work.tile([P, 512], U8, name="xsc", bufs=4, align_bytes=64)
             nc.vector.quantize_mx(out=xc[:].bitcast(FP8X4), scales=xsc[:], in_=state["xg", n][:])
             state["xc", n] = (xc, xsc)
 
 
         def mm_a(n, j):
             xc, xsc = state["xc", n]
-            if n == PAIRS - 1:
-                bank = ps_x.tile([P, 4, P], F32, name="xt")
-                pa = bank[:].rearrange("p a b -> p (a b)")
-            else:
-                bank = ps_a.tile([P, QR], F32, name="pa")
-                pa = bank[:]
+            pa = ps_a.tile([P, QR], F32, name="pa")
             for g in range(2):
                 cols = slice((2 * j + g) * P, (2 * j + g + 1) * P)
                 nc.tensor.matmul_mx(
-                    out=pa,
+                    out=pa[:],
                     lhsT=xc[:, cols].bitcast(FP8X4),
                     lhsT_scale=xsc[:, cols],
                     rhs=wa_c[:, g, :].bitcast(FP8X4),
@@ -270,29 +208,28 @@ def tile_mla_model_t_kernel(
                 )
             state["pa", n, j] = pa
 
-        def stat(kind, s):
-            if (kind, s) not in state:
-                state[kind, s] = work.tile([P, 4], F32, name=kind, bufs=6)
-            return state[kind, s]
+        def stat(kind, n):
+            if (kind, n) not in state:
+                state[kind, n] = work.tile([P, 4], F32, name=kind, bufs=4)
+            return state[kind, n]
 
         def square_a(n, j):
             squares = work.tile([P, QR], BF16, name="squares_a")
-            mean = stat("mean", n + NORM_LAG)
             nc.scalar.activation(
-                squares[:], state["pa", n, j], ACT.Square, scale=QR**-0.5, accum_out=mean[:, j : j + 1]
+                squares[:], state["pa", n, j][:], ACT.Square, scale=QR**-0.5, accum_out=stat("mean", n)[:, 1 - j : 2 - j]
             )
 
-        def inverse_rms(s, c0, c1):
+        def inverse_rms(n, c0, c1):
             nc.scalar.activation(
-                stat("rinv", s)[:, c0:c1], stat("mean", s)[:, c0:c1], ACT.Abs_reciprocal_sqrt, bias=eps[:]
+                stat("rinv", n)[:, c0:c1], stat("mean", n)[:, c0:c1], ACT.Abs_reciprocal_sqrt, bias=eps[:]
             )
 
         def norm_a(n, j):
-            cq = work.tile([P, QR], BF16, name="cq", bufs=4)
+            cq = work.tile([P, QR], BF16, name="cq", bufs=3)
             nc.vector.scalar_tensor_tensor(
                 out=cq[:],
-                in0=state["pa", n, j],
-                scalar=stat("rinv", n + NORM_LAG)[:, j : j + 1],
+                in0=state["pa", n, j][:],
+                scalar=stat("rinv", n)[:, 1 - j : 2 - j],
                 in1=gq[:],
                 op0=MULT,
                 op1=MULT,
@@ -306,8 +243,11 @@ def tile_mla_model_t_kernel(
             for u in range(2):
                 nc.tensor.transpose(state["ct", n][:, j, u, :], words[:, u * P : (u + 1) * P], ident[:])
 
+        def shared(n, shape, dtype):
+            return work.tile(shape, dtype, name="shared%d" % (n % 2), bufs=1, align_bytes=64)
+
         def empty_c(n):
-            cg = work.tile([P, 1024], BF16, name="cg", bufs=4, align_bytes=64)
+            cg = shared(n, [P, 1024], BF16)
             nc.scalar.copy(
                 out=cg[:].bitcast(F32).rearrange("p (j n u) -> p j n u", j=2, u=2),
                 in_=state["ct", n][:].rearrange("p j u n -> p j n u"),
@@ -315,8 +255,8 @@ def tile_mla_model_t_kernel(
             state["cg", n] = cg
 
         def quant_c(n):
-            cc = work.tile([P, 256], U32, name="cc", bufs=4, align_bytes=64)
-            cs = work.tile([P, 256], U8, name="cs", bufs=4, align_bytes=64)
+            cc = work.tile([P, 256], U32, name="cc", bufs=2, align_bytes=64)
+            cs = work.tile([P, 256], U8, name="cs", bufs=2, align_bytes=64)
             nc.vector.quantize_mx(out=cc[:].bitcast(FP8X4), scales=cs[:], in_=state["cg", n][:])
             state["cc", n] = (cc, cs)
 
@@ -324,9 +264,8 @@ def tile_mla_model_t_kernel(
         def mm_kv_rope(n):
             cc, cs = state["cc", n]
             xc, xsc = state["xc", n]
-            pr = ps_q.tile([P, OUT_W], F32, name="pr", bufs=2)
+            pr = ps_r.tile([P, OUT_W], F32, name="pr")
             for j in range(2):
-                cols = slice(j * P, (j + 1) * P)
                 for g in range(2):
                     xcols = slice((2 * j + g) * P, (2 * j + g + 1) * P)
                     nc.tensor.matmul_mx(
@@ -338,6 +277,8 @@ def tile_mla_model_t_kernel(
                         start=(g == 0),
                         stop=(g == 1),
                     )
+            for j in range(2):
+                cols = slice(j * P, (j + 1) * P)
                 nc.tensor.matmul_mx(
                     out=pr[:, 128 + 128 * j : 256 + 128 * j],
                     lhsT=cc[:, cols].bitcast(FP8X4),
@@ -351,7 +292,7 @@ def tile_mla_model_t_kernel(
 
         def mm_nope(n):
             cc, cs = state["cc", n]
-            pn = ps_q.tile([P, 2, 256], F32, name="pn", bufs=1)
+            pn = ps_n.tile([P, 2, 256], F32, name="pn")
             for j in range(2):
                 cols = slice(j * P, (j + 1) * P)
                 nc.tensor.matmul_mx(
@@ -368,7 +309,7 @@ def tile_mla_model_t_kernel(
 
         def out_tile(n):
             if ("ot", n) not in state:
-                state["ot", n] = work.tile([P, 1152], F32, name="ot", bufs=6)
+                state["ot", n] = work.tile([P, 1152], F32, name="ot", bufs=4)
             return state["ot", n]
 
         def copy_nope(n):
@@ -377,8 +318,13 @@ def tile_mla_model_t_kernel(
                 in_=state["pn", n][:].rearrange("p j (h c) -> p (j h) c", h=NH),
             )
 
+        def copy_rope(n):
+            if n < PAIRS - ROPED_ON_VECTOR:
+                to_rope = work.tile([P, 6 * DR], F32, name="to_rope", bufs=3)
+                nc.scalar.copy(out=to_rope[:], in_=state["pr", n][:, 64:448])
+                state["to_rope", n] = to_rope
+
         def square_kv(n):
-            mean = stat("mean", n + KV_LAG)
             for j in range(2):
                 squares = work.tile([P, KVR], BF16, name="squares_kv")
                 nc.scalar.activation(
@@ -386,34 +332,25 @@ def tile_mla_model_t_kernel(
                     state["pr", n][:, 448 * j : 448 * j + KVR],
                     ACT.Square,
                     scale=KVR**-0.5,
-                    accum_out=mean[:, 2 + j : 3 + j],
+                    accum_out=stat("mean", n + 2)[:, 2 + j : 3 + j],
                 )
 
-        def gain_kv(n):
-            gained = work.tile([P, 2, KVR], F32, name="gained", bufs=5)
-            nc.vector.tensor_tensor(
-                out=gained[:],
-                in0=state["pr", n][:].rearrange("p (b c) -> p b c", c=KVR)[:, 0:8:7, :],
-                in1=gkv[:].unsqueeze(1).to_broadcast([P, 2, KVR]),
-                op=MULT,
-            )
-            state["gained", n] = gained
-
-        def scale_ckv(n):
+        def norm_kv(n):
             for j in range(2):
-                nc.scalar.activation(
-                    out_tile(n)[:, 960 * j : 960 * j + KVR],
-                    state["gained", n][:, j, :],
-                    ACT.Copy,
-                    scale=stat("rinv", n + KV_LAG)[:, 2 + j : 3 + j],
+                nc.vector.scalar_tensor_tensor(
+                    out=out_tile(n)[:, 960 * j : 960 * j + KVR],
+                    in0=state["pr", n][:, 448 * j : 448 * j + KVR],
+                    scalar=stat("rinv", n + 2)[:, 2 + j : 3 + j],
+                    in1=gkv[:],
+                    op0=MULT,
+                    op1=MULT,
                 )
 
-        def rope_products(n):
-            products = work.tile([P, 6, 2, 2, HALF], F32, name="products", bufs=4)
-            nc.vector.tensor_tensor(
+        def rope_products(n, engine, source):
+            products = shared(n + 1, [P, 6, 2, 2, HALF], F32)
+            engine.tensor_tensor(
                 out=products[:].rearrange("p (j s) h w d -> p j s h w d", j=2),
-                in0=state["pr", n][:, 64:448]
-                .rearrange("p (j s h d) -> p j s h d", j=2, s=3, h=2)
+                in0=source.rearrange("p (j s h d) -> p j s h d", j=2, s=3, h=2)
                 .unsqueeze(4)
                 .to_broadcast([P, 2, 3, 2, 2, HALF]),
                 in1=factors[:, 2 * n : 2 * n + 2].unsqueeze(2).to_broadcast([P, 2, 3, 2, 2, HALF]),
@@ -430,6 +367,14 @@ def tile_mla_model_t_kernel(
                 op=ADD,
             )
 
+        def rope(n):
+            if n < PAIRS - ROPED_ON_VECTOR:
+                rope_products(n, nc.gpsimd, state["to_rope", n][:])
+                rope_add(n, nc.gpsimd)
+            else:
+                rope_products(n, nc.vector, state["pr", n][:, 64:448])
+                rope_add(n, nc.vector)
+
         def store(n):
             ot = out_tile(n)
             nc.sync.dma_start(
@@ -440,53 +385,61 @@ def tile_mla_model_t_kernel(
                 in_=ot[:].rearrange("p (b c) -> p b c", c=192)[:, 0:6:5, 0:128],
             )
 
-        OPS = dict(
-            mult=(-1, mult_x),
-            gate=(-1, gate),
-            turn0=(0, lambda n: turn_x(n, 0)),
-            turn1=(0, lambda n: turn_x(n, 1)),
-            empty0=(0, lambda n: empty_x(n, 0)),
-            empty1=(0, lambda n: empty_x(n, 1)),
-            quant_x=(1, quant_x),
-            a0=(NORM_LAG, lambda n: mm_a(n, 0)),
-            a1=(NORM_LAG, lambda n: mm_a(n, 1)),
-            square0=(NORM_LAG, lambda n: square_a(n, 0)),
-            square1=(NORM_LAG, lambda n: square_a(n, 1)),
-            norm0=(NORM_LAG, lambda n: norm_a(n, 0)),
-            norm1=(NORM_LAG, lambda n: norm_a(n, 1)),
-            turn_c0=(NORM_LAG, lambda n: turn_c(n, 0)),
-            turn_c1=(NORM_LAG, lambda n: turn_c(n, 1)),
-            empty_c=(NORM_LAG, empty_c),
-            quant_c=(3, quant_c),
-            kv_rope=(3, mm_kv_rope),
-            nope=(3, mm_nope),
-            copy=(3, copy_nope),
-            rope=(4, rope_products),
-            gain=(4, gain_kv),
-            square_kv=(4, square_kv),
-            add=(5, lambda n: rope_add(n, nc.gpsimd)),
-            add_vector=(5, lambda n: rope_add(n, nc.vector)),
-            ckv=(KV_LAG, scale_ckv),
-            store=(5, store),
-            rms=(0, lambda s: inverse_rms(s, 0, 4)),
-            rms_a=(0, lambda n: inverse_rms(n + NORM_LAG, 0, 2)),
-            rms_kv=(0, lambda n: inverse_rms(n + KV_LAG, 2, 4)),
-            wa_scalar=(0, lambda part: wa_copy(nc.scalar.copy, part)),
-            wa_vector=(0, lambda part: wa_copy(nc.vector.tensor_copy, part)),
-            wa_quant=(0, wa_quant),
-            gamma=(0, gamma_copy),
-            wb_copy=(0, wb_copy),
-            wb_quant=(0, wb_quant),
-            table=(0, rope_table),
-            dummies=(0, dummies),
+        def rms_tile0(n):
+            inverse_rms(n, 1 if n < PAIRS else 2, 4 if n >= 2 else 2)
+
+        on_vector = {
+            -1: (lambda: wa_copy(0), lambda: wa_copy(1), lambda: wa_copy(2), lambda: wa_quant(0)),
+            0: (lambda: wa_copy(3),),
+            1: (lambda: wa_quant(1),),
+            2: (wkv_quant,),
+            3: (wb_quant,),
+        }
+        on_scalar = {
+            0: (wkv_copy, gamma_copy),
+            1: (wb_copy,),
+            2: (lambda: rope_table(sin),),
+            3: (lambda: rope_table(cos),),
+        }
+
+        def prepare(parts):
+            return lambda s: [part() for part in parts.get(s, ())]
+
+        step = (
+            (prepare(on_vector), None),
+            (empty_c, 3),
+            (rms_tile0, 2),
+            (quant_x, 1),
+            (quant_c, 3),
+            (rope, 4),
+            (lambda n: turn_x(n, 1), 0),
+            (lambda n: square_a(n, 1), 2),
+            (lambda n: widen(n, 0), -2),
+            (lambda n: inverse_rms(n, 0, 1), 2),
+            (lambda n: widen(n, 1), -2),
+            (mm_kv_rope, 3),
+            (mm_nope, 3),
+            (lambda n: norm_a(n, 0), 2),
+            (lambda n: scale_x(n, 0), 0),
+            (prepare(on_scalar), None),
+            (copy_rope, 3),
+            (square_kv, 3),
+            (copy_nope, 3),
+            (lambda n: mm_a(n, 0), 1),
+            (lambda n: turn_c(n, 0), 2),
+            (lambda n: turn_x(n, 0), -1),
+            (lambda n: square_a(n, 0), 1),
+            (lambda n: norm_a(n, 1), 2),
+            (lambda n: scale_x(n, 1), 0),
+            (norm_kv, 4),
+            (store, 4),
+            (lambda n: turn_c(n, 1), 2),
+            (lambda n: mm_a(n, 1), 1),
         )
-        for word in FIRST.split():
-            stage, number = word.split(":")
-            OPS[stage][1](int(number))
-        for s in range(FIRST_STEP, PAIRS - 1):
-            for stage in STEP.split():
-                lag, run = OPS[stage]
-                run(s - lag)
-        for word in LAST.split():
-            stage, number = word.split(":")
-            OPS[stage][1](PAIRS + int(number))
+        for s in range(-2, PAIRS + 4):
+            for stage, lag in step:
+                last = PAIRS + 2 if stage is rms_tile0 else PAIRS
+                if lag is None:
+                    stage(s)
+                elif 0 <= s - lag < last:
+                    stage(s - lag)

@@ -14,7 +14,7 @@ FLOPS = 2 * T * (H * (QR + KVR + DR) + QR * NH * (DN + DR))
 P = 128
 N_TILES = T // P
 PAIRS = N_TILES // 2
-ROPED_ON_VECTOR = 2
+ROPED_ON_VECTOR = 3
 
 F32 = mybir.dt.float32
 BF16 = mybir.dt.bfloat16
@@ -61,13 +61,12 @@ def tile_mla_model_t_kernel(
         one = keep.tile([P, 1], F32, name="one")
         eps = keep.tile([P, 1], F32, name="eps")
 
-        wa_g = keep.tile([P, 2 * QR * 4], BF16, name="wa_g", align_bytes=64)
+        wa_g = keep.tile([P, 2 * QR * 4], BF16, name="grouped", align_bytes=64)
         wa_c = keep.tile([P, 2, QR], U32, name="wa_c", align_bytes=64)
         wa_s = keep.tile([P, 2, QR], U8, name="wa_s", align_bytes=64)
-        wkv_g = keep.tile([P, 4 * 128 * 4], BF16, name="wkv_g", align_bytes=64)
-        wkv_c = keep.tile([P, 2, 2, 128], U32, name="wkv_c", align_bytes=64)
-        wkv_s = keep.tile([P, 2, 2, 128], U8, name="wkv_s", align_bytes=64)
-        wb_g = keep.tile([P, 384 * 4], BF16, name="wb_g", align_bytes=64)
+        wkv_g = keep.tile([P, 2 * 128 * 4], BF16, name="wkv_g", align_bytes=64)
+        wkv_c = keep.tile([P, 2, 128], U32, name="wkv_c", align_bytes=64)
+        wkv_s = keep.tile([P, 2, 128], U8, name="wkv_s", align_bytes=64)
         wb_c = keep.tile([P, 384], U32, name="wb_c", align_bytes=64)
         wb_s = keep.tile([P, 384], U8, name="wb_s", align_bytes=64)
 
@@ -91,11 +90,11 @@ def tile_mla_model_t_kernel(
         load_x(2, 4)
         nc.sync.dma_start(out=wkv_raw[:], in_=wkv.rearrange("(g p j) c -> p g j c", p=P, j=4))
         load_x(4, 6)
-        nc.sync.dma_start(out=gq_raw[:], in_=gamma_cq.partition_broadcast(P))
         nc.sync.dma_start(out=wb_raw[:], in_=wq_b.rearrange("(p j) c -> p j c", j=4))
+        nc.sync.dma_start(out=cos[:], in_=cos_hbm)
+        nc.sync.dma_start(out=gq_raw[:], in_=gamma_cq.partition_broadcast(P))
         load_x(6, 8)
         nc.sync.dma_start(out=sin[:], in_=sin_hbm)
-        nc.sync.dma_start(out=cos[:], in_=cos_hbm)
         nc.sync.dma_start(out=gkv[:], in_=gamma_ckv.partition_broadcast(P))
         for i0 in range(8, N_TILES, 4):
             load_x(i0, i0 + 4)
@@ -107,13 +106,25 @@ def tile_mla_model_t_kernel(
         state = {}
 
 
-        def wa_copy(part):
+        def gpsimd_copy(out, in_):
+            nc.gpsimd.tensor_scalar(out=out, in0=in_, scalar1=1.0, scalar2=0.0, op0=MULT, op1=ADD)
+
+        def wa_views(part):
             g, half = divmod(part, 2)
             grouped = wa_g[:].rearrange("p (g u m e j) -> p g u m e j", g=2, u=2, e=2, j=4)
-            nc.vector.tensor_copy(
-                out=grouped[:, g, :, 64 * half : 64 * (half + 1)],
-                in_=wa_raw[part][:].rearrange("p j (m u e) -> p u m e j", u=2, e=2),
+            return (
+                grouped[:, g, :, 64 * half : 64 * (half + 1)],
+                wa_raw[part][:].rearrange("p j (m u e) -> p u m e j", u=2, e=2),
             )
+
+        def wa_copy(part, copy):
+            dst, src = wa_views(part)
+            copy(out=dst, in_=src)
+
+        def wa_copy_gpsimd(part):
+            dst, src = wa_views(part)
+            for u in range(2):
+                gpsimd_copy(dst[:, u], src[:, u])
 
         def wa_quant(g):
             nc.vector.quantize_mx(
@@ -127,40 +138,44 @@ def tile_mla_model_t_kernel(
             )
 
         def wkv_copy():
-            kv_dst = wkv_g[:].rearrange("p (v g c j) -> p v g c j", v=2, g=2, j=4)
-            kv_src = wkv_raw[:].rearrange("p g j c -> p g c j")
-            nc.scalar.copy(out=kv_dst[:, 0], in_=kv_src)
-            nc.scalar.copy(out=kv_dst[:, 1, :, 0:64], in_=kv_src[:, :, 64:128])
-            nc.scalar.copy(out=kv_dst[:, 1, :, 64:128], in_=kv_src[:, :, 0:64])
+            nc.scalar.copy(
+                out=wkv_g[:].rearrange("p (g c j) -> p g c j", g=2, j=4), in_=wkv_raw[:].rearrange("p g j c -> p g c j")
+            )
 
         def wb_copy():
+            wb_g = keep.tile([P, 384 * 4], BF16, name="grouped", align_bytes=64)
             wb_dst = wb_g[:].rearrange("p (c j) -> p c j", j=4)
             wb_src = wb_raw[:].rearrange("p j (h c) -> p h c j", h=NH)
-            nc.scalar.copy(out=wb_dst[:, 0:256].rearrange("p (h c) j -> p h c j", h=NH), in_=wb_src[:, :, 0:DN])
+            gpsimd_copy(wb_dst[:, 0:256].rearrange("p (h c) j -> p h c j", h=NH), wb_src[:, :, 0:DN])
             nc.scalar.copy(out=wb_dst[:, 256:384].rearrange("p (h c) j -> p h c j", h=NH), in_=wb_src[:, :, DN:])
+            state["wb_g"] = wb_g
 
         def wkv_quant():
             nc.vector.quantize_mx(
-                out=wkv_c[:].rearrange("p v g c -> p (v g c)").bitcast(FP8X4),
-                scales=wkv_s[:].rearrange("p v g c -> p (v g c)"),
+                out=wkv_c[:].rearrange("p g c -> p (g c)").bitcast(FP8X4),
+                scales=wkv_s[:].rearrange("p g c -> p (g c)"),
                 in_=wkv_g[:],
             )
 
         def wb_quant():
-            nc.vector.quantize_mx(out=wb_c[:].bitcast(FP8X4), scales=wb_s[:], in_=wb_g[:])
+            nc.vector.quantize_mx(out=wb_c[:].bitcast(FP8X4), scales=wb_s[:], in_=state["wb_g"][:])
 
-        def rope_table(source):
-            if source is sin:
-                nc.scalar.copy(out=factors[:, :, 0, 1, :], in_=sin[:, :, HALF:])
-                nc.scalar.activation(factors[:, :, 1, 0, :], sin[:, :, 0:HALF], ACT.Copy, scale=-1.0)
-            else:
-                nc.scalar.copy(out=factors[:, :, 0, 0, :], in_=cos[:, :, 0:HALF])
-                nc.scalar.copy(out=factors[:, :, 1, 1, :], in_=cos[:, :, HALF:])
+        def table_cos():
+            nc.scalar.copy(
+                out=factors[:].rearrange("p i h w d -> p i (h w) d")[:, :, 0:4:3, :],
+                in_=cos[:].rearrange("p i (h d) -> p i h d", h=2),
+            )
+
+        def table_sin():
+            nc.scalar.copy(out=factors[:, :, 0, 1, :], in_=sin[:, :, HALF:])
+
+        def table_minus_sin():
+            nc.scalar.activation(factors[:, :, 1, 0, :], sin[:, :, 0:HALF], ACT.Copy, scale=-1.0)
 
 
         def widen(n, j):
             i = 2 * n + j
-            xw = work.tile([P, H], BF16, name="xw", bufs=6)
+            xw = work.tile([P, H], BF16, name="xw", bufs=4)
             nc.scalar.copy(out=xw[:], in_=x_raw[:, i * H : (i + 1) * H].bitcast(FP8))
             state["xw", n, j] = xw
 
@@ -192,9 +207,13 @@ def tile_mla_model_t_kernel(
             state["xc", n] = (xc, xsc)
 
 
-        def mm_a(n, j):
+        def spare_bank(shape):
+            return ps_x.tile(shape, F32, name="xt")
+
+        def mm_a(n, j, pa=None):
             xc, xsc = state["xc", n]
-            pa = ps_a.tile([P, QR], F32, name="pa")
+            if pa is None:
+                pa = ps_a.tile([P, QR], F32, name="pa")
             for g in range(2):
                 cols = slice((2 * j + g) * P, (2 * j + g + 1) * P)
                 nc.tensor.matmul_mx(
@@ -216,7 +235,7 @@ def tile_mla_model_t_kernel(
         def square_a(n, j):
             squares = work.tile([P, QR], BF16, name="squares_a")
             nc.scalar.activation(
-                squares[:], state["pa", n, j][:], ACT.Square, scale=QR**-0.5, accum_out=stat("mean", n)[:, 1 - j : 2 - j]
+                squares[:], state["pa", n, j][:], ACT.Square, scale=QR**-0.5, accum_out=stat("mean", n)[:, j : j + 1]
             )
 
         def inverse_rms(n, c0, c1):
@@ -229,107 +248,110 @@ def tile_mla_model_t_kernel(
             nc.vector.scalar_tensor_tensor(
                 out=cq[:],
                 in0=state["pa", n, j][:],
-                scalar=stat("rinv", n)[:, 1 - j : 2 - j],
+                scalar=stat("rinv", n)[:, j : j + 1],
                 in1=gq[:],
                 op0=MULT,
                 op1=MULT,
             )
             state["cq", n, j] = cq
 
-        def turn_c(n, j):
+        def turn_c(n, j, own_bank=None):
             if j == 0:
                 state["ct", n] = ps_c.tile([P, 2, 2, P], F32, name="ct")
+            ct = state["ct", n] if own_bank is None else own_bank
             words = state["cq", n, j][:].bitcast(F32)
             for u in range(2):
-                nc.tensor.transpose(state["ct", n][:, j, u, :], words[:, u * P : (u + 1) * P], ident[:])
+                nc.tensor.transpose(ct[:, j, u, :], words[:, u * P : (u + 1) * P], ident[:])
+            state["ct", n, j] = ct
 
         def shared(n, shape, dtype):
             return work.tile(shape, dtype, name="shared%d" % (n % 2), bufs=1, align_bytes=64)
 
-        def empty_c(n):
-            cg = shared(n, [P, 1024], BF16)
-            nc.scalar.copy(
-                out=cg[:].bitcast(F32).rearrange("p (j n u) -> p j n u", j=2, u=2),
-                in_=state["ct", n][:].rearrange("p j u n -> p j n u"),
+        def empty_c(n, j0=0, j1=2, copy=nc.scalar.copy):
+            if j0 == 0:
+                state["cg", n] = shared(n, [P, 1024], BF16)
+            copy(
+                out=state["cg", n][:].bitcast(F32).rearrange("p (j n u) -> p j n u", j=2, u=2)[:, j0:j1],
+                in_=state["ct", n, j0][:, j0:j1].rearrange("p j u n -> p j n u"),
             )
-            state["cg", n] = cg
 
-        def quant_c(n):
-            cc = work.tile([P, 256], U32, name="cc", bufs=2, align_bytes=64)
-            cs = work.tile([P, 256], U8, name="cs", bufs=2, align_bytes=64)
-            nc.vector.quantize_mx(out=cc[:].bitcast(FP8X4), scales=cs[:], in_=state["cg", n][:])
-            state["cc", n] = (cc, cs)
-
-
-        def mm_kv_rope(n):
+        def quant_c(n, j0=0, j1=2):
+            if j0 == 0:
+                cc = work.tile([P, 256], U32, name="cc", bufs=2, align_bytes=64)
+                cs = work.tile([P, 256], U8, name="cs", bufs=2, align_bytes=64)
+                state["cc", n] = (cc, cs)
             cc, cs = state["cc", n]
+            cols = slice(j0 * P, j1 * P)
+            nc.vector.quantize_mx(
+                out=cc[:, cols].bitcast(FP8X4), scales=cs[:, cols], in_=state["cg", n][:, j0 * QR : j1 * QR]
+            )
+
+
+        def mm_kv(n, tiles=(0, 1), pr=None):
             xc, xsc = state["xc", n]
-            pr = ps_r.tile([P, OUT_W], F32, name="pr")
-            for j in range(2):
+            if pr is None:
+                pr = ps_r.tile([P, 2, 256], F32, name="pr")
+            for j in tiles:
+                state["pr", n, j] = pr
                 for g in range(2):
                     xcols = slice((2 * j + g) * P, (2 * j + g + 1) * P)
                     nc.tensor.matmul_mx(
-                        out=pr[:, 384 * j : 384 * j + 128],
+                        out=pr[:, j, 0:128],
                         lhsT=xc[:, xcols].bitcast(FP8X4),
                         lhsT_scale=xsc[:, xcols],
-                        rhs=wkv_c[:, j, g, :].bitcast(FP8X4),
-                        rhs_scale=wkv_s[:, j, g, :],
+                        rhs=wkv_c[:, g, :].bitcast(FP8X4),
+                        rhs_scale=wkv_s[:, g, :],
                         start=(g == 0),
                         stop=(g == 1),
                     )
-            for j in range(2):
-                cols = slice(j * P, (j + 1) * P)
-                nc.tensor.matmul_mx(
-                    out=pr[:, 128 + 128 * j : 256 + 128 * j],
-                    lhsT=cc[:, cols].bitcast(FP8X4),
-                    lhsT_scale=cs[:, cols],
-                    rhs=wb_c[:, 256:384].bitcast(FP8X4),
-                    rhs_scale=wb_s[:, 256:384],
-                    start=True,
-                    stop=True,
-                )
-            state["pr", n] = pr
 
-        def mm_nope(n):
+        def mm_q(n, j, dst, c0, c1):
             cc, cs = state["cc", n]
-            pn = ps_n.tile([P, 2, 256], F32, name="pn")
-            for j in range(2):
-                cols = slice(j * P, (j + 1) * P)
-                nc.tensor.matmul_mx(
-                    out=pn[:, j, :],
-                    lhsT=cc[:, cols].bitcast(FP8X4),
-                    lhsT_scale=cs[:, cols],
-                    rhs=wb_c[:, 0:256].bitcast(FP8X4),
-                    rhs_scale=wb_s[:, 0:256],
-                    start=True,
-                    stop=True,
-                )
-            state["pn", n] = pn
+            cols = slice(j * P, (j + 1) * P)
+            nc.tensor.matmul_mx(
+                out=dst,
+                lhsT=cc[:, cols].bitcast(FP8X4),
+                lhsT_scale=cs[:, cols],
+                rhs=wb_c[:, c0:c1].bitcast(FP8X4),
+                rhs_scale=wb_s[:, c0:c1],
+                start=True,
+                stop=True,
+            )
+
+        def mm_rope(n, tiles=(0, 1)):
+            for j in tiles:
+                mm_q(n, j, state["pr", n, j][:, j, 128:256], 256, 384)
+
+        def mm_nope(n, tiles=(0, 1), pn=None):
+            if pn is None:
+                pn = ps_n.tile([P, 2, 256], F32, name="pn")
+            for j in tiles:
+                mm_q(n, j, pn[:, j, :], 0, 256)
+                state["pn", n, j] = pn
 
 
         def out_tile(n):
             if ("ot", n) not in state:
-                state["ot", n] = work.tile([P, 1152], F32, name="ot", bufs=4)
+                state["ot", n] = work.tile([P, 2, 576], F32, name="ot", bufs=4)
             return state["ot", n]
 
-        def copy_nope(n):
-            nc.scalar.copy(
-                out=out_tile(n)[:, 128:896].rearrange("p (h c) -> p h c", c=DN + DR)[:, :, 0:DN],
-                in_=state["pn", n][:].rearrange("p j (h c) -> p (j h) c", h=NH),
+        def copy_nope(n, j0=0, j1=2, copy=nc.scalar.copy):
+            copy(
+                out=out_tile(n)[:, j0:j1, 128:512].rearrange("p j (h c) -> p j h c", h=NH)[:, :, :, 0:DN],
+                in_=state["pn", n, j0][:, j0:j1].rearrange("p j (h c) -> p j h c", h=NH),
             )
 
         def copy_rope(n):
-            if n < PAIRS - ROPED_ON_VECTOR:
-                to_rope = work.tile([P, 6 * DR], F32, name="to_rope", bufs=3)
-                nc.scalar.copy(out=to_rope[:], in_=state["pr", n][:, 64:448])
-                state["to_rope", n] = to_rope
+            to_rope = work.tile([P, 2, 3 * DR], F32, name="to_rope", bufs=3)
+            nc.scalar.copy(out=to_rope[:], in_=state["pr", n, 0][:, :, 64:256])
+            state["to_rope", n] = to_rope
 
         def square_kv(n):
             for j in range(2):
                 squares = work.tile([P, KVR], BF16, name="squares_kv")
                 nc.scalar.activation(
                     squares[:],
-                    state["pr", n][:, 448 * j : 448 * j + KVR],
+                    state["pr", n, j][:, j, 0:KVR],
                     ACT.Square,
                     scale=KVR**-0.5,
                     accum_out=stat("mean", n + 2)[:, 2 + j : 3 + j],
@@ -338,108 +360,201 @@ def tile_mla_model_t_kernel(
         def norm_kv(n):
             for j in range(2):
                 nc.vector.scalar_tensor_tensor(
-                    out=out_tile(n)[:, 960 * j : 960 * j + KVR],
-                    in0=state["pr", n][:, 448 * j : 448 * j + KVR],
+                    out=out_tile(n)[:, j, 0:KVR],
+                    in0=state["pr", n, j][:, j, 0:KVR],
                     scalar=stat("rinv", n + 2)[:, 2 + j : 3 + j],
                     in1=gkv[:],
                     op0=MULT,
                     op1=MULT,
                 )
 
-        def rope_products(n, engine, source):
-            products = shared(n + 1, [P, 6, 2, 2, HALF], F32)
+        def rope_products(n, engine, source, j0, j1):
+            shape = [P, j1 - j0, 3, 2, 2, HALF]
             engine.tensor_tensor(
-                out=products[:].rearrange("p (j s) h w d -> p j s h w d", j=2),
-                in0=source.rearrange("p (j s h d) -> p j s h d", j=2, s=3, h=2)
-                .unsqueeze(4)
-                .to_broadcast([P, 2, 3, 2, 2, HALF]),
-                in1=factors[:, 2 * n : 2 * n + 2].unsqueeze(2).to_broadcast([P, 2, 3, 2, 2, HALF]),
+                out=state["products", n][:, 3 * j0 : 3 * j1].rearrange("p (j s) h w d -> p j s h w d", s=3),
+                in0=source[:, j0:j1].rearrange("p j (s h d) -> p j s h d", s=3, h=2).unsqueeze(4).to_broadcast(shape),
+                in1=factors[:, 2 * n + j0 : 2 * n + j1].unsqueeze(2).to_broadcast(shape),
                 op=MULT,
             )
-            state["products", n] = products
 
-        def rope_add(n, engine):
-            products = state["products", n][:].rearrange("p s h w d -> p s h (w d)")
+        def rope_add(n, engine, j0=0, j1=2):
+            halves = state["products", n][:, 3 * j0 : 3 * j1].rearrange("p s h w d -> p s h (w d)")
             engine.tensor_tensor(
-                out=out_tile(n)[:].rearrange("p (s c) -> p s c", c=DN + DR)[:, :, 64:128],
-                in0=products[:, :, 0, :],
-                in1=products[:, :, 1, :],
+                out=out_tile(n)[:, j0:j1].rearrange("p j (s c) -> p (j s) c", c=DN + DR)[:, :, 64:128],
+                in0=halves[:, :, 0, :],
+                in1=halves[:, :, 1, :],
                 op=ADD,
             )
 
         def rope(n):
-            if n < PAIRS - ROPED_ON_VECTOR:
-                rope_products(n, nc.gpsimd, state["to_rope", n][:])
-                rope_add(n, nc.gpsimd)
-            else:
-                rope_products(n, nc.vector, state["pr", n][:, 64:448])
-                rope_add(n, nc.vector)
+            state["products", n] = shared(n + 1, [P, 6, 2, 2, HALF], F32)
+            rope_products(n, nc.gpsimd, state["to_rope", n][:], 0, 2)
+            rope_add(n, nc.gpsimd)
 
-        def store(n):
+        def products_from_psum(n, j):
+            if j == 0:
+                state["products", n] = work.tile([P, 6, 2, 2, HALF], F32, name="products", bufs=ROPED_ON_VECTOR)
+            rope_products(n, nc.vector, state["pr", n, j][:, :, 64:256], j, j + 1)
+
+        def store(n, j0=0, j1=2):
             ot = out_tile(n)
-            nc.sync.dma_start(
-                out=out_hbm[:, 2 * n : 2 * n + 2, 0:384], in_=ot[:, 128:896].rearrange("p (j c) -> p j c", j=2)
-            )
-            nc.sync.dma_start(
-                out=out_hbm[:, 2 * n : 2 * n + 2, 384:512],
-                in_=ot[:].rearrange("p (b c) -> p b c", c=192)[:, 0:6:5, 0:128],
-            )
+            tiles = slice(2 * n + j0, 2 * n + j1)
+            nc.sync.dma_start(out=out_hbm[:, tiles, 0:384], in_=ot[:, j0:j1, 128:512])
+            nc.sync.dma_start(out=out_hbm[:, tiles, 384:512], in_=ot[:, j0:j1, 0:128])
 
-        def rms_tile0(n):
+        def rms_tile1(n):
             inverse_rms(n, 1 if n < PAIRS else 2, 4 if n >= 2 else 2)
 
-        on_vector = {
-            -1: (lambda: wa_copy(0), lambda: wa_copy(1), lambda: wa_copy(2), lambda: wa_quant(0)),
-            0: (lambda: wa_copy(3),),
-            1: (lambda: wa_quant(1),),
-            2: (wkv_quant,),
-            3: (wb_quant,),
-        }
-        on_scalar = {
-            0: (wkv_copy, gamma_copy),
-            1: (wb_copy,),
-            2: (lambda: rope_table(sin),),
-            3: (lambda: rope_table(cos),),
-        }
-
-        def prepare(parts):
-            return lambda s: [part() for part in parts.get(s, ())]
-
         step = (
-            (prepare(on_vector), None),
-            (empty_c, 3),
-            (rms_tile0, 2),
             (quant_x, 1),
             (quant_c, 3),
             (rope, 4),
             (lambda n: turn_x(n, 1), 0),
-            (lambda n: square_a(n, 1), 2),
-            (lambda n: widen(n, 0), -2),
-            (lambda n: inverse_rms(n, 0, 1), 2),
-            (lambda n: widen(n, 1), -2),
-            (mm_kv_rope, 3),
+            (lambda n: widen(n, 0), -1),
+            (rms_tile1, 2),
+            (lambda n: widen(n, 1), -1),
+            (mm_kv, 3),
+            (lambda n: mm_a(n, 0), 1),
+            (mm_rope, 3),
             (mm_nope, 3),
-            (lambda n: norm_a(n, 0), 2),
             (lambda n: scale_x(n, 0), 0),
-            (prepare(on_scalar), None),
+            (lambda n: norm_a(n, 1), 2),
+            (lambda n: square_a(n, 0), 1),
             (copy_rope, 3),
+            (lambda n: inverse_rms(n, 0, 1), 1),
             (square_kv, 3),
             (copy_nope, 3),
-            (lambda n: mm_a(n, 0), 1),
             (lambda n: turn_c(n, 0), 2),
             (lambda n: turn_x(n, 0), -1),
-            (lambda n: square_a(n, 0), 1),
-            (lambda n: norm_a(n, 1), 2),
-            (lambda n: scale_x(n, 1), 0),
-            (norm_kv, 4),
-            (store, 4),
             (lambda n: turn_c(n, 1), 2),
             (lambda n: mm_a(n, 1), 1),
+            (lambda n: scale_x(n, 1), 0),
+            (lambda n: norm_a(n, 0), 1),
+            (norm_kv, 4),
+            (store, 4),
+            (empty_c, 2),
+            (lambda n: square_a(n, 1), 1),
         )
-        for s in range(-2, PAIRS + 4):
+
+        wa_copy(0, nc.vector.tensor_copy)
+        widen(0, 0)
+        turn_x(0, 0)
+        wa_copy(1, nc.vector.tensor_copy)
+        widen(0, 1)
+        turn_x(0, 1)
+        wa_quant(0)
+        wa_copy(2, nc.scalar.copy)
+        wa_copy_gpsimd(3)
+        scale_x(0, 0)
+        widen(1, 0)
+        turn_x(1, 0)
+        scale_x(0, 1)
+        widen(1, 1)
+        turn_x(1, 1)
+        wa_quant(1)
+        quant_x(0)
+        wkv_copy()
+        widen(2, 0)
+        widen(2, 1)
+        wb_copy()
+        mm_a(0, 0)
+        scale_x(1, 0)
+        turn_x(2, 0)
+        mm_a(0, 1)
+        scale_x(1, 1)
+        turn_x(2, 1)
+        wkv_quant()
+        quant_x(1)
+        square_a(0, 0)
+        gamma_copy()
+        inverse_rms(0, 0, 1)
+        table_cos()
+        square_a(0, 1)
+        widen(3, 0)
+        rms_tile1(0)
+        widen(3, 1)
+        norm_a(0, 0)
+        mm_a(1, 0)
+        scale_x(2, 0)
+        norm_a(0, 1)
+        square_a(1, 0)
+        table_sin()
+        inverse_rms(1, 0, 1)
+        table_minus_sin()
+        turn_c(0, 0)
+        turn_x(3, 0)
+        turn_c(0, 1)
+        mm_a(1, 1)
+        scale_x(2, 1)
+        norm_a(1, 0)
+        empty_c(0)
+        square_a(1, 1)
+        wb_quant()
+
+        for s in range(3, PAIRS):
             for stage, lag in step:
-                last = PAIRS + 2 if stage is rms_tile0 else PAIRS
-                if lag is None:
-                    stage(s)
-                elif 0 <= s - lag < last:
+                if 0 <= s - lag < PAIRS:
                     stage(s - lag)
+
+        a, b, c, d = range(PAIRS - 4, PAIRS)
+        quant_x(d)
+        quant_c(b)
+        rope(a)
+        rms_tile1(c)
+        mm_kv(b)
+        square_kv(b)
+        mm_a(d, 0)
+        mm_rope(b)
+        mm_a(d, 1, spare_bank([P, QR]))
+        inverse_rms(d, 2, 4)
+        norm_a(c, 1)
+        norm_kv(a)
+        store(a)
+        norm_kv(b)
+        square_a(d, 0)
+        turn_c(c, 0)
+        turn_c(c, 1)
+        mm_kv(c)
+        mm_kv(d, (0, 1), ps_a.tile([P, 2, 256], F32, name="pa"))
+        mm_nope(b)
+        products_from_psum(b, 0)
+        products_from_psum(b, 1)
+        inverse_rms(d, 0, 1)
+        square_a(d, 1)
+        square_kv(c)
+        inverse_rms(d, 1, 2)
+        empty_c(c)
+        norm_a(d, 0)
+        norm_a(d, 1)
+        quant_c(c)
+        square_kv(d)
+        copy_nope(b)
+        turn_c(d, 0)
+        turn_c(d, 1, spare_bank([P, 2, 2, P]))
+        mm_rope(c)
+        mm_nope(c, (0, 1), ps_a.tile([P, 2, 256], F32, name="pa"))
+        empty_c(d, 0, 1)
+        rms_tile1(d + 1)
+        rms_tile1(d + 2)
+        empty_c(d, 1, 2)
+        copy_nope(c)
+        rope_add(b, nc.vector)
+        store(b)
+        quant_c(d, 0, 1)
+        products_from_psum(c, 0)
+        quant_c(d, 1, 2)
+        norm_kv(d)
+        mm_rope(d)
+        mm_nope(d)
+        products_from_psum(c, 1)
+        norm_kv(c)
+        rope_add(c, nc.vector)
+        store(c)
+        products_from_psum(d, 0)
+        products_from_psum(d, 1)
+        copy_nope(d, 0, 1)
+        copy_nope(d, 1, 2)
+        rope_add(d, nc.vector, 0, 1)
+        store(d, 0, 1)
+        rope_add(d, nc.vector, 1, 2)
+        store(d, 1, 2)

@@ -48,7 +48,7 @@ def tile_mla_model_t_kernel(
 
         x_raw = keep.tile([P, N_TILES * H], U8, name="x_raw")
         scale = keep.tile([P, 2, 4], F32, name="scale")
-        wa_raw = [keep.tile([P, 4, QR // 2], BF16, name="wa_raw%d" % part) for part in range(4)]
+        wa_raw = [keep.tile([P, 4, QR], BF16, name="wa_raw%d" % g) for g in range(2)]
         wkv_raw = keep.tile([P, 2, 4, KVR + DR], BF16, name="wkv_raw")
         wb_raw = keep.tile([P, 4, NH * (DN + DR)], BF16, name="wb_raw")
         gq_raw = keep.tile([P, QR], BF16, name="gq_raw")
@@ -56,7 +56,6 @@ def tile_mla_model_t_kernel(
         gkv = keep.tile([P, KVR], BF16, name="gkv")
         cos = keep.tile([P, N_TILES, DR], BF16, name="cos")
         sin = keep.tile([P, N_TILES, DR], BF16, name="sin")
-        factors = keep.tile([P, N_TILES, 2, 2, HALF], BF16, name="factors")
         ident = keep.tile([P, P], F32, name="ident")
         one = keep.tile([P, 1], F32, name="one")
         eps = keep.tile([P, 1], F32, name="eps")
@@ -75,28 +74,25 @@ def tile_mla_model_t_kernel(
                 out=x_raw[:, i0 * H : i1 * H], in_=x_hbm[:, i0:i1, :].rearrange("p i k -> p (i k)")
             )
 
-        def load_wa(part):
-            g, half = divmod(part, 2)
-            rows = wq_a.rearrange("(g p j) c -> g p j c", p=P, j=4)[g]
-            nc.sync.dma_start(out=wa_raw[part][:], in_=rows[:, :, 256 * half : 256 * (half + 1)])
+        def load_wa(g):
+            nc.sync.dma_start(out=wa_raw[g][:], in_=wq_a.rearrange("(g p j) c -> g p j c", p=P, j=4)[g])
 
-        load_wa(0)
         load_x(0, 1)
         nc.sync.dma_start(out=scale[:], in_=x_scale.rearrange("o (g p t) -> p (o g) t", g=2, t=4))
-        load_wa(1)
         load_x(1, 2)
-        load_wa(2)
-        load_wa(3)
+        load_wa(0)
+        load_wa(1)
         load_x(2, 4)
         nc.sync.dma_start(out=wkv_raw[:], in_=wkv.rearrange("(g p j) c -> p g j c", p=P, j=4))
         load_x(4, 6)
         nc.sync.dma_start(out=wb_raw[:], in_=wq_b.rearrange("(p j) c -> p j c", j=4))
-        nc.sync.dma_start(out=cos[:], in_=cos_hbm)
         nc.sync.dma_start(out=gq_raw[:], in_=gamma_cq.partition_broadcast(P))
         load_x(6, 8)
+        nc.sync.dma_start(out=cos[:], in_=cos_hbm)
+        load_x(8, 12)
         nc.sync.dma_start(out=sin[:], in_=sin_hbm)
         nc.sync.dma_start(out=gkv[:], in_=gamma_ckv.partition_broadcast(P))
-        for i0 in range(8, N_TILES, 4):
+        for i0 in range(12, N_TILES, 4):
             load_x(i0, i0 + 4)
 
         make_identity(nc, ident[:])
@@ -106,15 +102,15 @@ def tile_mla_model_t_kernel(
         state = {}
 
 
-        def gpsimd_copy(out, in_):
-            nc.gpsimd.tensor_scalar(out=out, in0=in_, scalar1=1.0, scalar2=0.0, op0=MULT, op1=ADD)
+        def gpsimd_copy(out, in_, sign=1.0):
+            nc.gpsimd.tensor_scalar(out=out, in0=in_, scalar1=sign, scalar2=0.0, op0=MULT, op1=ADD)
 
         def wa_views(part):
             g, half = divmod(part, 2)
             grouped = wa_g[:].rearrange("p (g u m e j) -> p g u m e j", g=2, u=2, e=2, j=4)
             return (
                 grouped[:, g, :, 64 * half : 64 * (half + 1)],
-                wa_raw[part][:].rearrange("p j (m u e) -> p u m e j", u=2, e=2),
+                wa_raw[g][:, :, 256 * half : 256 * (half + 1)].rearrange("p j (m u e) -> p u m e j", u=2, e=2),
             )
 
         def wa_copy(part, copy):
@@ -160,17 +156,17 @@ def tile_mla_model_t_kernel(
         def wb_quant():
             nc.vector.quantize_mx(out=wb_c[:].bitcast(FP8X4), scales=wb_s[:], in_=state["wb_g"][:])
 
-        def table_cos():
-            nc.scalar.copy(
-                out=factors[:].rearrange("p i h w d -> p i (h w) d")[:, :, 0:4:3, :],
-                in_=cos[:].rearrange("p i (h d) -> p i h d", h=2),
+        def rope_table():
+            factors = keep.tile([P, N_TILES, 2, 2, HALF], BF16, name="factors", align_bytes=64)
+            gpsimd_copy(factors[:, :, 1, 0, :], sin[:, :, 0:HALF], -1.0)
+            gpsimd_copy(
+                factors[:].rearrange("p i h w d -> p i (h w) d")[:, :, 0:4:3, :],
+                cos[:].rearrange("p i (h d) -> p i h d", h=2),
             )
+            state["factors"] = factors
 
         def table_sin():
-            nc.scalar.copy(out=factors[:, :, 0, 1, :], in_=sin[:, :, HALF:])
-
-        def table_minus_sin():
-            nc.scalar.activation(factors[:, :, 1, 0, :], sin[:, :, 0:HALF], ACT.Copy, scale=-1.0)
+            nc.scalar.copy(out=state["factors"][:, :, 0, 1, :], in_=sin[:, :, HALF:])
 
 
         def widen(n, j):
@@ -189,7 +185,10 @@ def tile_mla_model_t_kernel(
 
         def scale_x(n, j):
             if j == 0:
-                state["xg", n] = work.tile([P, 2 * H], BF16, name="xg", bufs=2, align_bytes=64)
+                if n == 1:
+                    state["xg", n] = keep.tile([P, 2 * H], BF16, name="factors", align_bytes=64)
+                else:
+                    state["xg", n] = work.tile([P, 2 * H], BF16, name="xg", bufs=2, align_bytes=64)
             nc.vector.tensor_tensor(
                 out=state["xg", n][:, j * H : (j + 1) * H].rearrange("p (g n u e) -> p g n u e", g=2, u=2, e=2),
                 in0=state["xt", n, j][:]
@@ -373,7 +372,7 @@ def tile_mla_model_t_kernel(
             engine.tensor_tensor(
                 out=state["products", n][:, 3 * j0 : 3 * j1].rearrange("p (j s) h w d -> p j s h w d", s=3),
                 in0=source[:, j0:j1].rearrange("p j (s h d) -> p j s h d", s=3, h=2).unsqueeze(4).to_broadcast(shape),
-                in1=factors[:, 2 * n + j0 : 2 * n + j1].unsqueeze(2).to_broadcast(shape),
+                in1=state["factors"][:, 2 * n + j0 : 2 * n + j1].unsqueeze(2).to_broadcast(shape),
                 op=MULT,
             )
 
@@ -402,28 +401,43 @@ def tile_mla_model_t_kernel(
             nc.sync.dma_start(out=out_hbm[:, tiles, 0:384], in_=ot[:, j0:j1, 128:512])
             nc.sync.dma_start(out=out_hbm[:, tiles, 384:512], in_=ot[:, j0:j1, 0:128])
 
+        def store_plain(n):
+            for h in range(NH):
+                c0 = h * (DN + DR)
+                nc.sync.dma_start(
+                    out=out_hbm[:, 2 * n : 2 * n + 2, c0 : c0 + DN], in_=out_tile(n)[:, :, 128 + c0 : 128 + c0 + DN]
+                )
+
+        def store_roped(n):
+            for h in range(NH):
+                c0 = h * (DN + DR) + DN
+                nc.sync.dma_start(
+                    out=out_hbm[:, 2 * n : 2 * n + 2, c0 : c0 + DR], in_=out_tile(n)[:, :, 128 + c0 : 128 + c0 + DR]
+                )
+            nc.sync.dma_start(out=out_hbm[:, 2 * n : 2 * n + 2, 384:512], in_=out_tile(n)[:, :, 0:128])
+
         def rms_tile1(n):
             inverse_rms(n, 1 if n < PAIRS else 2, 4 if n >= 2 else 2)
 
         step = (
-            (quant_x, 1),
             (quant_c, 3),
+            (quant_x, 1),
             (rope, 4),
             (lambda n: turn_x(n, 1), 0),
-            (lambda n: widen(n, 0), -1),
+            (copy_nope, 4),
             (rms_tile1, 2),
-            (lambda n: widen(n, 1), -1),
+            (lambda n: widen(n, 0), -1),
             (mm_kv, 3),
-            (lambda n: mm_a(n, 0), 1),
             (mm_rope, 3),
+            (lambda n: mm_a(n, 0), 1),
             (mm_nope, 3),
+            (copy_rope, 3),
+            (lambda n: widen(n, 1), -1),
             (lambda n: scale_x(n, 0), 0),
             (lambda n: norm_a(n, 1), 2),
             (lambda n: square_a(n, 0), 1),
-            (copy_rope, 3),
-            (lambda n: inverse_rms(n, 0, 1), 1),
             (square_kv, 3),
-            (copy_nope, 3),
+            (lambda n: inverse_rms(n, 0, 1), 1),
             (lambda n: turn_c(n, 0), 2),
             (lambda n: turn_x(n, 0), -1),
             (lambda n: turn_c(n, 1), 2),
@@ -436,13 +450,12 @@ def tile_mla_model_t_kernel(
             (lambda n: square_a(n, 1), 1),
         )
 
-        wa_copy(0, nc.vector.tensor_copy)
         widen(0, 0)
         turn_x(0, 0)
-        wa_copy(1, nc.vector.tensor_copy)
         widen(0, 1)
         turn_x(0, 1)
-        wa_quant(0)
+        wa_copy(0, nc.vector.tensor_copy)
+        wa_copy(1, nc.scalar.copy)
         wa_copy(2, nc.scalar.copy)
         wa_copy_gpsimd(3)
         scale_x(0, 0)
@@ -451,8 +464,9 @@ def tile_mla_model_t_kernel(
         scale_x(0, 1)
         widen(1, 1)
         turn_x(1, 1)
-        wa_quant(1)
+        wa_quant(0)
         quant_x(0)
+        wa_quant(1)
         wkv_copy()
         widen(2, 0)
         widen(2, 1)
@@ -468,11 +482,11 @@ def tile_mla_model_t_kernel(
         square_a(0, 0)
         gamma_copy()
         inverse_rms(0, 0, 1)
-        table_cos()
-        square_a(0, 1)
         widen(3, 0)
-        rms_tile1(0)
+        square_a(0, 1)
         widen(3, 1)
+        rms_tile1(0)
+        rope_table()
         norm_a(0, 0)
         mm_a(1, 0)
         scale_x(2, 0)
@@ -480,14 +494,13 @@ def tile_mla_model_t_kernel(
         square_a(1, 0)
         table_sin()
         inverse_rms(1, 0, 1)
-        table_minus_sin()
         turn_c(0, 0)
         turn_x(3, 0)
         turn_c(0, 1)
         mm_a(1, 1)
         scale_x(2, 1)
-        norm_a(1, 0)
         empty_c(0)
+        norm_a(1, 0)
         square_a(1, 1)
         wb_quant()
 
@@ -506,15 +519,16 @@ def tile_mla_model_t_kernel(
         mm_a(d, 0)
         mm_rope(b)
         mm_a(d, 1, spare_bank([P, QR]))
+        copy_nope(a)
         inverse_rms(d, 2, 4)
         norm_a(c, 1)
         norm_kv(a)
         store(a)
         norm_kv(b)
         square_a(d, 0)
+        mm_kv(c)
         turn_c(c, 0)
         turn_c(c, 1)
-        mm_kv(c)
         mm_kv(d, (0, 1), ps_a.tile([P, 2, 256], F32, name="pa"))
         mm_nope(b)
         products_from_psum(b, 0)
@@ -528,29 +542,30 @@ def tile_mla_model_t_kernel(
         norm_a(d, 1)
         quant_c(c)
         square_kv(d)
-        copy_nope(b)
         turn_c(d, 0)
         turn_c(d, 1, spare_bank([P, 2, 2, P]))
+        rope_add(b, nc.vector)
         mm_rope(c)
         mm_nope(c, (0, 1), ps_a.tile([P, 2, 256], F32, name="pa"))
-        empty_c(d, 0, 1)
         rms_tile1(d + 1)
+        copy_nope(b)
+        store(b)
+        empty_c(d, 0, 1)
         rms_tile1(d + 2)
         empty_c(d, 1, 2)
         copy_nope(c)
-        rope_add(b, nc.vector)
-        store(b)
+        store_plain(c)
+        norm_kv(c)
         quant_c(d, 0, 1)
-        products_from_psum(c, 0)
-        quant_c(d, 1, 2)
         norm_kv(d)
+        quant_c(d, 1, 2)
         mm_rope(d)
         mm_nope(d)
+        products_from_psum(c, 0)
         products_from_psum(c, 1)
-        norm_kv(c)
-        rope_add(c, nc.vector)
-        store(c)
         products_from_psum(d, 0)
+        rope_add(c, nc.vector)
+        store_roped(c)
         products_from_psum(d, 1)
         copy_nope(d, 0, 1)
         copy_nope(d, 1, 2)

@@ -331,12 +331,23 @@ def tile_mla_model_t_kernel(
 
         def out_tile(n):
             if ("ot", n) not in state:
-                state["ot", n] = work.tile([P, 2, 576], F32, name="ot", bufs=4)
+                if n < PAIRS - ROPED_ON_VECTOR:
+                    state["ot", n] = work.tile([P, 2, 576], F32, name="ot", bufs=4)
+                else:
+                    state["ot", n] = work.tile([P, 2, OUT_W], F32, name="ot_last", bufs=ROPED_ON_VECTOR)
             return state["ot", n]
+
+        def out_q(n):
+            q0 = 128 if n < PAIRS - ROPED_ON_VECTOR else 0
+            return out_tile(n)[:, :, q0 : q0 + 384].rearrange("p j (h c) -> p j h c", h=NH)
+
+        def out_kv(n):
+            kv0 = 0 if n < PAIRS - ROPED_ON_VECTOR else 384
+            return out_tile(n)[:, :, kv0 : kv0 + 128]
 
         def copy_nope(n, j0=0, j1=2, copy=nc.scalar.copy):
             copy(
-                out=out_tile(n)[:, j0:j1, 128:512].rearrange("p j (h c) -> p j h c", h=NH)[:, :, :, 0:DN],
+                out=out_q(n)[:, j0:j1, :, 0:DN],
                 in_=state["pn", n, j0][:, j0:j1].rearrange("p j (h c) -> p j h c", h=NH),
             )
 
@@ -347,7 +358,7 @@ def tile_mla_model_t_kernel(
 
         def square_kv(n):
             for j in range(2):
-                squares = work.tile([P, KVR], BF16, name="squares_kv")
+                squares = work.tile([P, KVR], BF16, name="squares_kv", bufs=4)
                 nc.scalar.activation(
                     squares[:],
                     state["pr", n, j][:, j, 0:KVR],
@@ -359,7 +370,7 @@ def tile_mla_model_t_kernel(
         def norm_kv(n):
             for j in range(2):
                 nc.vector.scalar_tensor_tensor(
-                    out=out_tile(n)[:, j, 0:KVR],
+                    out=out_kv(n)[:, j, 0:KVR],
                     in0=state["pr", n, j][:, j, 0:KVR],
                     scalar=stat("rinv", n + 2)[:, 2 + j : 3 + j],
                     in1=gkv[:],
@@ -376,68 +387,61 @@ def tile_mla_model_t_kernel(
                 op=MULT,
             )
 
-        def rope_add(n, engine, j0=0, j1=2):
-            halves = state["products", n][:, 3 * j0 : 3 * j1].rearrange("p s h w d -> p s h (w d)")
-            engine.tensor_tensor(
-                out=out_tile(n)[:, j0:j1].rearrange("p j (s c) -> p (j s) c", c=DN + DR)[:, :, 64:128],
+        def rope(n):
+            state["products", n] = shared(n + 1, [P, 6, 2, 2, HALF], F32)
+            rope_products(n, nc.gpsimd, state["to_rope", n][:], 0, 2)
+            halves = state["products", n][:].rearrange("p s h w d -> p s h (w d)")
+            nc.gpsimd.tensor_tensor(
+                out=out_tile(n)[:].rearrange("p j (s c) -> p (j s) c", c=DN + DR)[:, :, 64:128],
                 in0=halves[:, :, 0, :],
                 in1=halves[:, :, 1, :],
                 op=ADD,
             )
-
-        def rope(n):
-            state["products", n] = shared(n + 1, [P, 6, 2, 2, HALF], F32)
-            rope_products(n, nc.gpsimd, state["to_rope", n][:], 0, 2)
-            rope_add(n, nc.gpsimd)
 
         def products_from_psum(n, j):
             if j == 0:
                 state["products", n] = work.tile([P, 6, 2, 2, HALF], F32, name="products", bufs=ROPED_ON_VECTOR)
             rope_products(n, nc.vector, state["pr", n, j][:, :, 64:256], j, j + 1)
 
-        def store(n, j0=0, j1=2):
+        def add_on_vector(n, j0=0, j1=2):
+            halves = state["products", n][:].rearrange("p (j s) h w d -> p j s h (w d)", j=2)[:, j0:j1]
+            nc.vector.tensor_tensor(
+                out=out_kv(n)[:, j0:j1, KVR:], in0=halves[:, :, 0, 0, :], in1=halves[:, :, 0, 1, :], op=ADD
+            )
+            nc.vector.tensor_tensor(
+                out=out_q(n)[:, j0:j1, :, DN:], in0=halves[:, :, 1:, 0, :], in1=halves[:, :, 1:, 1, :], op=ADD
+            )
+
+        def store(n):
             ot = out_tile(n)
-            tiles = slice(2 * n + j0, 2 * n + j1)
-            nc.sync.dma_start(out=out_hbm[:, tiles, 0:384], in_=ot[:, j0:j1, 128:512])
-            nc.sync.dma_start(out=out_hbm[:, tiles, 384:512], in_=ot[:, j0:j1, 0:128])
+            nc.sync.dma_start(out=out_hbm[:, 2 * n : 2 * n + 2, 0:384], in_=ot[:, :, 128:512])
+            nc.sync.dma_start(out=out_hbm[:, 2 * n : 2 * n + 2, 384:512], in_=ot[:, :, 0:128])
 
-        def store_plain(n):
-            for h in range(NH):
-                c0 = h * (DN + DR)
-                nc.sync.dma_start(
-                    out=out_hbm[:, 2 * n : 2 * n + 2, c0 : c0 + DN], in_=out_tile(n)[:, :, 128 + c0 : 128 + c0 + DN]
-                )
-
-        def store_roped(n):
-            for h in range(NH):
-                c0 = h * (DN + DR) + DN
-                nc.sync.dma_start(
-                    out=out_hbm[:, 2 * n : 2 * n + 2, c0 : c0 + DR], in_=out_tile(n)[:, :, 128 + c0 : 128 + c0 + DR]
-                )
-            nc.sync.dma_start(out=out_hbm[:, 2 * n : 2 * n + 2, 384:512], in_=out_tile(n)[:, :, 0:128])
+        def store_rows(n, j0=0, j1=2):
+            nc.sync.dma_start(out=out_hbm[:, 2 * n + j0 : 2 * n + j1, :], in_=out_tile(n)[:, j0:j1, :])
 
         def rms_tile1(n):
             inverse_rms(n, 1 if n < PAIRS else 2, 4 if n >= 2 else 2)
 
         step = (
-            (quant_c, 3),
             (quant_x, 1),
+            (quant_c, 3),
             (rope, 4),
             (lambda n: turn_x(n, 1), 0),
-            (copy_nope, 4),
-            (rms_tile1, 2),
             (lambda n: widen(n, 0), -1),
-            (mm_kv, 3),
-            (mm_rope, 3),
-            (lambda n: mm_a(n, 0), 1),
-            (mm_nope, 3),
-            (copy_rope, 3),
+            (rms_tile1, 2),
             (lambda n: widen(n, 1), -1),
+            (mm_kv, 3),
+            (lambda n: mm_a(n, 0), 1),
+            (mm_rope, 3),
+            (mm_nope, 3),
             (lambda n: scale_x(n, 0), 0),
             (lambda n: norm_a(n, 1), 2),
             (lambda n: square_a(n, 0), 1),
-            (square_kv, 3),
+            (copy_rope, 3),
             (lambda n: inverse_rms(n, 0, 1), 1),
+            (square_kv, 3),
+            (copy_nope, 3),
             (lambda n: turn_c(n, 0), 2),
             (lambda n: turn_x(n, 0), -1),
             (lambda n: turn_c(n, 1), 2),
@@ -504,72 +508,99 @@ def tile_mla_model_t_kernel(
         square_a(1, 1)
         wb_quant()
 
-        for s in range(3, PAIRS):
+        for s in range(3, PAIRS - 1):
             for stage, lag in step:
                 if 0 <= s - lag < PAIRS:
                     stage(s - lag)
 
         a, b, c, d = range(PAIRS - 4, PAIRS)
+        quant_x(c)
+        quant_c(a)
+        rope(a - 1)
+        turn_x(d, 1)
+        rms_tile1(b)
+        mm_kv(a)
+        mm_a(c, 0)
+        mm_rope(a)
+        mm_nope(a)
+        scale_x(d, 0)
+        norm_a(b, 1)
+        square_a(c, 0)
+        copy_rope(a)
+        inverse_rms(c, 0, 1)
+        square_kv(a)
+        turn_c(b, 0)
+        mm_kv(b, (0, 1), spare_bank([P, 2, 256]))
+        square_kv(b)
+        turn_c(b, 1)
+        mm_a(c, 1)
+        scale_x(d, 1)
+        norm_a(c, 0)
+        norm_kv(a - 1)
+        store(a - 1)
+        empty_c(b)
+        inverse_rms(c, 2, 4)
+        inverse_rms(d, 2, 4)
+        square_a(c, 1)
+        copy_nope(a)
+        inverse_rms(c, 1, 2)
         quant_x(d)
         quant_c(b)
         rope(a)
-        rms_tile1(c)
-        mm_kv(b)
-        square_kv(b)
-        mm_a(d, 0)
-        mm_rope(b)
-        mm_a(d, 1, spare_bank([P, QR]))
-        copy_nope(a)
-        inverse_rms(d, 2, 4)
-        norm_a(c, 1)
+        mm_kv(c)
+        square_kv(c)
         norm_kv(a)
         store(a)
         norm_kv(b)
+        mm_a(d, 0)
+        mm_a(d, 1, spare_bank([P, QR]))
+        mm_rope(b)
+        norm_a(c, 1)
+        rms_tile1(d + 1)
         square_a(d, 0)
-        mm_kv(c)
+        square_a(d, 1)
         turn_c(c, 0)
         turn_c(c, 1)
-        mm_kv(d, (0, 1), ps_a.tile([P, 2, 256], F32, name="pa"))
+        mm_kv(d, (0,))
+        mm_kv(d, (1,), ps_a.tile([P, 2, 256], F32, name="pa"))
         mm_nope(b)
+        norm_kv(c)
         products_from_psum(b, 0)
         products_from_psum(b, 1)
         inverse_rms(d, 0, 1)
-        square_a(d, 1)
-        square_kv(c)
         inverse_rms(d, 1, 2)
         empty_c(c)
+        square_kv(d)
         norm_a(d, 0)
         norm_a(d, 1)
         quant_c(c)
-        square_kv(d)
+        copy_nope(b)
+        rms_tile1(d + 2)
         turn_c(d, 0)
         turn_c(d, 1, spare_bank([P, 2, 2, P]))
-        rope_add(b, nc.vector)
+        add_on_vector(b)
+        store_rows(b)
         mm_rope(c)
         mm_nope(c, (0, 1), ps_a.tile([P, 2, 256], F32, name="pa"))
-        rms_tile1(d + 1)
-        copy_nope(b)
-        store(b)
         empty_c(d, 0, 1)
-        rms_tile1(d + 2)
         empty_c(d, 1, 2)
         copy_nope(c)
-        store_plain(c)
-        norm_kv(c)
-        quant_c(d, 0, 1)
         norm_kv(d)
-        quant_c(d, 1, 2)
-        mm_rope(d)
-        mm_nope(d)
+        quant_c(d, 0, 1)
+        mm_rope(d, (0,))
+        mm_nope(d, (0,))
         products_from_psum(c, 0)
+        quant_c(d, 1, 2)
+        mm_rope(d, (1,))
+        mm_nope(d, (1,), ps_c.tile([P, 2, 256], F32, name="ct"))
         products_from_psum(c, 1)
         products_from_psum(d, 0)
-        rope_add(c, nc.vector)
-        store_roped(c)
+        add_on_vector(c)
+        store_rows(c)
         products_from_psum(d, 1)
         copy_nope(d, 0, 1)
         copy_nope(d, 1, 2)
-        rope_add(d, nc.vector, 0, 1)
-        store(d, 0, 1)
-        rope_add(d, nc.vector, 1, 2)
-        store(d, 1, 2)
+        add_on_vector(d, 0, 1)
+        store_rows(d, 0, 1)
+        add_on_vector(d, 1, 2)
+        store_rows(d, 1, 2)

@@ -88,9 +88,9 @@ def tile_mla_model_t_kernel(
         nc.sync.dma_start(out=wb_raw[:], in_=wq_b.rearrange("(p j) c -> p j c", j=4))
         nc.sync.dma_start(out=gq_raw[:], in_=gamma_cq.partition_broadcast(P))
         load_x(6, 8)
+        nc.sync.dma_start(out=sin[:], in_=sin_hbm)
         nc.sync.dma_start(out=cos[:], in_=cos_hbm)
         load_x(8, 12)
-        nc.sync.dma_start(out=sin[:], in_=sin_hbm)
         nc.sync.dma_start(out=gkv[:], in_=gamma_ckv.partition_broadcast(P))
         for i0 in range(12, N_TILES, 4):
             load_x(i0, i0 + 4)
@@ -159,11 +159,13 @@ def tile_mla_model_t_kernel(
         def rope_table():
             factors = keep.tile([P, N_TILES, 2, 2, HALF], BF16, name="factors", align_bytes=64)
             gpsimd_copy(factors[:, :, 1, 0, :], sin[:, :, 0:HALF], -1.0)
-            gpsimd_copy(
-                factors[:].rearrange("p i h w d -> p i (h w) d")[:, :, 0:4:3, :],
-                cos[:].rearrange("p i (h d) -> p i h d", h=2),
-            )
             state["factors"] = factors
+
+        def table_cos():
+            nc.scalar.copy(
+                out=state["factors"][:].rearrange("p i h w d -> p i (h w) d")[:, :, 0:4:3, :],
+                in_=cos[:].rearrange("p i (h d) -> p i h d", h=2),
+            )
 
         def table_sin():
             nc.scalar.copy(out=state["factors"][:, :, 0, 1, :], in_=sin[:, :, HALF:])
@@ -506,6 +508,7 @@ def tile_mla_model_t_kernel(
         empty_c(0)
         norm_a(1, 0)
         square_a(1, 1)
+        table_cos()
         wb_quant()
 
         for s in range(3, PAIRS - 1):

@@ -380,6 +380,16 @@ def tile_mla_model_t_kernel(
                     op1=MULT,
                 )
 
+        def gain_kv(n):
+            gained = work.tile([P, 2, KVR], F32, name="gained", bufs=2)
+            nc.vector.tensor_tensor(
+                out=gained[:],
+                in0=state["pr", n, 0][:, :, 0:KVR],
+                in1=gkv[:].unsqueeze(1).to_broadcast([P, 2, KVR]),
+                op=MULT,
+            )
+            state["gained", n] = gained
+
         def rope_products(n, engine, source, j0, j1):
             shape = [P, j1 - j0, 3, 2, 2, HALF]
             engine.tensor_tensor(
@@ -392,6 +402,12 @@ def tile_mla_model_t_kernel(
         def rope(n):
             state["products", n] = shared(n + 1, [P, 6, 2, 2, HALF], F32)
             rope_products(n, nc.gpsimd, state["to_rope", n][:], 0, 2)
+            nc.gpsimd.tensor_tensor(
+                out=out_kv(n)[:, :, 0:KVR],
+                in0=state["gained", n][:],
+                in1=stat("rinv", n + 2)[:, 2:4].unsqueeze(2).to_broadcast([P, 2, KVR]),
+                op=MULT,
+            )
             halves = state["products", n][:].rearrange("p s h w d -> p s h (w d)")
             nc.gpsimd.tensor_tensor(
                 out=out_tile(n)[:].rearrange("p j (s c) -> p (j s) c", c=DN + DR)[:, :, 64:128],
@@ -428,10 +444,10 @@ def tile_mla_model_t_kernel(
         step = (
             (quant_x, 1),
             (quant_c, 3),
-            (rope, 4),
             (lambda n: turn_x(n, 1), 0),
             (lambda n: widen(n, 0), -1),
             (rms_tile1, 2),
+            (rope, 4),
             (lambda n: widen(n, 1), -1),
             (mm_kv, 3),
             (lambda n: mm_a(n, 0), 1),
@@ -450,7 +466,7 @@ def tile_mla_model_t_kernel(
             (lambda n: mm_a(n, 1), 1),
             (lambda n: scale_x(n, 1), 0),
             (lambda n: norm_a(n, 0), 1),
-            (norm_kv, 4),
+            (gain_kv, 3),
             (store, 4),
             (empty_c, 2),
             (lambda n: square_a(n, 1), 1),
@@ -519,9 +535,9 @@ def tile_mla_model_t_kernel(
         a, b, c, d = range(PAIRS - 4, PAIRS)
         quant_x(c)
         quant_c(a)
-        rope(a - 1)
         turn_x(d, 1)
         rms_tile1(b)
+        rope(a - 1)
         mm_kv(a)
         mm_a(c, 0)
         mm_rope(a)
@@ -539,7 +555,7 @@ def tile_mla_model_t_kernel(
         mm_a(c, 1)
         scale_x(d, 1)
         norm_a(c, 0)
-        norm_kv(a - 1)
+        gain_kv(a)
         store(a - 1)
         empty_c(b)
         inverse_rms(c, 2, 4)
@@ -552,7 +568,6 @@ def tile_mla_model_t_kernel(
         rope(a)
         mm_kv(c)
         square_kv(c)
-        norm_kv(a)
         store(a)
         norm_kv(b)
         mm_a(d, 0)

@@ -40,10 +40,10 @@ def tile_mla_model_t_kernel(
         keep = ctx.enter_context(tc.tile_pool(name="keep", bufs=1))
         work = ctx.enter_context(tc.tile_pool(name="work", bufs=2))
         ps_x = ctx.enter_context(tc.psum_pool(name="ps_x", bufs=2))
-        ps_a = ctx.enter_context(tc.psum_pool(name="ps_a", bufs=2))
+        ps_a = ctx.enter_context(tc.psum_pool(name="ps_a", bufs=3))
         ps_c = ctx.enter_context(tc.psum_pool(name="ps_c", bufs=1))
         ps_n = ctx.enter_context(tc.psum_pool(name="ps_n", bufs=1))
-        ps_r = ctx.enter_context(tc.psum_pool(name="ps_r", bufs=2))
+        ps_r = ctx.enter_context(tc.psum_pool(name="ps_r", bufs=1))
         ctx.enter_context(tc.manual_schedule())
 
         x_raw = keep.tile([P, N_TILES * H], U8, name="x_raw")
@@ -156,30 +156,31 @@ def tile_mla_model_t_kernel(
         def wb_quant():
             nc.vector.quantize_mx(out=wb_c[:].bitcast(FP8X4), scales=wb_s[:], in_=state["wb_g"][:])
 
-        def rope_table():
-            factors = keep.tile([P, N_TILES, 2, 2, HALF], BF16, name="factors", align_bytes=64)
-            gpsimd_copy(factors[:, :, 1, 0, :], sin[:, :, 0:HALF], -1.0)
-            state["factors"] = factors
-
-        def table_cos():
-            nc.scalar.copy(
-                out=state["factors"][:].rearrange("p i h w d -> p i (h w) d")[:, :, 0:4:3, :],
-                in_=cos[:].rearrange("p i (h d) -> p i h d", h=2),
+        def rope_table(part):
+            tiles = slice(PAIRS * part, PAIRS * (part + 1))
+            factors = keep.tile([P, PAIRS, 2, 2, HALF], BF16, name="factors%d" % part, align_bytes=64)
+            gpsimd_copy(factors[:, :, 1, 0, :], sin[:, tiles, 0:HALF], -1.0)
+            gpsimd_copy(
+                factors[:].rearrange("p i h w d -> p i (h w) d")[:, :, 0:4:3, :],
+                cos[:, tiles].rearrange("p i (h d) -> p i h d", h=2),
             )
+            state["factors", part] = factors
 
-        def table_sin():
-            nc.scalar.copy(out=state["factors"][:, :, 0, 1, :], in_=sin[:, :, HALF:])
+        def table_sin(part, copy):
+            tiles = slice(PAIRS * part, PAIRS * (part + 1))
+            copy(out=state["factors", part][:, :, 0, 1, :], in_=sin[:, tiles, HALF:])
 
 
-        def widen(n, j):
-            i = 2 * n + j
-            xw = work.tile([P, H], BF16, name="xw", bufs=4)
-            nc.scalar.copy(out=xw[:], in_=x_raw[:, i * H : (i + 1) * H].bitcast(FP8))
-            state["xw", n, j] = xw
+        def widen(n, j0=0, j1=2):
+            if j0 == 0:
+                state["xw", n] = work.tile([P, 2 * H], BF16, name="xw", bufs=2)
+            nc.scalar.copy(
+                out=state["xw", n][:, j0 * H : j1 * H], in_=x_raw[:, (2 * n + j0) * H : (2 * n + j1) * H].bitcast(FP8)
+            )
 
         def turn_x(n, j):
             xt = ps_x.tile([P, 2, 2, P], F32, name="xt")
-            words = state["xw", n, j][:].bitcast(F32)
+            words = state["xw", n][:, j * H : (j + 1) * H].bitcast(F32)
             for g in range(2):
                 for u in range(2):
                     nc.tensor.transpose(xt[:, u, g, :], words[:, 256 * g + u : 256 * (g + 1) : 2], ident[:])
@@ -187,8 +188,8 @@ def tile_mla_model_t_kernel(
 
         def scale_x(n, j):
             if j == 0:
-                if n == 1:
-                    state["xg", n] = keep.tile([P, 2 * H], BF16, name="factors", align_bytes=64)
+                if n in (1, 2):
+                    state["xg", n] = keep.tile([P, 2 * H], BF16, name="factors%d" % (n - 1), align_bytes=64)
                 else:
                     state["xg", n] = work.tile([P, 2 * H], BF16, name="xg", bufs=2, align_bytes=64)
             nc.vector.tensor_tensor(
@@ -392,10 +393,11 @@ def tile_mla_model_t_kernel(
 
         def rope_products(n, engine, source, j0, j1):
             shape = [P, j1 - j0, 3, 2, 2, HALF]
+            part, i = divmod(2 * n, PAIRS)
             engine.tensor_tensor(
                 out=state["products", n][:, 3 * j0 : 3 * j1].rearrange("p (j s) h w d -> p j s h w d", s=3),
                 in0=source[:, j0:j1].rearrange("p j (s h d) -> p j s h d", s=3, h=2).unsqueeze(4).to_broadcast(shape),
-                in1=state["factors"][:, 2 * n + j0 : 2 * n + j1].unsqueeze(2).to_broadcast(shape),
+                in1=state["factors", part][:, i + j0 : i + j1].unsqueeze(2).to_broadcast(shape),
                 op=MULT,
             )
 
@@ -438,60 +440,67 @@ def tile_mla_model_t_kernel(
         def store_rows(n, j0=0, j1=2):
             nc.sync.dma_start(out=out_hbm[:, 2 * n + j0 : 2 * n + j1, :], in_=out_tile(n)[:, j0:j1, :])
 
-        def rms_tile1(n):
-            inverse_rms(n, 1 if n < PAIRS else 2, 4 if n >= 2 else 2)
+        def rms_step(n):
+            inverse_rms(n, 0, 4 if n >= 2 else 2)
+
+        def second_table(n):
+            if n == 0:
+                rope_table(1)
+
+        def second_table_sin(n):
+            if n == 0:
+                table_sin(1, nc.vector.tensor_copy)
 
         step = (
-            (quant_x, 1),
+            (second_table_sin, 4),
             (quant_c, 3),
-            (lambda n: turn_x(n, 1), 0),
-            (lambda n: widen(n, 0), -1),
-            (rms_tile1, 2),
+            (quant_x, 1),
+            (square_kv, 3),
+            (rms_step, 2),
             (rope, 4),
-            (lambda n: widen(n, 1), -1),
-            (mm_kv, 3),
-            (lambda n: mm_a(n, 0), 1),
+            (second_table, 3),
             (mm_rope, 3),
             (mm_nope, 3),
-            (lambda n: scale_x(n, 0), 0),
-            (lambda n: norm_a(n, 1), 2),
-            (lambda n: square_a(n, 0), 1),
+            (lambda n: mm_a(n, 0), 1),
+            (widen, -1),
             (copy_rope, 3),
-            (lambda n: inverse_rms(n, 0, 1), 1),
-            (square_kv, 3),
             (copy_nope, 3),
+            (lambda n: norm_a(n, 0), 2),
+            (lambda n: norm_a(n, 1), 2),
+            (lambda n: turn_x(n, 1), 0),
+            (lambda n: square_a(n, 0), 1),
             (lambda n: turn_c(n, 0), 2),
-            (lambda n: turn_x(n, 0), -1),
             (lambda n: turn_c(n, 1), 2),
             (lambda n: mm_a(n, 1), 1),
-            (lambda n: scale_x(n, 1), 0),
-            (lambda n: norm_a(n, 0), 1),
+            (lambda n: scale_x(n, 0), 0),
             (gain_kv, 3),
+            (mm_kv, 2),
+            (lambda n: turn_x(n, 0), -1),
+            (lambda n: scale_x(n, 1), 0),
             (store, 4),
             (empty_c, 2),
             (lambda n: square_a(n, 1), 1),
         )
 
-        widen(0, 0)
+        widen(0, 0, 1)
         turn_x(0, 0)
-        widen(0, 1)
+        widen(0, 1, 2)
         turn_x(0, 1)
         wa_copy(0, nc.vector.tensor_copy)
         wa_copy(1, nc.scalar.copy)
         wa_copy(2, nc.scalar.copy)
         wa_copy_gpsimd(3)
         scale_x(0, 0)
-        widen(1, 0)
+        widen(1, 0, 1)
         turn_x(1, 0)
         scale_x(0, 1)
-        widen(1, 1)
+        widen(1, 1, 2)
         turn_x(1, 1)
         wa_quant(0)
         quant_x(0)
         wa_quant(1)
+        widen(2)
         wkv_copy()
-        widen(2, 0)
-        widen(2, 1)
         wb_copy()
         mm_a(0, 0)
         scale_x(1, 0)
@@ -504,27 +513,25 @@ def tile_mla_model_t_kernel(
         square_a(0, 0)
         gamma_copy()
         inverse_rms(0, 0, 1)
-        widen(3, 0)
+        rope_table(0)
+        widen(3, 0, 1)
         square_a(0, 1)
-        widen(3, 1)
-        rms_tile1(0)
-        rope_table()
-        norm_a(0, 0)
+        widen(3, 1, 2)
+        inverse_rms(0, 1, 2)
         mm_a(1, 0)
+        norm_a(0, 0)
+        turn_c(0, 0)
         scale_x(2, 0)
         norm_a(0, 1)
         square_a(1, 0)
-        table_sin()
-        inverse_rms(1, 0, 1)
-        turn_c(0, 0)
-        turn_x(3, 0)
+        table_sin(0, nc.scalar.copy)
         turn_c(0, 1)
         mm_a(1, 1)
+        mm_kv(0)
+        turn_x(3, 0)
         scale_x(2, 1)
         empty_c(0)
-        norm_a(1, 0)
         square_a(1, 1)
-        table_cos()
         wb_quant()
 
         for s in range(3, PAIRS - 1):
@@ -533,53 +540,51 @@ def tile_mla_model_t_kernel(
                     stage(s - lag)
 
         a, b, c, d = range(PAIRS - 4, PAIRS)
-        quant_x(c)
         quant_c(a)
-        turn_x(d, 1)
-        rms_tile1(b)
+        quant_x(c)
+        square_kv(a)
+        rms_step(b)
         rope(a - 1)
-        mm_kv(a)
-        mm_a(c, 0)
         mm_rope(a)
         mm_nope(a)
-        scale_x(d, 0)
-        norm_a(b, 1)
-        square_a(c, 0)
+        mm_a(c, 0)
         copy_rope(a)
-        inverse_rms(c, 0, 1)
-        square_kv(a)
+        copy_nope(a)
+        norm_a(b, 0)
+        norm_a(b, 1)
+        turn_x(d, 1)
+        square_a(c, 0)
         turn_c(b, 0)
-        mm_kv(b, (0, 1), spare_bank([P, 2, 256]))
-        square_kv(b)
         turn_c(b, 1)
         mm_a(c, 1)
-        scale_x(d, 1)
-        norm_a(c, 0)
+        scale_x(d, 0)
         gain_kv(a)
+        mm_kv(b)
+        mm_kv(c, (0, 1), spare_bank([P, 2, 256]))
+        scale_x(d, 1)
         store(a - 1)
         empty_c(b)
-        inverse_rms(c, 2, 4)
-        inverse_rms(d, 2, 4)
         square_a(c, 1)
-        copy_nope(a)
-        inverse_rms(c, 1, 2)
-        quant_x(d)
+        square_kv(b)
         quant_c(b)
-        rope(a)
-        mm_kv(c)
+        quant_x(d)
+        rms_step(c)
         square_kv(c)
+        inverse_rms(d, 2, 4)
+        rope(a)
         store(a)
-        norm_kv(b)
         mm_a(d, 0)
+        norm_a(c, 0)
         mm_a(d, 1, spare_bank([P, QR]))
-        mm_rope(b)
+        norm_kv(b)
         norm_a(c, 1)
-        rms_tile1(d + 1)
+        mm_rope(b)
+        inverse_rms(d + 1, 2, 4)
         square_a(d, 0)
         square_a(d, 1)
         turn_c(c, 0)
         turn_c(c, 1)
-        mm_kv(d, (0,))
+        mm_kv(d, (0,), ps_a.tile([P, 2, 256], F32, name="pa"))
         mm_kv(d, (1,), ps_a.tile([P, 2, 256], F32, name="pa"))
         mm_nope(b)
         norm_kv(c)
@@ -593,9 +598,9 @@ def tile_mla_model_t_kernel(
         norm_a(d, 1)
         quant_c(c)
         copy_nope(b)
-        rms_tile1(d + 2)
+        inverse_rms(d + 2, 2, 4)
         turn_c(d, 0)
-        turn_c(d, 1, spare_bank([P, 2, 2, P]))
+        turn_c(d, 1, ps_r.tile([P, 2, 2, P], F32, name="pr"))
         add_on_vector(b)
         store_rows(b)
         mm_rope(c)

@@ -51,9 +51,10 @@ def tile_mla_model_t_kernel(
         wa_raw = [keep.tile([P, 4, QR], BF16, name="wa_raw%d" % g) for g in range(2)]
         wkv_raw = keep.tile([P, 2, 4, KVR + DR], BF16, name="wkv_raw")
         wb_raw = keep.tile([P, 4, NH * (DN + DR)], BF16, name="wb_raw")
-        gq_raw = keep.tile([P, QR], BF16, name="gq_raw")
-        gq = keep.tile([P, QR], BF16, name="gq")
-        gkv = keep.tile([P, KVR], BF16, name="gkv")
+        gq_col = keep.tile([P, 4], BF16, name="gq_col")
+        gkv_col = keep.tile([P, 2], BF16, name="gkv_col")
+        gains = keep.tile([P, QR + KVR], BF16, name="gains")
+        gq, gkv = gains[:, 0:QR], gains[:, QR:]
         cos = keep.tile([P, N_TILES, DR], BF16, name="cos")
         sin = keep.tile([P, N_TILES, DR], BF16, name="sin")
         ident = keep.tile([P, P], F32, name="ident")
@@ -77,6 +78,8 @@ def tile_mla_model_t_kernel(
         def load_wa(g):
             nc.sync.dma_start(out=wa_raw[g][:], in_=wq_a.rearrange("(g p j) c -> g p j c", p=P, j=4)[g])
 
+        nc.vector.memset(gkv_col[:], 0.0)
+
         load_x(0, 1)
         nc.sync.dma_start(out=scale[:], in_=x_scale.rearrange("o (g p t) -> p (o g) t", g=2, t=4))
         load_x(1, 2)
@@ -85,13 +88,13 @@ def tile_mla_model_t_kernel(
         load_x(2, 4)
         nc.sync.dma_start(out=wkv_raw[:], in_=wkv.rearrange("(g p j) c -> p g j c", p=P, j=4))
         load_x(4, 6)
+        nc.sync.dma_start(out=gq_col[:], in_=gamma_cq.rearrange("(p t) -> p t", t=4))
+        nc.sync.dma_start(out=gkv_col[0:32, :], in_=gamma_ckv.rearrange("(p e) -> p e", e=2))
         nc.sync.dma_start(out=wb_raw[:], in_=wq_b.rearrange("(p j) c -> p j c", j=4))
-        nc.sync.dma_start(out=gq_raw[:], in_=gamma_cq.partition_broadcast(P))
         load_x(6, 8)
         nc.sync.dma_start(out=sin[:], in_=sin_hbm)
         nc.sync.dma_start(out=cos[:], in_=cos_hbm)
         load_x(8, 12)
-        nc.sync.dma_start(out=gkv[:], in_=gamma_ckv.partition_broadcast(P))
         for i0 in range(12, N_TILES, 4):
             load_x(i0, i0 + 4)
 
@@ -127,11 +130,16 @@ def tile_mla_model_t_kernel(
                 out=wa_c[:, g, :].bitcast(FP8X4), scales=wa_s[:, g, :], in_=wa_g[:, g * 2048 : (g + 1) * 2048]
             )
 
+        def gamma_turn():
+            bank = ps_n.tile([P, 3, P], F32, name="pn")
+            for u in range(2):
+                nc.tensor.transpose(bank[:, u, :], gq_col[:].bitcast(F32)[:, u : u + 1].to_broadcast([P, P]), ident[:])
+            nc.tensor.transpose(bank[:, 2, :], gkv_col[:].bitcast(F32).to_broadcast([P, P]), ident[:])
+            state["gains"] = bank
+
         def gamma_copy():
-            nc.scalar.copy(
-                out=gq[:].rearrange("p (u m e) -> p u m e", u=2, e=2),
-                in_=gq_raw[:].rearrange("p (m u e) -> p u m e", u=2, e=2),
-            )
+            words = (QR + KVR) // 2
+            nc.scalar.copy(out=gains[:].bitcast(F32), in_=state["gains"][:].rearrange("p u m -> p (u m)")[:, 0:words])
 
         def wkv_copy():
             nc.scalar.copy(
@@ -251,7 +259,7 @@ def tile_mla_model_t_kernel(
                 out=cq[:],
                 in0=state["pa", n, j][:],
                 scalar=stat("rinv", n)[:, j : j + 1],
-                in1=gq[:],
+                in1=gq,
                 op0=MULT,
                 op1=MULT,
             )
@@ -376,7 +384,7 @@ def tile_mla_model_t_kernel(
                     out=out_kv(n)[:, j, 0:KVR],
                     in0=state["pr", n, j][:, j, 0:KVR],
                     scalar=stat("rinv", n + 2)[:, 2 + j : 3 + j],
-                    in1=gkv[:],
+                    in1=gkv,
                     op0=MULT,
                     op1=MULT,
                 )
@@ -386,7 +394,7 @@ def tile_mla_model_t_kernel(
             nc.vector.tensor_tensor(
                 out=gained[:],
                 in0=state["pr", n, 0][:, :, 0:KVR],
-                in1=gkv[:].unsqueeze(1).to_broadcast([P, 2, KVR]),
+                in1=gkv.unsqueeze(1).to_broadcast([P, 2, KVR]),
                 op=MULT,
             )
             state["gained", n] = gained
@@ -502,6 +510,7 @@ def tile_mla_model_t_kernel(
         widen(2)
         wkv_copy()
         wb_copy()
+        gamma_turn()
         mm_a(0, 0)
         scale_x(1, 0)
         turn_x(2, 0)

@@ -110,10 +110,10 @@ def tile_mla_model_t_kernel(
 
         def wa_views(part):
             g, half = divmod(part, 2)
-            grouped = wa_g[:].rearrange("p (g u m e j) -> p g u m e j", g=2, u=2, e=2, j=4)
+            grouped = wa_g[:].rearrange("p (g u m e j) -> p g m j u e", g=2, u=2, e=2, j=4)
             return (
-                grouped[:, g, :, 64 * half : 64 * (half + 1)],
-                wa_raw[g][:, :, 256 * half : 256 * (half + 1)].rearrange("p j (m u e) -> p u m e j", u=2, e=2),
+                grouped[:, g, 64 * half : 64 * (half + 1)],
+                wa_raw[g][:, :, 256 * half : 256 * (half + 1)].rearrange("p j (m u e) -> p m j u e", u=2, e=2),
             )
 
         def wa_copy(part, copy):
@@ -123,7 +123,7 @@ def tile_mla_model_t_kernel(
         def wa_copy_gpsimd(part):
             dst, src = wa_views(part)
             for u in range(2):
-                gpsimd_copy(dst[:, u], src[:, u])
+                gpsimd_copy(dst[:, :, :, u], src[:, :, :, u])
 
         def wa_quant(g):
             nc.vector.quantize_mx(
@@ -143,15 +143,18 @@ def tile_mla_model_t_kernel(
 
         def wkv_copy():
             nc.scalar.copy(
-                out=wkv_g[:].rearrange("p (g c j) -> p g c j", g=2, j=4), in_=wkv_raw[:].rearrange("p g j c -> p g c j")
+                out=wkv_g[:].rearrange("p (g c i j) -> p g c j i", g=2, i=4, j=4),
+                in_=wkv_raw[:].rearrange("p g j (c i) -> p g c j i", i=4),
             )
 
         def wb_copy():
             wb_g = keep.tile([P, 384 * 4], BF16, name="grouped", align_bytes=64)
-            wb_dst = wb_g[:].rearrange("p (c j) -> p c j", j=4)
-            wb_src = wb_raw[:].rearrange("p j (h c) -> p h c j", h=NH)
-            gpsimd_copy(wb_dst[:, 0:256].rearrange("p (h c) j -> p h c j", h=NH), wb_src[:, :, 0:DN])
-            nc.scalar.copy(out=wb_dst[:, 256:384].rearrange("p (h c) j -> p h c j", h=NH), in_=wb_src[:, :, DN:])
+            wb_src = wb_raw[:].rearrange("p j (h c i) -> p h c j i", h=NH, i=4)
+            plain = wb_g[:, 0:1024].rearrange("p (h c i j) -> p h c j i", h=NH, i=4, j=4)
+            roped = wb_g[:, 1024:].rearrange("p (h c i j) -> p h c j i", h=NH, i=4, j=4)
+            for h in range(NH):
+                gpsimd_copy(plain[:, h], wb_src[:, h, 0 : DN // 4])
+            nc.scalar.copy(out=roped, in_=wb_src[:, :, DN // 4 :])
             state["wb_g"] = wb_g
 
         def wkv_quant():

@@ -7,14 +7,17 @@ T, H, QR = 4096, 1024, 512
 NH, DN, DR, KVR = 2, 128, 64, 64
 HALF = DR // 2
 EPS = 1e-6
-OUT_W = NH * (DN + DR) + KVR + DR
+HEAD = DN + DR
+ROW = 3 * HEAD
 
 FLOPS = 2 * T * (H * (QR + KVR + DR) + QR * NH * (DN + DR))
 
 P = 128
 N_TILES = T // P
 PAIRS = N_TILES // 2
-ROPED_ON_VECTOR = 3
+
+WB_ON_GPSIMD = 96
+WKV_ON_GPSIMD = 96
 
 F32 = mybir.dt.float32
 BF16 = mybir.dt.bfloat16
@@ -50,13 +53,12 @@ def tile_mla_model_t_kernel(
         scale = keep.tile([P, 2, 4], F32, name="scale")
         wa_raw = [keep.tile([P, 4, QR], BF16, name="wa_raw%d" % g) for g in range(2)]
         wkv_raw = keep.tile([P, 2, 4, KVR + DR], BF16, name="wkv_raw")
-        wb_raw = keep.tile([P, 4, NH * (DN + DR)], BF16, name="wb_raw")
+        wb_raw = keep.tile([P, 4, NH * HEAD], BF16, name="wb_raw")
         gq_col = keep.tile([P, 4], BF16, name="gq_col")
         gkv_col = keep.tile([P, 2], BF16, name="gkv_col")
         gains = keep.tile([P, QR + KVR], BF16, name="gains")
         gq, gkv = gains[:, 0:QR], gains[:, QR:]
-        cos = keep.tile([P, N_TILES, DR], BF16, name="cos")
-        sin = keep.tile([P, N_TILES, DR], BF16, name="sin")
+        factors = [keep.tile([P, PAIRS, 2, 2, HALF], BF16, name="factors%d" % part, align_bytes=64) for part in range(2)]
         ident = keep.tile([P, P], F32, name="ident")
         one = keep.tile([P, 1], F32, name="one")
         eps = keep.tile([P, 1], F32, name="eps")
@@ -64,7 +66,6 @@ def tile_mla_model_t_kernel(
         wa_g = keep.tile([P, 2 * QR * 4], BF16, name="grouped", align_bytes=64)
         wa_c = keep.tile([P, 2, QR], U32, name="wa_c", align_bytes=64)
         wa_s = keep.tile([P, 2, QR], U8, name="wa_s", align_bytes=64)
-        wkv_g = keep.tile([P, 2 * 128 * 4], BF16, name="wkv_g", align_bytes=64)
         wkv_c = keep.tile([P, 2, 128], U32, name="wkv_c", align_bytes=64)
         wkv_s = keep.tile([P, 2, 128], U8, name="wkv_s", align_bytes=64)
         wb_c = keep.tile([P, 384], U32, name="wb_c", align_bytes=64)
@@ -78,25 +79,41 @@ def tile_mla_model_t_kernel(
         def load_wa(g):
             nc.sync.dma_start(out=wa_raw[g][:], in_=wq_a.rearrange("(g p j) c -> g p j c", p=P, j=4)[g])
 
+        def load_factors(part):
+            tiles = slice(PAIRS * part, PAIRS * (part + 1))
+            flat = factors[part][:].rearrange("p i w h d -> p (i w h d)")
+            cos_flat = cos_hbm[:, tiles, :].rearrange("p i d -> p (i d)")
+            nc.sync.dma_start(
+                out=flat.rearrange("p (i c) -> p i c", i=PAIRS)[:, :, HALF : 3 * HALF], in_=sin_hbm[:, tiles, :]
+            )
+            nc.sync.dma_start(
+                out=flat[:, 3 * HALF : 3 * HALF + (PAIRS - 1) * 2 * DR].rearrange("p (i c) -> p i c", c=2 * DR)[:, :, 0:DR],
+                in_=cos_flat[:, HALF : HALF + (PAIRS - 1) * DR].rearrange("p (i c) -> p i c", c=DR),
+            )
+            nc.sync.dma_start(
+                out=flat.rearrange("p (c d) -> p c d", d=HALF)[:, 0 : 4 * PAIRS : 4 * PAIRS - 1],
+                in_=cos_flat.rearrange("p (c d) -> p c d", d=HALF)[:, 0 : 2 * PAIRS : 2 * PAIRS - 1],
+            )
+
         nc.vector.memset(gkv_col[:], 0.0)
 
         load_x(0, 1)
         nc.sync.dma_start(out=scale[:], in_=x_scale.rearrange("o (g p t) -> p (o g) t", g=2, t=4))
         load_x(1, 2)
+        load_x(2, 4)
         load_wa(0)
         load_wa(1)
-        load_x(2, 4)
-        nc.sync.dma_start(out=wkv_raw[:], in_=wkv.rearrange("(g p j) c -> p g j c", p=P, j=4))
         load_x(4, 6)
         nc.sync.dma_start(out=gq_col[:], in_=gamma_cq.rearrange("(p t) -> p t", t=4))
         nc.sync.dma_start(out=gkv_col[0:32, :], in_=gamma_ckv.rearrange("(p e) -> p e", e=2))
         nc.sync.dma_start(out=wb_raw[:], in_=wq_b.rearrange("(p j) c -> p j c", j=4))
         load_x(6, 8)
-        nc.sync.dma_start(out=sin[:], in_=sin_hbm)
-        nc.sync.dma_start(out=cos[:], in_=cos_hbm)
+        nc.sync.dma_start(out=wkv_raw[:], in_=wkv.rearrange("(g p j) c -> p g j c", p=P, j=4))
         load_x(8, 12)
+        load_factors(0)
         for i0 in range(12, N_TILES, 4):
             load_x(i0, i0 + 4)
+        load_factors(1)
 
         make_identity(nc, ident[:])
         nc.vector.memset(one[:], 1.0)
@@ -108,22 +125,20 @@ def tile_mla_model_t_kernel(
         def gpsimd_copy(out, in_, sign=1.0):
             nc.gpsimd.tensor_scalar(out=out, in0=in_, scalar1=sign, scalar2=0.0, op0=MULT, op1=ADD)
 
-        def wa_views(part):
-            g, half = divmod(part, 2)
-            grouped = wa_g[:].rearrange("p (g u m e j) -> p g m j u e", g=2, u=2, e=2, j=4)
-            return (
-                grouped[:, g, 64 * half : 64 * (half + 1)],
-                wa_raw[g][:, :, 256 * half : 256 * (half + 1)].rearrange("p j (m u e) -> p m j u e", u=2, e=2),
+        wa_grouped = wa_g[:].rearrange("p (g u m e j) -> p g u m e j", g=2, u=2, e=2, j=4)
+
+        def wa_copy(g, m0, m1):
+            nc.scalar.copy(
+                out=wa_grouped[:, g, :, m0:m1].rearrange("p u m e j -> p m j u e"),
+                in_=wa_raw[g][:, :, 4 * m0 : 4 * m1].rearrange("p j (m u e) -> p m j u e", u=2, e=2),
             )
 
-        def wa_copy(part, copy):
-            dst, src = wa_views(part)
-            copy(out=dst, in_=src)
-
-        def wa_copy_gpsimd(part):
-            dst, src = wa_views(part)
+        def wa_copy_gpsimd(g, m0, m1):
             for u in range(2):
-                gpsimd_copy(dst[:, :, :, u], src[:, :, :, u])
+                gpsimd_copy(
+                    wa_grouped[:, g, u, m0:m1],
+                    wa_raw[g][:, :, 4 * m0 : 4 * m1].rearrange("p j (m u e) -> p u m e j", u=2, e=2)[:, u],
+                )
 
         def wa_quant(g):
             nc.vector.quantize_mx(
@@ -141,45 +156,48 @@ def tile_mla_model_t_kernel(
             words = (QR + KVR) // 2
             nc.scalar.copy(out=gains[:].bitcast(F32), in_=state["gains"][:].rearrange("p u m -> p (u m)")[:, 0:words])
 
-        def wkv_copy():
-            nc.scalar.copy(
-                out=wkv_g[:].rearrange("p (g c i j) -> p g c j i", g=2, i=4, j=4),
-                in_=wkv_raw[:].rearrange("p g j (c i) -> p g c j i", i=4),
+        def wkv_copy_gpsimd():
+            state["wkv_g"] = keep.tile([P, 2 * 128 * 4], BF16, name="wkv_g", align_bytes=64)
+            gpsimd_copy(
+                state["wkv_g"][:].rearrange("p (g c j) -> p g c j", g=2, j=4)[:, :, 0:WKV_ON_GPSIMD],
+                wkv_raw[:].rearrange("p g j c -> p g c j")[:, :, 0:WKV_ON_GPSIMD],
             )
 
-        def wb_copy():
-            wb_g = keep.tile([P, 384 * 4], BF16, name="grouped", align_bytes=64)
-            wb_src = wb_raw[:].rearrange("p j (h c i) -> p h c j i", h=NH, i=4)
-            plain = wb_g[:, 0:1024].rearrange("p (h c i j) -> p h c j i", h=NH, i=4, j=4)
-            roped = wb_g[:, 1024:].rearrange("p (h c i j) -> p h c j i", h=NH, i=4, j=4)
-            for h in range(NH):
-                gpsimd_copy(plain[:, h], wb_src[:, h, 0 : DN // 4])
-            nc.scalar.copy(out=roped, in_=wb_src[:, :, DN // 4 :])
-            state["wb_g"] = wb_g
+        def wkv_copy():
+            nc.scalar.copy(
+                out=state["wkv_g"][:].rearrange("p (g c i j) -> p g c j i", g=2, i=4, j=4)[:, :, WKV_ON_GPSIMD // 4 :],
+                in_=wkv_raw[:].rearrange("p g j (c i) -> p g c j i", i=4)[:, :, WKV_ON_GPSIMD // 4 :],
+            )
+
+        def wb_copy_gpsimd():
+            state["wb_g"] = keep.tile([P, 384 * 4], BF16, name="grouped", align_bytes=64)
+            gpsimd_copy(
+                state["wb_g"][:, 0:1024].rearrange("p (h c j) -> p h c j", h=NH, j=4)[:, :, 0:WB_ON_GPSIMD],
+                wb_raw[:].rearrange("p j (h c) -> p h c j", h=NH)[:, :, 0:WB_ON_GPSIMD],
+            )
+
+        def wb_copy(roped):
+            src = wb_raw[:].rearrange("p j (h c i) -> p h c j i", h=NH, i=4)
+            if roped:
+                dst = state["wb_g"][:, 1024:].rearrange("p (h c i j) -> p h c j i", h=NH, i=4, j=4)
+                nc.scalar.copy(out=dst, in_=src[:, :, DN // 4 :])
+            else:
+                dst = state["wb_g"][:, 0:1024].rearrange("p (h c i j) -> p h c j i", h=NH, i=4, j=4)
+                nc.scalar.copy(out=dst[:, :, WB_ON_GPSIMD // 4 :], in_=src[:, :, WB_ON_GPSIMD // 4 : DN // 4])
 
         def wkv_quant():
             nc.vector.quantize_mx(
                 out=wkv_c[:].rearrange("p g c -> p (g c)").bitcast(FP8X4),
                 scales=wkv_s[:].rearrange("p g c -> p (g c)"),
-                in_=wkv_g[:],
+                in_=state["wkv_g"][:],
             )
 
         def wb_quant():
             nc.vector.quantize_mx(out=wb_c[:].bitcast(FP8X4), scales=wb_s[:], in_=state["wb_g"][:])
 
-        def rope_table(part):
-            tiles = slice(PAIRS * part, PAIRS * (part + 1))
-            factors = keep.tile([P, PAIRS, 2, 2, HALF], BF16, name="factors%d" % part, align_bytes=64)
-            gpsimd_copy(factors[:, :, 1, 0, :], sin[:, tiles, 0:HALF], -1.0)
-            gpsimd_copy(
-                factors[:].rearrange("p i h w d -> p i (h w) d")[:, :, 0:4:3, :],
-                cos[:, tiles].rearrange("p i (h d) -> p i h d", h=2),
-            )
-            state["factors", part] = factors
-
-        def table_sin(part, copy):
-            tiles = slice(PAIRS * part, PAIRS * (part + 1))
-            copy(out=state["factors", part][:, :, 0, 1, :], in_=sin[:, tiles, HALF:])
+        def table_sign(part):
+            quarter = factors[part][:, :, 0, 1, :]
+            nc.vector.tensor_scalar(out=quarter, in0=quarter, scalar1=-1.0, scalar2=None, op0=MULT)
 
 
         def widen(n, j0=0, j1=2):
@@ -189,8 +207,9 @@ def tile_mla_model_t_kernel(
                 out=state["xw", n][:, j0 * H : j1 * H], in_=x_raw[:, (2 * n + j0) * H : (2 * n + j1) * H].bitcast(FP8)
             )
 
-        def turn_x(n, j):
-            xt = ps_x.tile([P, 2, 2, P], F32, name="xt")
+        def turn_x(n, j, xt=None):
+            if xt is None:
+                xt = ps_x.tile([P, 2, 2, P], F32, name="xt")
             words = state["xw", n][:, j * H : (j + 1) * H].bitcast(F32)
             for g in range(2):
                 for u in range(2):
@@ -199,8 +218,8 @@ def tile_mla_model_t_kernel(
 
         def scale_x(n, j):
             if j == 0:
-                if n in (1, 2):
-                    state["xg", n] = keep.tile([P, 2 * H], BF16, name="factors%d" % (n - 1), align_bytes=64)
+                if n == 1:
+                    state["xg", n] = keep.tile([P, 2 * H], BF16, name="wkv_g", align_bytes=64)
                 else:
                     state["xg", n] = work.tile([P, 2 * H], BF16, name="xg", bufs=2, align_bytes=64)
             nc.vector.tensor_tensor(
@@ -278,7 +297,7 @@ def tile_mla_model_t_kernel(
             state["ct", n, j] = ct
 
         def shared(n, shape, dtype):
-            return work.tile(shape, dtype, name="shared%d" % (n % 2), bufs=1, align_bytes=64)
+            return work.tile(shape, dtype, name="shared%d" % n, bufs=1, align_bytes=64)
 
         def empty_c(n, j0=0, j1=2, copy=nc.scalar.copy):
             if j0 == 0:
@@ -345,33 +364,22 @@ def tile_mla_model_t_kernel(
 
         def out_tile(n):
             if ("ot", n) not in state:
-                if n < PAIRS - ROPED_ON_VECTOR:
-                    state["ot", n] = work.tile([P, 2, 576], F32, name="ot", bufs=4)
-                else:
-                    state["ot", n] = work.tile([P, 2, OUT_W], F32, name="ot_last", bufs=ROPED_ON_VECTOR)
+                state["ot", n] = work.tile([P, 2, ROW], F32, name="ot", bufs=PAIRS)
             return state["ot", n]
 
-        def out_q(n):
-            q0 = 128 if n < PAIRS - ROPED_ON_VECTOR else 0
-            return out_tile(n)[:, :, q0 : q0 + 384].rearrange("p j (h c) -> p j h c", h=NH)
-
-        def out_kv(n):
-            kv0 = 0 if n < PAIRS - ROPED_ON_VECTOR else 384
-            return out_tile(n)[:, :, kv0 : kv0 + 128]
-
-        def copy_nope(n, j0=0, j1=2, copy=nc.scalar.copy):
-            copy(
-                out=out_q(n)[:, j0:j1, :, 0:DN],
+        def copy_nope(n, j0=0, j1=2):
+            nc.scalar.copy(
+                out=out_tile(n)[:, j0:j1, 128:512].rearrange("p j (h c) -> p j h c", h=NH)[:, :, :, 0:DN],
                 in_=state["pn", n, j0][:, j0:j1].rearrange("p j (h c) -> p j h c", h=NH),
             )
 
-        def copy_rope(n):
-            to_rope = work.tile([P, 2, 3 * DR], F32, name="to_rope", bufs=3)
-            nc.scalar.copy(out=to_rope[:], in_=state["pr", n, 0][:, :, 64:256])
-            state["to_rope", n] = to_rope
+        def copy_rope(n, j0=0, j1=2):
+            if ("to_rope", n) not in state:
+                state["to_rope", n] = work.tile([P, 2, 3 * DR], F32, name="to_rope", bufs=2)
+            nc.scalar.copy(out=state["to_rope", n][:, j0:j1], in_=state["pr", n, j0][:, j0:j1, 64:256])
 
-        def square_kv(n):
-            for j in range(2):
+        def square_kv(n, tiles=(0, 1)):
+            for j in tiles:
                 squares = work.tile([P, KVR], BF16, name="squares_kv", bufs=4)
                 nc.scalar.activation(
                     squares[:],
@@ -381,10 +389,10 @@ def tile_mla_model_t_kernel(
                     accum_out=stat("mean", n + 2)[:, 2 + j : 3 + j],
                 )
 
-        def norm_kv(n):
-            for j in range(2):
+        def norm_kv(n, tiles=(0, 1)):
+            for j in tiles:
                 nc.vector.scalar_tensor_tensor(
-                    out=out_kv(n)[:, j, 0:KVR],
+                    out=out_tile(n)[:, j, 0:KVR],
                     in0=state["pr", n, j][:, j, 0:KVR],
                     scalar=stat("rinv", n + 2)[:, 2 + j : 3 + j],
                     in1=gkv,
@@ -402,79 +410,76 @@ def tile_mla_model_t_kernel(
             )
             state["gained", n] = gained
 
-        def rope_products(n, engine, source, j0, j1):
-            shape = [P, j1 - j0, 3, 2, 2, HALF]
-            part, i = divmod(2 * n, PAIRS)
-            engine.tensor_tensor(
-                out=state["products", n][:, 3 * j0 : 3 * j1].rearrange("p (j s) h w d -> p j s h w d", s=3),
-                in0=source[:, j0:j1].rearrange("p j (s h d) -> p j s h d", s=3, h=2).unsqueeze(4).to_broadcast(shape),
-                in1=state["factors", part][:, i + j0 : i + j1].unsqueeze(2).to_broadcast(shape),
-                op=MULT,
-            )
-
-        def rope(n):
-            state["products", n] = shared(n + 1, [P, 6, 2, 2, HALF], F32)
-            rope_products(n, nc.gpsimd, state["to_rope", n][:], 0, 2)
+        def finish_kv(n):
+            state["ckv", n] = shared(n + 1, [P, 2, KVR], F32)
             nc.gpsimd.tensor_tensor(
-                out=out_kv(n)[:, :, 0:KVR],
+                out=state["ckv", n][:],
                 in0=state["gained", n][:],
                 in1=stat("rinv", n + 2)[:, 2:4].unsqueeze(2).to_broadcast([P, 2, KVR]),
                 op=MULT,
             )
-            halves = state["products", n][:].rearrange("p s h w d -> p s h (w d)")
-            nc.gpsimd.tensor_tensor(
-                out=out_tile(n)[:].rearrange("p j (s c) -> p (j s) c", c=DN + DR)[:, :, 64:128],
-                in0=halves[:, :, 0, :],
-                in1=halves[:, :, 1, :],
-                op=ADD,
+
+        def rope_products(n, engine, source, j0, j1):
+            if ("products", n) not in state:
+                state["products", n] = work.tile([P, 6, 2, 2, HALF], F32, name="products", bufs=2)
+            shape = [P, j1 - j0, 3, 2, DR]
+            part, i = divmod(2 * n, PAIRS)
+            engine.tensor_tensor(
+                out=state["products", n][:, 3 * j0 : 3 * j1].rearrange("p (j s) w h d -> p j s w (h d)", s=3),
+                in0=source[:, j0:j1].rearrange("p j (s c) -> p j s c", s=3).unsqueeze(3).to_broadcast(shape),
+                in1=factors[part][:, i + j0 : i + j1]
+                .rearrange("p j w h d -> p j w (h d)")
+                .unsqueeze(2)
+                .to_broadcast(shape),
+                op=MULT,
             )
 
-        def products_from_psum(n, j):
-            if j == 0:
-                state["products", n] = work.tile([P, 6, 2, 2, HALF], F32, name="products", bufs=ROPED_ON_VECTOR)
+        def products_gpsimd(n, j0=0, j1=2):
+            rope_products(n, nc.gpsimd, state["to_rope", n][:], j0, j1)
+
+        def products_vector(n, j):
             rope_products(n, nc.vector, state["pr", n, j][:, :, 64:256], j, j + 1)
 
-        def add_on_vector(n, j0=0, j1=2):
-            halves = state["products", n][:].rearrange("p (j s) h w d -> p j s h (w d)", j=2)[:, j0:j1]
-            nc.vector.tensor_tensor(
-                out=out_kv(n)[:, j0:j1, KVR:], in0=halves[:, :, 0, 0, :], in1=halves[:, :, 0, 1, :], op=ADD
+        def rope_sum(n, engine, j0=0, j1=2):
+            terms = state["products", n][:, 3 * j0 : 3 * j1]
+            groups = out_tile(n)[:].rearrange("p j (s c) -> p (j s) c", c=HEAD)[:, 3 * j0 : 3 * j1, 64:128]
+            engine.tensor_tensor(
+                out=groups.rearrange("p s (w d) -> p s w d", w=2), in0=terms[:, :, :, 0, :], in1=terms[:, :, :, 1, :], op=ADD
             )
-            nc.vector.tensor_tensor(
-                out=out_q(n)[:, j0:j1, :, DN:], in0=halves[:, :, 1:, 0, :], in1=halves[:, :, 1:, 1, :], op=ADD
-            )
+
+        def store_q(n, j0=0, j1=2):
+            nc.sync.dma_start(out=out_hbm[:, 2 * n + j0 : 2 * n + j1, 0:384], in_=out_tile(n)[:, j0:j1, 128:512])
+
+        def store_kv(n, j0=0, j1=2):
+            nc.sync.dma_start(out=out_hbm[:, 2 * n + j0 : 2 * n + j1, 384:512], in_=out_tile(n)[:, j0:j1, 0:128])
 
         def store(n):
-            ot = out_tile(n)
-            nc.sync.dma_start(out=out_hbm[:, 2 * n : 2 * n + 2, 0:384], in_=ot[:, :, 128:512])
-            nc.sync.dma_start(out=out_hbm[:, 2 * n : 2 * n + 2, 384:512], in_=ot[:, :, 0:128])
-
-        def store_rows(n, j0=0, j1=2):
-            nc.sync.dma_start(out=out_hbm[:, 2 * n + j0 : 2 * n + j1, :], in_=out_tile(n)[:, j0:j1, :])
+            nc.sync.dma_start(out=out_hbm[:, 2 * n : 2 * n + 2, 384:448], in_=state["ckv", n][:])
+            nc.sync.dma_start(out=out_hbm[:, 2 * n : 2 * n + 2, 448:512], in_=out_tile(n)[:, :, 64:128])
+            store_q(n)
 
         def rms_step(n):
             inverse_rms(n, 0, 4 if n >= 2 else 2)
 
-        def second_table(n):
+        def late_sign(n):
             if n == 0:
-                rope_table(1)
-
-        def second_table_sin(n):
-            if n == 0:
-                table_sin(1, nc.vector.tensor_copy)
+                table_sign(1)
 
         step = (
-            (second_table_sin, 4),
+            (late_sign, 7),
             (quant_c, 3),
             (quant_x, 1),
             (square_kv, 3),
             (rms_step, 2),
-            (rope, 4),
-            (second_table, 3),
+            (finish_kv, 4),
+            (lambda n: rope_sum(n, nc.gpsimd), 4),
+            (store, 4),
             (mm_rope, 3),
             (mm_nope, 3),
             (lambda n: mm_a(n, 0), 1),
             (widen, -1),
             (copy_rope, 3),
+            (products_gpsimd, 3),
             (copy_nope, 3),
             (lambda n: norm_a(n, 0), 2),
             (lambda n: norm_a(n, 1), 2),
@@ -488,7 +493,6 @@ def tile_mla_model_t_kernel(
             (mm_kv, 2),
             (lambda n: turn_x(n, 0), -1),
             (lambda n: scale_x(n, 1), 0),
-            (store, 4),
             (empty_c, 2),
             (lambda n: square_a(n, 1), 1),
         )
@@ -497,145 +501,158 @@ def tile_mla_model_t_kernel(
         turn_x(0, 0)
         widen(0, 1, 2)
         turn_x(0, 1)
-        wa_copy(0, nc.vector.tensor_copy)
-        wa_copy(1, nc.scalar.copy)
-        wa_copy(2, nc.scalar.copy)
-        wa_copy_gpsimd(3)
-        scale_x(0, 0)
         widen(1, 0, 1)
-        turn_x(1, 0)
-        scale_x(0, 1)
+        turn_x(1, 0, ps_a.tile([P, 2, 2, P], F32, name="pa"))
         widen(1, 1, 2)
-        turn_x(1, 1)
+        turn_x(1, 1, ps_a.tile([P, 2, 2, P], F32, name="pa"))
+        scale_x(0, 0)
+        wa_copy(0, 0, 64)
+        wa_copy_gpsimd(0, 64, 128)
+        wa_copy(1, 0, 128)
+        scale_x(0, 1)
+        scale_x(1, 0)
         wa_quant(0)
         quant_x(0)
         wa_quant(1)
-        widen(2)
-        wkv_copy()
-        wb_copy()
         gamma_turn()
-        mm_a(0, 0)
-        scale_x(1, 0)
+        widen(2, 0, 1)
         turn_x(2, 0)
-        mm_a(0, 1)
+        gamma_copy()
+        widen(2, 1, 2)
+        widen(3, 0, 1)
+        wb_copy_gpsimd()
+        wb_copy(True)
+        wb_copy(False)
+        widen(3, 1, 2)
+        mm_a(0, 0)
         scale_x(1, 1)
+        mm_a(0, 1)
         turn_x(2, 1)
-        wkv_quant()
+        scale_x(2, 0)
+        wb_quant()
         quant_x(1)
         square_a(0, 0)
-        gamma_copy()
+        wkv_copy_gpsimd()
         inverse_rms(0, 0, 1)
-        rope_table(0)
-        widen(3, 0, 1)
         square_a(0, 1)
-        widen(3, 1, 2)
         inverse_rms(0, 1, 2)
+        wkv_copy()
+        widen(4, 0, 1)
         mm_a(1, 0)
         norm_a(0, 0)
-        turn_c(0, 0)
-        scale_x(2, 0)
         norm_a(0, 1)
         square_a(1, 0)
-        table_sin(0, nc.scalar.copy)
+        turn_c(0, 0)
         turn_c(0, 1)
         mm_a(1, 1)
-        mm_kv(0)
         turn_x(3, 0)
         scale_x(2, 1)
         empty_c(0)
         square_a(1, 1)
-        wb_quant()
+        wkv_quant()
+        quant_c(0)
+        quant_x(2)
+        rms_step(1)
+        widen(4, 1, 2)
+        mm_kv(0)
+        mm_rope(0)
+        mm_nope(0)
+        mm_a(2, 0)
+        copy_rope(0)
+        norm_a(1, 0)
+        table_sign(0)
+        products_gpsimd(0)
+        square_kv(0)
+        copy_nope(0)
+        norm_a(1, 1)
+        turn_x(3, 1)
+        square_a(2, 0)
+        turn_c(1, 0)
+        turn_c(1, 1)
+        mm_a(2, 1)
+        scale_x(3, 0)
+        gain_kv(0)
+        mm_kv(1)
+        turn_x(4, 0)
+        scale_x(3, 1)
+        empty_c(1)
+        square_a(2, 1)
 
-        for s in range(3, PAIRS - 1):
+        for s in range(4, PAIRS):
             for stage, lag in step:
                 if 0 <= s - lag < PAIRS:
                     stage(s - lag)
 
         a, b, c, d = range(PAIRS - 4, PAIRS)
-        quant_c(a)
-        quant_x(c)
-        square_kv(a)
-        rms_step(b)
-        rope(a - 1)
-        mm_rope(a)
-        mm_nope(a)
-        mm_a(c, 0)
-        copy_rope(a)
-        copy_nope(a)
-        norm_a(b, 0)
-        norm_a(b, 1)
-        turn_x(d, 1)
-        square_a(c, 0)
-        turn_c(b, 0)
-        turn_c(b, 1)
-        mm_a(c, 1)
-        scale_x(d, 0)
-        gain_kv(a)
-        mm_kv(b)
         mm_kv(c, (0, 1), spare_bank([P, 2, 256]))
-        scale_x(d, 1)
-        store(a - 1)
-        empty_c(b)
-        square_a(c, 1)
-        square_kv(b)
         quant_c(b)
         quant_x(d)
+        square_kv(b)
         rms_step(c)
         square_kv(c)
         inverse_rms(d, 2, 4)
-        rope(a)
+        finish_kv(a)
+        rope_sum(a, nc.gpsimd)
         store(a)
-        mm_a(d, 0)
-        norm_a(c, 0)
-        mm_a(d, 1, spare_bank([P, QR]))
-        norm_kv(b)
-        norm_a(c, 1)
         mm_rope(b)
+        mm_nope(b)
+        mm_a(d, 0)
+        mm_a(d, 1, spare_bank([P, QR]))
         inverse_rms(d + 1, 2, 4)
-        square_a(d, 0)
-        square_a(d, 1)
+        copy_nope(b)
+        norm_a(c, 0)
+        norm_a(c, 1)
         turn_c(c, 0)
         turn_c(c, 1)
         mm_kv(d, (0,), ps_a.tile([P, 2, 256], F32, name="pa"))
         mm_kv(d, (1,), ps_a.tile([P, 2, 256], F32, name="pa"))
-        mm_nope(b)
-        norm_kv(c)
-        products_from_psum(b, 0)
-        products_from_psum(b, 1)
+        products_vector(b, 0)
+        products_vector(b, 1)
+        norm_kv(b)
+        rope_sum(b, nc.gpsimd)
+        store_kv(b)
+        store_q(b)
+        square_a(d, 0)
+        square_a(d, 1)
         inverse_rms(d, 0, 1)
+        square_kv(d, (0,))
         inverse_rms(d, 1, 2)
-        empty_c(c)
-        square_kv(d)
+        square_kv(d, (1,))
+        empty_c(c, 0, 2, nc.vector.tensor_copy)
         norm_a(d, 0)
-        norm_a(d, 1)
         quant_c(c)
-        copy_nope(b)
-        inverse_rms(d + 2, 2, 4)
+        norm_a(d, 1)
         turn_c(d, 0)
-        turn_c(d, 1, ps_r.tile([P, 2, 2, P], F32, name="pr"))
-        add_on_vector(b)
-        store_rows(b)
         mm_rope(c)
-        mm_nope(c, (0, 1), ps_a.tile([P, 2, 256], F32, name="pa"))
+        mm_nope(c)
+        turn_c(d, 1, ps_r.tile([P, 2, 2, P], F32, name="pr"))
+        inverse_rms(d + 2, 2, 4)
         empty_c(d, 0, 1)
+        copy_nope(c, 0, 1)
         empty_c(d, 1, 2)
-        copy_nope(c)
-        norm_kv(d)
+        copy_nope(c, 1, 2)
+        products_vector(c, 0)
         quant_c(d, 0, 1)
-        mm_rope(d, (0,))
-        mm_nope(d, (0,))
-        products_from_psum(c, 0)
+        norm_kv(c)
+        rope_sum(c, nc.vector, 0, 1)
+        store_q(c, 0, 1)
+        products_vector(c, 1)
         quant_c(d, 1, 2)
+        mm_rope(d, (0,))
+        mm_nope(d, (0,), ps_a.tile([P, 2, 256], F32, name="pa"))
         mm_rope(d, (1,))
         mm_nope(d, (1,), ps_c.tile([P, 2, 256], F32, name="ct"))
-        products_from_psum(c, 1)
-        products_from_psum(d, 0)
-        add_on_vector(c)
-        store_rows(c)
-        products_from_psum(d, 1)
+        norm_kv(d, (0,))
+        rope_sum(c, nc.vector, 1, 2)
+        store_q(c, 1, 2)
+        store_kv(c)
+        products_vector(d, 0)
+        products_vector(d, 1)
         copy_nope(d, 0, 1)
         copy_nope(d, 1, 2)
-        add_on_vector(d, 0, 1)
-        store_rows(d, 0, 1)
-        add_on_vector(d, 1, 2)
-        store_rows(d, 1, 2)
+        rope_sum(d, nc.vector, 0, 1)
+        store_q(d, 0, 1)
+        norm_kv(d, (1,))
+        rope_sum(d, nc.vector, 1, 2)
+        store_q(d, 1, 2)
+        store_kv(d)

@@ -17,7 +17,7 @@ N_TILES = T // P
 PAIRS = N_TILES // 2
 
 WB_ON_GPSIMD = 96
-WKV_ON_GPSIMD = 96
+WKV_ON_GPSIMD = 128
 
 F32 = mybir.dt.float32
 BF16 = mybir.dt.bfloat16
@@ -63,7 +63,6 @@ def tile_mla_model_t_kernel(
         one = keep.tile([P, 1], F32, name="one")
         eps = keep.tile([P, 1], F32, name="eps")
 
-        wa_g = keep.tile([P, 2 * QR * 4], BF16, name="grouped", align_bytes=64)
         wa_c = keep.tile([P, 2, QR], U32, name="wa_c", align_bytes=64)
         wa_s = keep.tile([P, 2, QR], U8, name="wa_s", align_bytes=64)
         wkv_c = keep.tile([P, 2, 128], U32, name="wkv_c", align_bytes=64)
@@ -98,11 +97,12 @@ def tile_mla_model_t_kernel(
         nc.vector.memset(gkv_col[:], 0.0)
 
         load_x(0, 1)
+        load_wa(0)
         nc.sync.dma_start(out=scale[:], in_=x_scale.rearrange("o (g p t) -> p (o g) t", g=2, t=4))
         load_x(1, 2)
-        load_x(2, 4)
-        load_wa(0)
+        load_x(2, 3)
         load_wa(1)
+        load_x(3, 4)
         load_x(4, 6)
         nc.sync.dma_start(out=gq_col[:], in_=gamma_cq.rearrange("(p t) -> p t", t=4))
         nc.sync.dma_start(out=gkv_col[0:32, :], in_=gamma_ckv.rearrange("(p e) -> p e", e=2))
@@ -125,24 +125,27 @@ def tile_mla_model_t_kernel(
         def gpsimd_copy(out, in_, sign=1.0):
             nc.gpsimd.tensor_scalar(out=out, in0=in_, scalar1=sign, scalar2=0.0, op0=MULT, op1=ADD)
 
-        wa_grouped = wa_g[:].rearrange("p (g u m e j) -> p g u m e j", g=2, u=2, e=2, j=4)
+        def wa_grouped(g):
+            if ("wa_g", g) not in state:
+                state["wa_g", g] = keep.tile([P, QR * 4], BF16, name="grouped", align_bytes=64)
+            return state["wa_g", g][:].rearrange("p (u m e j) -> p u m e j", u=2, e=2, j=4)
 
-        def wa_copy(g, m0, m1):
-            nc.scalar.copy(
-                out=wa_grouped[:, g, :, m0:m1].rearrange("p u m e j -> p m j u e"),
+        def wa_copy(g, m0, m1, copy=nc.scalar.copy):
+            copy(
+                out=wa_grouped(g)[:, :, m0:m1].rearrange("p u m e j -> p m j u e"),
                 in_=wa_raw[g][:, :, 4 * m0 : 4 * m1].rearrange("p j (m u e) -> p m j u e", u=2, e=2),
             )
 
         def wa_copy_gpsimd(g, m0, m1):
             for u in range(2):
                 gpsimd_copy(
-                    wa_grouped[:, g, u, m0:m1],
+                    wa_grouped(g)[:, u, m0:m1],
                     wa_raw[g][:, :, 4 * m0 : 4 * m1].rearrange("p j (m u e) -> p u m e j", u=2, e=2)[:, u],
                 )
 
         def wa_quant(g):
             nc.vector.quantize_mx(
-                out=wa_c[:, g, :].bitcast(FP8X4), scales=wa_s[:, g, :], in_=wa_g[:, g * 2048 : (g + 1) * 2048]
+                out=wa_c[:, g, :].bitcast(FP8X4), scales=wa_s[:, g, :], in_=state["wa_g", g][:]
             )
 
         def gamma_turn():
@@ -261,7 +264,7 @@ def tile_mla_model_t_kernel(
 
         def stat(kind, n):
             if (kind, n) not in state:
-                state[kind, n] = work.tile([P, 4], F32, name=kind, bufs=4)
+                state[kind, n] = work.tile([P, 4], F32, name=kind, bufs=PAIRS + 2)
             return state[kind, n]
 
         def square_a(n, j):
@@ -373,10 +376,13 @@ def tile_mla_model_t_kernel(
                 in_=state["pn", n, j0][:, j0:j1].rearrange("p j (h c) -> p j h c", h=NH),
             )
 
-        def copy_rope(n, j0=0, j1=2):
-            if ("to_rope", n) not in state:
-                state["to_rope", n] = work.tile([P, 2, 3 * DR], F32, name="to_rope", bufs=2)
-            nc.scalar.copy(out=state["to_rope", n][:, j0:j1], in_=state["pr", n, j0][:, j0:j1, 64:256])
+        def roped_groups(n, j0, j1):
+            return out_tile(n)[:].rearrange("p j (s c) -> p j s c", c=HEAD)[:, j0:j1, :, 64:128]
+
+        def copy_rope(n):
+            nc.scalar.copy(
+                out=roped_groups(n, 0, 2), in_=state["pr", n, 0][:, :, 64:256].rearrange("p j (s c) -> p j s c", s=3)
+            )
 
         def square_kv(n, tiles=(0, 1)):
             for j in tiles:
@@ -400,21 +406,32 @@ def tile_mla_model_t_kernel(
                     op1=MULT,
                 )
 
+        def scale_kv(n):
+            for j in range(2):
+                nc.scalar.activation(
+                    out_tile(n)[:, j, 0:KVR],
+                    state["pr", n, j][:, j, 0:KVR],
+                    ACT.Copy,
+                    scale=stat("rinv", n + 2)[:, 2 + j : 3 + j],
+                )
+
+        def gain_kv_gpsimd(n):
+            ckv = out_tile(n)[:, :, 0:KVR]
+            nc.gpsimd.tensor_tensor(out=ckv, in0=ckv, in1=gkv.unsqueeze(1).to_broadcast([P, 2, KVR]), op=MULT)
+
         def gain_kv(n):
-            gained = work.tile([P, 2, KVR], F32, name="gained", bufs=2)
             nc.vector.tensor_tensor(
-                out=gained[:],
+                out=out_tile(n)[:, :, 0:KVR],
                 in0=state["pr", n, 0][:, :, 0:KVR],
                 in1=gkv.unsqueeze(1).to_broadcast([P, 2, KVR]),
                 op=MULT,
             )
-            state["gained", n] = gained
 
         def finish_kv(n):
             state["ckv", n] = shared(n + 1, [P, 2, KVR], F32)
             nc.gpsimd.tensor_tensor(
                 out=state["ckv", n][:],
-                in0=state["gained", n][:],
+                in0=out_tile(n)[:, :, 0:KVR],
                 in1=stat("rinv", n + 2)[:, 2:4].unsqueeze(2).to_broadcast([P, 2, KVR]),
                 op=MULT,
             )
@@ -426,7 +443,7 @@ def tile_mla_model_t_kernel(
             part, i = divmod(2 * n, PAIRS)
             engine.tensor_tensor(
                 out=state["products", n][:, 3 * j0 : 3 * j1].rearrange("p (j s) w h d -> p j s w (h d)", s=3),
-                in0=source[:, j0:j1].rearrange("p j (s c) -> p j s c", s=3).unsqueeze(3).to_broadcast(shape),
+                in0=source.unsqueeze(3).to_broadcast(shape),
                 in1=factors[part][:, i + j0 : i + j1]
                 .rearrange("p j w h d -> p j w (h d)")
                 .unsqueeze(2)
@@ -434,17 +451,20 @@ def tile_mla_model_t_kernel(
                 op=MULT,
             )
 
-        def products_gpsimd(n, j0=0, j1=2):
-            rope_products(n, nc.gpsimd, state["to_rope", n][:], j0, j1)
+        def products_gpsimd(n):
+            rope_products(n, nc.gpsimd, roped_groups(n, 0, 2), 0, 2)
 
         def products_vector(n, j):
-            rope_products(n, nc.vector, state["pr", n, j][:, :, 64:256], j, j + 1)
+            source = state["pr", n, j][:, j : j + 1, 64:256].rearrange("p j (s c) -> p j s c", s=3)
+            rope_products(n, nc.vector, source, j, j + 1)
 
         def rope_sum(n, engine, j0=0, j1=2):
             terms = state["products", n][:, 3 * j0 : 3 * j1]
-            groups = out_tile(n)[:].rearrange("p j (s c) -> p (j s) c", c=HEAD)[:, 3 * j0 : 3 * j1, 64:128]
             engine.tensor_tensor(
-                out=groups.rearrange("p s (w d) -> p s w d", w=2), in0=terms[:, :, :, 0, :], in1=terms[:, :, :, 1, :], op=ADD
+                out=roped_groups(n, j0, j1).rearrange("p j s (w d) -> p (j s) w d", w=2),
+                in0=terms[:, :, :, 0, :],
+                in1=terms[:, :, :, 1, :],
+                op=ADD,
             )
 
         def store_q(n, j0=0, j1=2):
@@ -499,6 +519,8 @@ def tile_mla_model_t_kernel(
 
         widen(0, 0, 1)
         turn_x(0, 0)
+        wa_copy(0, 0, 96, nc.vector.tensor_copy)
+        wa_copy(0, 96, 128)
         widen(0, 1, 2)
         turn_x(0, 1)
         widen(1, 0, 1)
@@ -506,12 +528,11 @@ def tile_mla_model_t_kernel(
         widen(1, 1, 2)
         turn_x(1, 1, ps_a.tile([P, 2, 2, P], F32, name="pa"))
         scale_x(0, 0)
-        wa_copy(0, 0, 64)
-        wa_copy_gpsimd(0, 64, 128)
-        wa_copy(1, 0, 128)
+        wa_quant(0)
+        wa_copy(1, 0, 72)
+        wa_copy_gpsimd(1, 72, 128)
         scale_x(0, 1)
         scale_x(1, 0)
-        wa_quant(0)
         quant_x(0)
         wa_quant(1)
         gamma_turn()
@@ -523,20 +544,18 @@ def tile_mla_model_t_kernel(
         wb_copy_gpsimd()
         wb_copy(True)
         wb_copy(False)
-        widen(3, 1, 2)
         mm_a(0, 0)
         scale_x(1, 1)
         mm_a(0, 1)
         turn_x(2, 1)
         scale_x(2, 0)
-        wb_quant()
         quant_x(1)
         square_a(0, 0)
         wkv_copy_gpsimd()
         inverse_rms(0, 0, 1)
         square_a(0, 1)
         inverse_rms(0, 1, 2)
-        wkv_copy()
+        widen(3, 1, 2)
         widen(4, 0, 1)
         mm_a(1, 0)
         norm_a(0, 0)
@@ -549,6 +568,7 @@ def tile_mla_model_t_kernel(
         scale_x(2, 1)
         empty_c(0)
         square_a(1, 1)
+        wb_quant()
         wkv_quant()
         quant_c(0)
         quant_x(2)

@@ -353,9 +353,10 @@ def tile_mla_model_t_kernel(
                 stop=True,
             )
 
-        def mm_rope(n, tiles=(0, 1)):
+        def mm_rope(n, tiles=(0, 1), own_bank=None):
             for j in tiles:
-                mm_q(n, j, state["pr", n, j][:, j, 128:256], 256, 384)
+                state["pq", n, j] = state["pr", n, j] if own_bank is None else own_bank
+                mm_q(n, j, state["pq", n, j][:, j, 128:256], 256, 384)
 
         def mm_nope(n, tiles=(0, 1), pn=None):
             if pn is None:
@@ -436,13 +437,13 @@ def tile_mla_model_t_kernel(
                 op=MULT,
             )
 
-        def rope_products(n, engine, source, j0, j1):
+        def rope_products(n, engine, source, j0, j1, s0=0, s1=3):
             if ("products", n) not in state:
-                state["products", n] = work.tile([P, 6, 2, 2, HALF], F32, name="products", bufs=2)
-            shape = [P, j1 - j0, 3, 2, DR]
+                state["products", n] = work.tile([P, 2, 3, 2, 2, HALF], F32, name="products", bufs=3)
+            shape = [P, j1 - j0, s1 - s0, 2, DR]
             part, i = divmod(2 * n, PAIRS)
             engine.tensor_tensor(
-                out=state["products", n][:, 3 * j0 : 3 * j1].rearrange("p (j s) w h d -> p j s w (h d)", s=3),
+                out=state["products", n][:, j0:j1, s0:s1].rearrange("p j s w h d -> p j s w (h d)"),
                 in0=source.unsqueeze(3).to_broadcast(shape),
                 in1=factors[part][:, i + j0 : i + j1]
                 .rearrange("p j w h d -> p j w (h d)")
@@ -458,14 +459,27 @@ def tile_mla_model_t_kernel(
             source = state["pr", n, j][:, j : j + 1, 64:256].rearrange("p j (s c) -> p j s c", s=3)
             rope_products(n, nc.vector, source, j, j + 1)
 
-        def rope_sum(n, engine, j0=0, j1=2):
-            terms = state["products", n][:, 3 * j0 : 3 * j1]
+        def products_k(n):
+            rope_products(n, nc.vector, state["pr", n, 0][:, :, 64:128].unsqueeze(2), 0, 2, 0, 1)
+
+        def products_q(n, j):
+            source = state["pq", n, j][:, j : j + 1, 128:256].rearrange("p j (s c) -> p j s c", s=NH)
+            rope_products(n, nc.vector, source, j, j + 1, 1, 3)
+
+        def rope_sum(n, engine, j0=0, j1=2, s0=0, s1=3):
+            terms = state["products", n][:, j0:j1, s0:s1].rearrange("p j s w h d -> p (j s) w h d")
             engine.tensor_tensor(
-                out=roped_groups(n, j0, j1).rearrange("p j s (w d) -> p (j s) w d", w=2),
+                out=roped_groups(n, j0, j1)[:, :, s0:s1].rearrange("p j s (w d) -> p (j s) w d", w=2),
                 in0=terms[:, :, :, 0, :],
                 in1=terms[:, :, :, 1, :],
                 op=ADD,
             )
+
+        def sum_k(n):
+            rope_sum(n, nc.vector, 0, 2, 0, 1)
+
+        def sum_q(n, j):
+            rope_sum(n, nc.vector, j, j + 1, 1, 3)
 
         def store_q(n, j0=0, j1=2):
             nc.sync.dma_start(out=out_hbm[:, 2 * n + j0 : 2 * n + j1, 0:384], in_=out_tile(n)[:, j0:j1, 128:512])
@@ -624,21 +638,21 @@ def tile_mla_model_t_kernel(
         norm_a(c, 1)
         turn_c(c, 0)
         turn_c(c, 1)
-        mm_kv(d, (0,), ps_a.tile([P, 2, 256], F32, name="pa"))
-        mm_kv(d, (1,), ps_a.tile([P, 2, 256], F32, name="pa"))
+        mm_kv(d, (0, 1), ps_a.tile([P, 2, 256], F32, name="pa"))
         products_vector(b, 0)
         products_vector(b, 1)
         norm_kv(b)
         rope_sum(b, nc.gpsimd)
         store_kv(b)
         store_q(b)
+        products_k(c)
+        norm_kv(c)
         square_a(d, 0)
         square_a(d, 1)
         inverse_rms(d, 0, 1)
-        square_kv(d, (0,))
+        empty_c(c)
         inverse_rms(d, 1, 2)
-        square_kv(d, (1,))
-        empty_c(c, 0, 2, nc.vector.tensor_copy)
+        square_kv(d)
         norm_a(d, 0)
         quant_c(c)
         norm_a(d, 1)
@@ -646,33 +660,34 @@ def tile_mla_model_t_kernel(
         mm_rope(c)
         mm_nope(c)
         turn_c(d, 1, ps_r.tile([P, 2, 2, P], F32, name="pr"))
-        inverse_rms(d + 2, 2, 4)
         empty_c(d, 0, 1)
+        inverse_rms(d + 2, 2, 4)
         copy_nope(c, 0, 1)
         empty_c(d, 1, 2)
         copy_nope(c, 1, 2)
-        products_vector(c, 0)
+        products_k(d)
+        products_q(c, 0)
         quant_c(d, 0, 1)
-        norm_kv(c)
-        rope_sum(c, nc.vector, 0, 1)
-        store_q(c, 0, 1)
-        products_vector(c, 1)
-        quant_c(d, 1, 2)
-        mm_rope(d, (0,))
-        mm_nope(d, (0,), ps_a.tile([P, 2, 256], F32, name="pa"))
-        mm_rope(d, (1,))
-        mm_nope(d, (1,), ps_c.tile([P, 2, 256], F32, name="ct"))
-        norm_kv(d, (0,))
-        rope_sum(c, nc.vector, 1, 2)
-        store_q(c, 1, 2)
+        sum_k(c)
         store_kv(c)
-        products_vector(d, 0)
-        products_vector(d, 1)
+        sum_q(c, 0)
+        store_q(c, 0, 1)
+        products_q(c, 1)
+        quant_c(d, 1, 2)
+        mm_rope(d, (0,), ps_a.tile([P, 2, 256], F32, name="pa"))
+        mm_nope(d, (0,), ps_a.tile([P, 2, 256], F32, name="pa"))
+        mm_rope(d, (1,), spare_bank([P, 2, 256]))
+        mm_nope(d, (1,), ps_c.tile([P, 2, 256], F32, name="ct"))
+        norm_kv(d)
+        sum_q(c, 1)
+        store_q(c, 1, 2)
+        sum_k(d)
+        store_kv(d)
+        products_q(d, 0)
+        products_q(d, 1)
         copy_nope(d, 0, 1)
         copy_nope(d, 1, 2)
-        rope_sum(d, nc.vector, 0, 1)
+        sum_q(d, 0)
         store_q(d, 0, 1)
-        norm_kv(d, (1,))
-        rope_sum(d, nc.vector, 1, 2)
+        sum_q(d, 1)
         store_q(d, 1, 2)
-        store_kv(d)

@@ -235,11 +235,16 @@ def tile_mla_model_t_kernel(
                 op=MULT,
             )
 
-        def quant_x(n):
-            xc = work.tile([P, 512], U32, name="xc", bufs=4, align_bytes=64)
-            xsc = work.tile([P, 512], U8, name="xsc", bufs=4, align_bytes=64)
-            nc.vector.quantize_mx(out=xc[:].bitcast(FP8X4), scales=xsc[:], in_=state["xg", n][:])
-            state["xc", n] = (xc, xsc)
+        def quant_x(n, j0=0, j1=2):
+            if j0 == 0:
+                xc = work.tile([P, 512], U32, name="xc", bufs=4, align_bytes=64)
+                xsc = work.tile([P, 512], U8, name="xsc", bufs=4, align_bytes=64)
+                state["xc", n] = (xc, xsc)
+            xc, xsc = state["xc", n]
+            cols = slice(j0 * 256, j1 * 256)
+            nc.vector.quantize_mx(
+                out=xc[:, cols].bitcast(FP8X4), scales=xsc[:, cols], in_=state["xg", n][:, j0 * H : j1 * H]
+            )
 
 
         def spare_bank(shape):
@@ -620,7 +625,8 @@ def tile_mla_model_t_kernel(
         a, b, c, d = range(PAIRS - 4, PAIRS)
         mm_kv(c, (0, 1), spare_bank([P, 2, 256]))
         quant_c(b)
-        quant_x(d)
+        quant_x(d, 0, 1)
+        quant_x(d, 1, 2)
         square_kv(b)
         rms_step(c)
         square_kv(c)
@@ -629,64 +635,66 @@ def tile_mla_model_t_kernel(
         rope_sum(a, nc.gpsimd)
         store(a)
         mm_rope(b)
-        mm_nope(b)
         mm_a(d, 0)
         mm_a(d, 1, spare_bank([P, QR]))
         inverse_rms(d + 1, 2, 4)
-        copy_nope(b)
+        scale_kv(c)
+        gain_kv_gpsimd(c)
         norm_a(c, 0)
         norm_a(c, 1)
         turn_c(c, 0)
         turn_c(c, 1)
         mm_kv(d, (0, 1), ps_a.tile([P, 2, 256], F32, name="pa"))
+        mm_nope(b)
         products_vector(b, 0)
         products_vector(b, 1)
-        norm_kv(b)
         rope_sum(b, nc.gpsimd)
+        norm_kv(b)
         store_kv(b)
-        store_q(b)
         products_k(c)
-        norm_kv(c)
         square_a(d, 0)
         square_a(d, 1)
         inverse_rms(d, 0, 1)
         empty_c(c)
         inverse_rms(d, 1, 2)
+        copy_nope(b)
+        store_q(b)
         square_kv(d)
         norm_a(d, 0)
-        quant_c(c)
         norm_a(d, 1)
+        quant_c(c)
         turn_c(d, 0)
-        mm_rope(c)
-        mm_nope(c)
         turn_c(d, 1, ps_r.tile([P, 2, 2, P], F32, name="pr"))
-        empty_c(d, 0, 1)
+        mm_rope(c)
+        mm_nope(c, (0,))
+        mm_nope(c, (1,), ps_a.tile([P, 2, 256], F32, name="pa"))
         inverse_rms(d + 2, 2, 4)
-        copy_nope(c, 0, 1)
+        empty_c(d, 0, 1)
         empty_c(d, 1, 2)
+        copy_nope(c, 0, 1)
         copy_nope(c, 1, 2)
         products_k(d)
-        products_q(c, 0)
-        quant_c(d, 0, 1)
         sum_k(c)
         store_kv(c)
-        sum_q(c, 0)
-        store_q(c, 0, 1)
-        products_q(c, 1)
-        quant_c(d, 1, 2)
-        mm_rope(d, (0,), ps_a.tile([P, 2, 256], F32, name="pa"))
-        mm_nope(d, (0,), ps_a.tile([P, 2, 256], F32, name="pa"))
-        mm_rope(d, (1,), spare_bank([P, 2, 256]))
-        mm_nope(d, (1,), ps_c.tile([P, 2, 256], F32, name="ct"))
         norm_kv(d)
-        sum_q(c, 1)
-        store_q(c, 1, 2)
         sum_k(d)
         store_kv(d)
-        products_q(d, 0)
-        products_q(d, 1)
+        quant_c(d, 0, 1)
+        products_q(c, 0)
+        quant_c(d, 1, 2)
+        mm_rope(d, (0,), ps_a.tile([P, 2, 256], F32, name="pa"))
+        mm_nope(d, (0,), ps_c.tile([P, 2, 256], F32, name="ct"))
+        mm_rope(d, (1,), ps_n.tile([P, 2, 256], F32, name="pn"))
+        mm_nope(d, (1,), ps_r.tile([P, 2, 256], F32, name="pr"))
         copy_nope(d, 0, 1)
         copy_nope(d, 1, 2)
+        products_q(c, 1)
+        sum_q(c, 0)
+        store_q(c, 0, 1)
+        products_q(d, 0)
+        sum_q(c, 1)
+        store_q(c, 1, 2)
+        products_q(d, 1)
         sum_q(d, 0)
         store_q(d, 0, 1)
         sum_q(d, 1)

from contextlib import ExitStack

import concourse.mybir as mybir
from concourse.masks import make_identity

T, H, QR = 4096, 1024, 512
NH, DN, DR, KVR = 2, 128, 64, 64
HALF = DR // 2
EPS = 1e-6
HEAD = DN + DR
ROW = 3 * HEAD

FLOPS = 2 * T * (H * (QR + KVR + DR) + QR * NH * (DN + DR))

P = 128
N_TILES = T // P
PAIRS = N_TILES // 2

WB_ON_GPSIMD = 96
WKV_ON_GPSIMD = 128

F32 = mybir.dt.float32
BF16 = mybir.dt.bfloat16
U32 = mybir.dt.uint32
U8 = mybir.dt.uint8
FP8 = mybir.dt.float8_e4m3fn
FP8X4 = mybir.dt.float8_e4m3fn_x4
MULT = mybir.AluOpType.mult
ADD = mybir.AluOpType.add
ACT = mybir.ActivationFunctionType


def tile_mla_model_t_kernel(
    tc, x_bytes, x_scale, wq_a, wq_b, wkv, rope_cos, rope_sin, gamma_cq, gamma_ckv, out
):
    nc = tc.nc
    x_hbm = x_bytes.rearrange("(p i) k -> p i k", i=N_TILES)
    cos_hbm = rope_cos.rearrange("(p i) d -> p i d", i=N_TILES)
    sin_hbm = rope_sin.rearrange("(p i) d -> p i d", i=N_TILES)
    out_hbm = out.rearrange("(p i) c -> p i c", i=N_TILES)

    with ExitStack() as ctx:
        keep = ctx.enter_context(tc.tile_pool(name="keep", bufs=1))
        work = ctx.enter_context(tc.tile_pool(name="work", bufs=2))
        ps_x = ctx.enter_context(tc.psum_pool(name="ps_x", bufs=2))
        ps_a = ctx.enter_context(tc.psum_pool(name="ps_a", bufs=3))
        ps_c = ctx.enter_context(tc.psum_pool(name="ps_c", bufs=1))
        ps_n = ctx.enter_context(tc.psum_pool(name="ps_n", bufs=1))
        ps_r = ctx.enter_context(tc.psum_pool(name="ps_r", bufs=1))
        ctx.enter_context(tc.manual_schedule())

        x_raw = keep.tile([P, N_TILES * H], U8, name="x_raw")
        scale = keep.tile([P, 2, 4], F32, name="scale")
        wa_raw = [keep.tile([P, 4, QR], BF16, name="wa_raw%d" % g) for g in range(2)]
        wkv_raw = keep.tile([P, 2, 4, KVR + DR], BF16, name="wkv_raw")
        wb_raw = keep.tile([P, 4, NH * HEAD], BF16, name="wb_raw")
        gq_col = keep.tile([P, 4], BF16, name="gq_col")
        gkv_col = keep.tile([P, 2], BF16, name="gkv_col")
        gains = keep.tile([P, QR + KVR], BF16, name="gains")
        gq, gkv = gains[:, 0:QR], gains[:, QR:]
        factors = [keep.tile([P, PAIRS, 2, 2, HALF], BF16, name="factors%d" % part, align_bytes=64) for part in range(2)]
        ident = keep.tile([P, P], F32, name="ident")
        one = keep.tile([P, 1], F32, name="one")
        eps = keep.tile([P, 1], F32, name="eps")

        wa_c = keep.tile([P, 2, QR], U32, name="wa_c", align_bytes=64)
        wa_s = keep.tile([P, 2, QR], U8, name="wa_s", align_bytes=64)
        wkv_c = keep.tile([P, 2, 128], U32, name="wkv_c", align_bytes=64)
        wkv_s = keep.tile([P, 2, 128], U8, name="wkv_s", align_bytes=64)
        wb_c = keep.tile([P, 384], U32, name="wb_c", align_bytes=64)
        wb_s = keep.tile([P, 384], U8, name="wb_s", align_bytes=64)

        def load_x(i0, i1):
            nc.sync.dma_start(
                out=x_raw[:, i0 * H : i1 * H], in_=x_hbm[:, i0:i1, :].rearrange("p i k -> p (i k)")
            )

        def load_wa(g):
            nc.sync.dma_start(out=wa_raw[g][:], in_=wq_a.rearrange("(g p j) c -> g p j c", p=P, j=4)[g])

        def load_factors(part):
            tiles = slice(PAIRS * part, PAIRS * (part + 1))
            flat = factors[part][:].rearrange("p i w h d -> p (i w h d)")
            cos_flat = cos_hbm[:, tiles, :].rearrange("p i d -> p (i d)")
            nc.sync.dma_start(
                out=flat.rearrange("p (i c) -> p i c", i=PAIRS)[:, :, HALF : 3 * HALF], in_=sin_hbm[:, tiles, :]
            )
            nc.sync.dma_start(
                out=flat[:, 3 * HALF : 3 * HALF + (PAIRS - 1) * 2 * DR].rearrange("p (i c) -> p i c", c=2 * DR)[:, :, 0:DR],
                in_=cos_flat[:, HALF : HALF + (PAIRS - 1) * DR].rearrange("p (i c) -> p i c", c=DR),
            )
            nc.sync.dma_start(
                out=flat.rearrange("p (c d) -> p c d", d=HALF)[:, 0 : 4 * PAIRS : 4 * PAIRS - 1],
                in_=cos_flat.rearrange("p (c d) -> p c d", d=HALF)[:, 0 : 2 * PAIRS : 2 * PAIRS - 1],
            )

        nc.vector.memset(gkv_col[:], 0.0)

        load_x(0, 1)
        load_wa(0)
        nc.sync.dma_start(out=scale[:], in_=x_scale.rearrange("o (g p t) -> p (o g) t", g=2, t=4))
        load_x(1, 2)
        load_x(2, 3)
        load_wa(1)
        load_x(3, 4)
        load_x(4, 6)
        nc.sync.dma_start(out=gq_col[:], in_=gamma_cq.rearrange("(p t) -> p t", t=4))
        nc.sync.dma_start(out=gkv_col[0:32, :], in_=gamma_ckv.rearrange("(p e) -> p e", e=2))
        nc.sync.dma_start(out=wb_raw[:], in_=wq_b.rearrange("(p j) c -> p j c", j=4))
        load_x(6, 8)
        nc.sync.dma_start(out=wkv_raw[:], in_=wkv.rearrange("(g p j) c -> p g j c", p=P, j=4))
        load_x(8, 12)
        load_factors(0)
        for i0 in range(12, N_TILES, 4):
            load_x(i0, i0 + 4)
        load_factors(1)

        make_identity(nc, ident[:])
        nc.vector.memset(one[:], 1.0)
        nc.scalar.activation(eps[:], one[:], ACT.Abs_reciprocal_sqrt, scale=EPS**-2)

        state = {}


        def gpsimd_copy(out, in_, sign=1.0):
            nc.gpsimd.tensor_scalar(out=out, in0=in_, scalar1=sign, scalar2=0.0, op0=MULT, op1=ADD)

        def wa_grouped(g):
            if ("wa_g", g) not in state:
                state["wa_g", g] = keep.tile([P, QR * 4], BF16, name="grouped", align_bytes=64)
            return state["wa_g", g][:].rearrange("p (u m e j) -> p u m e j", u=2, e=2, j=4)

        def wa_copy(g, m0, m1, copy=nc.scalar.copy):
            copy(
                out=wa_grouped(g)[:, :, m0:m1].rearrange("p u m e j -> p m j u e"),
                in_=wa_raw[g][:, :, 4 * m0 : 4 * m1].rearrange("p j (m u e) -> p m j u e", u=2, e=2),
            )

        def wa_copy_gpsimd(g, m0, m1):
            for u in range(2):
                gpsimd_copy(
                    wa_grouped(g)[:, u, m0:m1],
                    wa_raw[g][:, :, 4 * m0 : 4 * m1].rearrange("p j (m u e) -> p u m e j", u=2, e=2)[:, u],
                )

        def wa_quant(g):
            nc.vector.quantize_mx(
                out=wa_c[:, g, :].bitcast(FP8X4), scales=wa_s[:, g, :], in_=state["wa_g", g][:]
            )

        def gamma_turn():
            bank = ps_n.tile([P, 3, P], F32, name="pn")
            for u in range(2):
                nc.tensor.transpose(bank[:, u, :], gq_col[:].bitcast(F32)[:, u : u + 1].to_broadcast([P, P]), ident[:])
            nc.tensor.transpose(bank[:, 2, :], gkv_col[:].bitcast(F32).to_broadcast([P, P]), ident[:])
            state["gains"] = bank

        def gamma_copy():
            words = (QR + KVR) // 2
            nc.scalar.copy(out=gains[:].bitcast(F32), in_=state["gains"][:].rearrange("p u m -> p (u m)")[:, 0:words])

        def wkv_copy_gpsimd():
            state["wkv_g"] = keep.tile([P, 2 * 128 * 4], BF16, name="wkv_g", align_bytes=64)
            gpsimd_copy(
                state["wkv_g"][:].rearrange("p (g c j) -> p g c j", g=2, j=4)[:, :, 0:WKV_ON_GPSIMD],
                wkv_raw[:].rearrange("p g j c -> p g c j")[:, :, 0:WKV_ON_GPSIMD],
            )

        def wkv_copy():
            nc.scalar.copy(
                out=state["wkv_g"][:].rearrange("p (g c i j) -> p g c j i", g=2, i=4, j=4)[:, :, WKV_ON_GPSIMD // 4 :],
                in_=wkv_raw[:].rearrange("p g j (c i) -> p g c j i", i=4)[:, :, WKV_ON_GPSIMD // 4 :],
            )

        def wb_copy_gpsimd():
            state["wb_g"] = keep.tile([P, 384 * 4], BF16, name="grouped", align_bytes=64)
            gpsimd_copy(
                state["wb_g"][:, 0:1024].rearrange("p (h c j) -> p h c j", h=NH, j=4)[:, :, 0:WB_ON_GPSIMD],
                wb_raw[:].rearrange("p j (h c) -> p h c j", h=NH)[:, :, 0:WB_ON_GPSIMD],
            )

        def wb_copy(roped):
            src = wb_raw[:].rearrange("p j (h c i) -> p h c j i", h=NH, i=4)
            if roped:
                dst = state["wb_g"][:, 1024:].rearrange("p (h c i j) -> p h c j i", h=NH, i=4, j=4)
                nc.scalar.copy(out=dst, in_=src[:, :, DN // 4 :])
            else:
                dst = state["wb_g"][:, 0:1024].rearrange("p (h c i j) -> p h c j i", h=NH, i=4, j=4)
                nc.scalar.copy(out=dst[:, :, WB_ON_GPSIMD // 4 :], in_=src[:, :, WB_ON_GPSIMD // 4 : DN // 4])

        def wkv_quant():
            nc.vector.quantize_mx(
                out=wkv_c[:].rearrange("p g c -> p (g c)").bitcast(FP8X4),
                scales=wkv_s[:].rearrange("p g c -> p (g c)"),
                in_=state["wkv_g"][:],
            )

        def wb_quant():
            nc.vector.quantize_mx(out=wb_c[:].bitcast(FP8X4), scales=wb_s[:], in_=state["wb_g"][:])

        def table_sign(part):
            quarter = factors[part][:, :, 0, 1, :]
            nc.vector.tensor_scalar(out=quarter, in0=quarter, scalar1=-1.0, scalar2=None, op0=MULT)


        def widen(n, j0=0, j1=2):
            if j0 == 0:
                state["xw", n] = work.tile([P, 2 * H], BF16, name="xw", bufs=2)
            nc.scalar.copy(
                out=state["xw", n][:, j0 * H : j1 * H], in_=x_raw[:, (2 * n + j0) * H : (2 * n + j1) * H].bitcast(FP8)
            )

        def turn_x(n, j, xt=None):
            if xt is None:
                xt = ps_x.tile([P, 2, 2, P], F32, name="xt")
            words = state["xw", n][:, j * H : (j + 1) * H].bitcast(F32)
            for g in range(2):
                for u in range(2):
                    nc.tensor.transpose(xt[:, u, g, :], words[:, 256 * g + u : 256 * (g + 1) : 2], ident[:])
            state["xt", n, j] = xt

        def scale_x(n, j):
            if j == 0:
                if n == 1:
                    state["xg", n] = keep.tile([P, 2 * H], BF16, name="wkv_g", align_bytes=64)
                else:
                    state["xg", n] = work.tile([P, 2 * H], BF16, name="xg", bufs=2, align_bytes=64)
            nc.vector.tensor_tensor(
                out=state["xg", n][:, j * H : (j + 1) * H].rearrange("p (g n u e) -> p g n u e", g=2, u=2, e=2),
                in0=state["xt", n, j][:]
                .rearrange("p u g n -> p (u g n)")
                .bitcast(BF16)
                .rearrange("p (u g n e) -> p g n u e", u=2, g=2, e=2),
                in1=scale[:].rearrange("p g (u e) -> p g u e", u=2).unsqueeze(2).to_broadcast([P, 2, P, 2, 2]),
                op=MULT,
            )

        def quant_x(n, j0=0, j1=2):
            if j0 == 0:
                xc = work.tile([P, 512], U32, name="xc", bufs=4, align_bytes=64)
                xsc = work.tile([P, 512], U8, name="xsc", bufs=4, align_bytes=64)
                state["xc", n] = (xc, xsc)
            xc, xsc = state["xc", n]
            cols = slice(j0 * 256, j1 * 256)
            nc.vector.quantize_mx(
                out=xc[:, cols].bitcast(FP8X4), scales=xsc[:, cols], in_=state["xg", n][:, j0 * H : j1 * H]
            )


        def spare_bank(shape):
            return ps_x.tile(shape, F32, name="xt")

        def mm_a(n, j, pa=None):
            xc, xsc = state["xc", n]
            if pa is None:
                pa = ps_a.tile([P, QR], F32, name="pa")
            for g in range(2):
                cols = slice((2 * j + g) * P, (2 * j + g + 1) * P)
                nc.tensor.matmul_mx(
                    out=pa[:],
                    lhsT=xc[:, cols].bitcast(FP8X4),
                    lhsT_scale=xsc[:, cols],
                    rhs=wa_c[:, g, :].bitcast(FP8X4),
                    rhs_scale=wa_s[:, g, :],
                    start=(g == 0),
                    stop=(g == 1),
                )
            state["pa", n, j] = pa

        def stat(kind, n):
            if (kind, n) not in state:
                state[kind, n] = work.tile([P, 4], F32, name=kind, bufs=PAIRS + 2)
            return state[kind, n]

        def square_a(n, j):
            squares = work.tile([P, QR], BF16, name="squares_a")
            nc.scalar.activation(
                squares[:], state["pa", n, j][:], ACT.Square, scale=QR**-0.5, accum_out=stat("mean", n)[:, j : j + 1]
            )

        def inverse_rms(n, c0, c1):
            nc.scalar.activation(
                stat("rinv", n)[:, c0:c1], stat("mean", n)[:, c0:c1], ACT.Abs_reciprocal_sqrt, bias=eps[:]
            )

        def norm_a(n, j):
            cq = work.tile([P, QR], BF16, name="cq", bufs=3)
            nc.vector.scalar_tensor_tensor(
                out=cq[:],
                in0=state["pa", n, j][:],
                scalar=stat("rinv", n)[:, j : j + 1],
                in1=gq,
                op0=MULT,
                op1=MULT,
            )
            state["cq", n, j] = cq

        def turn_c(n, j, own_bank=None):
            if j == 0:
                state["ct", n] = ps_c.tile([P, 2, 2, P], F32, name="ct")
            ct = state["ct", n] if own_bank is None else own_bank
            words = state["cq", n, j][:].bitcast(F32)
            for u in range(2):
                nc.tensor.transpose(ct[:, j, u, :], words[:, u * P : (u + 1) * P], ident[:])
            state["ct", n, j] = ct

        def shared(n, shape, dtype):
            return work.tile(shape, dtype, name="shared%d" % n, bufs=1, align_bytes=64)

        def empty_c(n, j0=0, j1=2, copy=nc.scalar.copy):
            if j0 == 0:
                state["cg", n] = shared(n, [P, 1024], BF16)
            copy(
                out=state["cg", n][:].bitcast(F32).rearrange("p (j n u) -> p j n u", j=2, u=2)[:, j0:j1],
                in_=state["ct", n, j0][:, j0:j1].rearrange("p j u n -> p j n u"),
            )

        def quant_c(n, j0=0, j1=2):
            if j0 == 0:
                cc = work.tile([P, 256], U32, name="cc", bufs=2, align_bytes=64)
                cs = work.tile([P, 256], U8, name="cs", bufs=2, align_bytes=64)
                state["cc", n] = (cc, cs)
            cc, cs = state["cc", n]
            cols = slice(j0 * P, j1 * P)
            nc.vector.quantize_mx(
                out=cc[:, cols].bitcast(FP8X4), scales=cs[:, cols], in_=state["cg", n][:, j0 * QR : j1 * QR]
            )


        def mm_kv(n, tiles=(0, 1), pr=None):
            xc, xsc = state["xc", n]
            if pr is None:
                pr = ps_r.tile([P, 2, 256], F32, name="pr")
            for j in tiles:
                state["pr", n, j] = pr
                for g in range(2):
                    xcols = slice((2 * j + g) * P, (2 * j + g + 1) * P)
                    nc.tensor.matmul_mx(
                        out=pr[:, j, 0:128],
                        lhsT=xc[:, xcols].bitcast(FP8X4),
                        lhsT_scale=xsc[:, xcols],
                        rhs=wkv_c[:, g, :].bitcast(FP8X4),
                        rhs_scale=wkv_s[:, g, :],
                        start=(g == 0),
                        stop=(g == 1),
                    )

        def mm_q(n, j, dst, c0, c1):
            cc, cs = state["cc", n]
            cols = slice(j * P, (j + 1) * P)
            nc.tensor.matmul_mx(
                out=dst,
                lhsT=cc[:, cols].bitcast(FP8X4),
                lhsT_scale=cs[:, cols],
                rhs=wb_c[:, c0:c1].bitcast(FP8X4),
                rhs_scale=wb_s[:, c0:c1],
                start=True,
                stop=True,
            )

        def mm_rope(n, tiles=(0, 1), own_bank=None):
            for j in tiles:
                state["pq", n, j] = state["pr", n, j] if own_bank is None else own_bank
                mm_q(n, j, state["pq", n, j][:, j, 128:256], 256, 384)

        def mm_nope(n, tiles=(0, 1), pn=None):
            if pn is None:
                pn = ps_n.tile([P, 2, 256], F32, name="pn")
            for j in tiles:
                mm_q(n, j, pn[:, j, :], 0, 256)
                state["pn", n, j] = pn


        def out_tile(n):
            if ("ot", n) not in state:
                state["ot", n] = work.tile([P, 2, ROW], F32, name="ot", bufs=PAIRS)
            return state["ot", n]

        def copy_nope(n, j0=0, j1=2):
            nc.scalar.copy(
                out=out_tile(n)[:, j0:j1, 128:512].rearrange("p j (h c) -> p j h c", h=NH)[:, :, :, 0:DN],
                in_=state["pn", n, j0][:, j0:j1].rearrange("p j (h c) -> p j h c", h=NH),
            )

        def roped_groups(n, j0, j1):
            return out_tile(n)[:].rearrange("p j (s c) -> p j s c", c=HEAD)[:, j0:j1, :, 64:128]

        def copy_rope(n):
            nc.scalar.copy(
                out=roped_groups(n, 0, 2), in_=state["pr", n, 0][:, :, 64:256].rearrange("p j (s c) -> p j s c", s=3)
            )

        def square_kv(n, tiles=(0, 1)):
            for j in tiles:
                squares = work.tile([P, KVR], BF16, name="squares_kv", bufs=4)
                nc.scalar.activation(
                    squares[:],
                    state["pr", n, j][:, j, 0:KVR],
                    ACT.Square,
                    scale=KVR**-0.5,
                    accum_out=stat("mean", n + 2)[:, 2 + j : 3 + j],
                )

        def norm_kv(n, tiles=(0, 1)):
            for j in tiles:
                nc.vector.scalar_tensor_tensor(
                    out=out_tile(n)[:, j, 0:KVR],
                    in0=state["pr", n, j][:, j, 0:KVR],
                    scalar=stat("rinv", n + 2)[:, 2 + j : 3 + j],
                    in1=gkv,
                    op0=MULT,
                    op1=MULT,
                )

        def scale_kv(n):
            for j in range(2):
                nc.scalar.activation(
                    out_tile(n)[:, j, 0:KVR],
                    state["pr", n, j][:, j, 0:KVR],
                    ACT.Copy,
                    scale=stat("rinv", n + 2)[:, 2 + j : 3 + j],
                )

        def gain_kv_gpsimd(n):
            ckv = out_tile(n)[:, :, 0:KVR]
            nc.gpsimd.tensor_tensor(out=ckv, in0=ckv, in1=gkv.unsqueeze(1).to_broadcast([P, 2, KVR]), op=MULT)

        def gain_kv(n):
            nc.vector.tensor_tensor(
                out=out_tile(n)[:, :, 0:KVR],
                in0=state["pr", n, 0][:, :, 0:KVR],
                in1=gkv.unsqueeze(1).to_broadcast([P, 2, KVR]),
                op=MULT,
            )

        def finish_kv(n):
            state["ckv", n] = shared(n + 1, [P, 2, KVR], F32)
            nc.gpsimd.tensor_tensor(
                out=state["ckv", n][:],
                in0=out_tile(n)[:, :, 0:KVR],
                in1=stat("rinv", n + 2)[:, 2:4].unsqueeze(2).to_broadcast([P, 2, KVR]),
                op=MULT,
            )

        def rope_products(n, engine, source, j0, j1, s0=0, s1=3):
            if ("products", n) not in state:
                state["products", n] = work.tile([P, 2, 3, 2, 2, HALF], F32, name="products", bufs=3)
            shape = [P, j1 - j0, s1 - s0, 2, DR]
            part, i = divmod(2 * n, PAIRS)
            engine.tensor_tensor(
                out=state["products", n][:, j0:j1, s0:s1].rearrange("p j s w h d -> p j s w (h d)"),
                in0=source.unsqueeze(3).to_broadcast(shape),
                in1=factors[part][:, i + j0 : i + j1]
                .rearrange("p j w h d -> p j w (h d)")
                .unsqueeze(2)
                .to_broadcast(shape),
                op=MULT,
            )

        def products_gpsimd(n):
            rope_products(n, nc.gpsimd, roped_groups(n, 0, 2), 0, 2)

        def products_vector(n, j):
            source = state["pr", n, j][:, j : j + 1, 64:256].rearrange("p j (s c) -> p j s c", s=3)
            rope_products(n, nc.vector, source, j, j + 1)

        def products_k(n):
            rope_products(n, nc.vector, state["pr", n, 0][:, :, 64:128].unsqueeze(2), 0, 2, 0, 1)

        def products_q(n, j):
            source = state["pq", n, j][:, j : j + 1, 128:256].rearrange("p j (s c) -> p j s c", s=NH)
            rope_products(n, nc.vector, source, j, j + 1, 1, 3)

        def rope_sum(n, engine, j0=0, j1=2, s0=0, s1=3):
            terms = state["products", n][:, j0:j1, s0:s1].rearrange("p j s w h d -> p (j s) w h d")
            engine.tensor_tensor(
                out=roped_groups(n, j0, j1)[:, :, s0:s1].rearrange("p j s (w d) -> p (j s) w d", w=2),
                in0=terms[:, :, :, 0, :],
                in1=terms[:, :, :, 1, :],
                op=ADD,
            )

        def sum_k(n):
            rope_sum(n, nc.vector, 0, 2, 0, 1)

        def sum_q(n, j):
            rope_sum(n, nc.vector, j, j + 1, 1, 3)

        def store_q(n, j0=0, j1=2):
            nc.sync.dma_start(out=out_hbm[:, 2 * n + j0 : 2 * n + j1, 0:384], in_=out_tile(n)[:, j0:j1, 128:512])

        def store_kv(n, j0=0, j1=2):
            nc.sync.dma_start(out=out_hbm[:, 2 * n + j0 : 2 * n + j1, 384:512], in_=out_tile(n)[:, j0:j1, 0:128])

        def store(n):
            nc.sync.dma_start(out=out_hbm[:, 2 * n : 2 * n + 2, 384:448], in_=state["ckv", n][:])
            nc.sync.dma_start(out=out_hbm[:, 2 * n : 2 * n + 2, 448:512], in_=out_tile(n)[:, :, 64:128])
            store_q(n)

        def rms_step(n):
            inverse_rms(n, 0, 4 if n >= 2 else 2)

        def late_sign(n):
            if n == 0:
                table_sign(1)

        step = (
            (late_sign, 7),
            (quant_c, 3),
            (quant_x, 1),
            (square_kv, 3),
            (rms_step, 2),
            (finish_kv, 4),
            (lambda n: rope_sum(n, nc.gpsimd), 4),
            (store, 4),
            (mm_rope, 3),
            (mm_nope, 3),
            (lambda n: mm_a(n, 0), 1),
            (widen, -1),
            (copy_rope, 3),
            (products_gpsimd, 3),
            (copy_nope, 3),
            (lambda n: norm_a(n, 0), 2),
            (lambda n: norm_a(n, 1), 2),
            (lambda n: turn_x(n, 1), 0),
            (lambda n: square_a(n, 0), 1),
            (lambda n: turn_c(n, 0), 2),
            (lambda n: turn_c(n, 1), 2),
            (lambda n: mm_a(n, 1), 1),
            (lambda n: scale_x(n, 0), 0),
            (gain_kv, 3),
            (mm_kv, 2),
            (lambda n: turn_x(n, 0), -1),
            (lambda n: scale_x(n, 1), 0),
            (empty_c, 2),
            (lambda n: square_a(n, 1), 1),
        )

        widen(0, 0, 1)
        turn_x(0, 0)
        wa_copy(0, 0, 96, nc.vector.tensor_copy)
        wa_copy(0, 96, 128)
        widen(0, 1, 2)
        turn_x(0, 1)
        widen(1, 0, 1)
        turn_x(1, 0, ps_a.tile([P, 2, 2, P], F32, name="pa"))
        widen(1, 1, 2)
        turn_x(1, 1, ps_a.tile([P, 2, 2, P], F32, name="pa"))
        scale_x(0, 0)
        wa_quant(0)
        wa_copy(1, 0, 72)
        wa_copy_gpsimd(1, 72, 128)
        scale_x(0, 1)
        scale_x(1, 0)
        quant_x(0)
        wa_quant(1)
        gamma_turn()
        widen(2, 0, 1)
        turn_x(2, 0)
        gamma_copy()
        widen(2, 1, 2)
        widen(3, 0, 1)
        wb_copy_gpsimd()
        wb_copy(True)
        wb_copy(False)
        mm_a(0, 0)
        scale_x(1, 1)
        mm_a(0, 1)
        turn_x(2, 1)
        scale_x(2, 0)
        quant_x(1)
        square_a(0, 0)
        wkv_copy_gpsimd()
        inverse_rms(0, 0, 1)
        square_a(0, 1)
        inverse_rms(0, 1, 2)
        widen(3, 1, 2)
        widen(4, 0, 1)
        mm_a(1, 0)
        norm_a(0, 0)
        norm_a(0, 1)
        square_a(1, 0)
        turn_c(0, 0)
        turn_c(0, 1)
        mm_a(1, 1)
        turn_x(3, 0)
        scale_x(2, 1)
        empty_c(0)
        square_a(1, 1)
        wb_quant()
        wkv_quant()
        quant_c(0)
        quant_x(2)
        rms_step(1)
        widen(4, 1, 2)
        mm_kv(0)
        mm_rope(0)
        mm_nope(0)
        mm_a(2, 0)
        copy_rope(0)
        norm_a(1, 0)
        table_sign(0)
        products_gpsimd(0)
        square_kv(0)
        copy_nope(0)
        norm_a(1, 1)
        turn_x(3, 1)
        square_a(2, 0)
        turn_c(1, 0)
        turn_c(1, 1)
        mm_a(2, 1)
        scale_x(3, 0)
        gain_kv(0)
        mm_kv(1)
        turn_x(4, 0)
        scale_x(3, 1)
        empty_c(1)
        square_a(2, 1)

        for s in range(4, PAIRS):
            for stage, lag in step:
                if 0 <= s - lag < PAIRS:
                    stage(s - lag)

        a, b, c, d = range(PAIRS - 4, PAIRS)
        mm_kv(c, (0, 1), spare_bank([P, 2, 256]))
        quant_c(b)
        quant_x(d, 0, 1)
        quant_x(d, 1, 2)
        square_kv(b)
        rms_step(c)
        square_kv(c)
        inverse_rms(d, 2, 4)
        finish_kv(a)
        rope_sum(a, nc.gpsimd)
        store(a)
        mm_rope(b)
        mm_a(d, 0)
        mm_a(d, 1, spare_bank([P, QR]))
        inverse_rms(d + 1, 2, 4)
        scale_kv(c)
        gain_kv_gpsimd(c)
        norm_a(c, 0)
        norm_a(c, 1)
        turn_c(c, 0)
        turn_c(c, 1)
        mm_kv(d, (0, 1), ps_a.tile([P, 2, 256], F32, name="pa"))
        mm_nope(b)
        products_vector(b, 0)
        products_vector(b, 1)
        rope_sum(b, nc.gpsimd)
        norm_kv(b)
        store_kv(b)
        products_k(c)
        square_a(d, 0)
        square_a(d, 1)
        inverse_rms(d, 0, 1)
        empty_c(c)
        inverse_rms(d, 1, 2)
        copy_nope(b)
        store_q(b)
        square_kv(d)
        norm_a(d, 0)
        norm_a(d, 1)
        quant_c(c)
        turn_c(d, 0)
        turn_c(d, 1, ps_r.tile([P, 2, 2, P], F32, name="pr"))
        mm_rope(c)
        mm_nope(c, (0,))
        mm_nope(c, (1,), ps_a.tile([P, 2, 256], F32, name="pa"))
        inverse_rms(d + 2, 2, 4)
        empty_c(d, 0, 1)
        empty_c(d, 1, 2)
        copy_nope(c, 0, 1)
        copy_nope(c, 1, 2)
        products_k(d)
        sum_k(c)
        store_kv(c)
        norm_kv(d)
        sum_k(d)
        store_kv(d)
        quant_c(d, 0, 1)
        products_q(c, 0)
        quant_c(d, 1, 2)
        mm_rope(d, (0,), ps_a.tile([P, 2, 256], F32, name="pa"))
        mm_nope(d, (0,), ps_c.tile([P, 2, 256], F32, name="ct"))
        mm_rope(d, (1,), ps_n.tile([P, 2, 256], F32, name="pn"))
        mm_nope(d, (1,), ps_r.tile([P, 2, 256], F32, name="pr"))
        copy_nope(d, 0, 1)
        copy_nope(d, 1, 2)
        products_q(c, 1)
        sum_q(c, 0)
        store_q(c, 0, 1)
        products_q(d, 0)
        sum_q(c, 1)
        store_q(c, 1, 2)
        products_q(d, 1)
        sum_q(d, 0)
        store_q(d, 0, 1)
        sum_q(d, 1)
        store_q(d, 1, 2)
